import numpy as np
import ml_dtypes


def mxq(x, axis, fmt="e4m3"):
    dtype, down = {"e4m3": (ml_dtypes.float8_e4m3fn, 7), "e5m2": (ml_dtypes.float8_e5m2, 14)}[fmt]
    v = np.moveaxis(np.asarray(x, np.float32).astype(ml_dtypes.bfloat16).astype(np.float64), axis, -1)
    blocks = v.reshape(v.shape[:-1] + (-1, 32))
    amax = np.abs(blocks).max(-1, keepdims=True)
    byte = np.maximum(np.where(amax > 0, np.frexp(amax)[1] - 1 + 127, 0) - down, 1)
    scale = np.exp2(byte - 127.0)
    codes = (blocks / scale).astype(np.float32).astype(dtype).astype(np.float64)
    return np.moveaxis((codes * scale).reshape(v.shape), -1, axis)


WIDE = False


def mx_kscale(k):
    if not WIDE:
        return np.ones(k)
    levels = np.array([10, -10, 5, -5, 0])
    a = np.random.permutation(np.resize(levels, k // 512 * 4)).reshape(k // 512, 4)
    idx = np.arange(k)
    return np.exp2(a[idx // 512, idx % 128 // 32])


BF16 = ml_dtypes.bfloat16


def bf(x):
    return np.asarray(x, np.float32).astype(BF16)


def f64(x):
    return np.asarray(x).astype(np.float64)


B, T, M, N, D, ORDER, CO = 1, 16, 256, 512, 256, 3, 1024
C = (ORDER + 1) * D


def setup_inputs():
    t = mx_kscale(C)[:D]
    tc = np.tile(t, ORDER + 1)
    return {
        "feat_context": bf(np.random.standard_normal((B, N, D, T)) * 0.4 * np.sqrt(N) * t[:, None]),
        "feat_target": bf(np.random.standard_normal((B, M, D, T)) * 0.5 * t[:, None]),
        "adj": bf(np.random.uniform(size=(B, ORDER, M, N)) * 12.0 / N),
        "missing_mask_context": bf(np.random.randint(0, 2, (B, T, N))),
        "W_mlp": bf(np.random.standard_normal((CO, C)) * 1.5 / np.sqrt(C) / tc),
        "b_mlp": bf(np.random.standard_normal(CO) * 0.3),
    }


def reference(feat_context, feat_target, adj, missing_mask_context, W_mlp, b_mlp):
    fc = f64(feat_context).transpose(0, 3, 1, 2)
    ft = f64(feat_target).transpose(0, 3, 1, 2)
    keep = 1.0 - f64(missing_mask_context)
    fcq = mxq(fc, 2, "e4m3")
    outs = [f64(feat_target)]
    for i in range(ORDER):
        a = f64(adj)[:, i][:, None, :, :] * keep[:, :, None, :]
        norm = a / (a.sum(-1, keepdims=True) + 1.0)
        agg = ft + (mxq(norm, 3, "e4m3") @ fcq)
        outs.append(agg.transpose(0, 2, 3, 1))
    cat = np.concatenate(outs, axis=2)
    y = (mxq(f64(W_mlp), 1, "e4m3") @ mxq(cat, 2, "e4m3")) + f64(b_mlp)[None, None, :, None]
    return np.maximum(y, 0.0)

@@ -1,0 +1,237 @@
+from contextlib import ExitStack
+
+import concourse.mybir as mybir
+from concourse.masks import make_identity
+
+BF16 = mybir.dt.bfloat16
+F32 = mybir.dt.float32
+U32 = mybir.dt.uint32
+U8 = mybir.dt.uint8
+FP8X4 = mybir.dt.float8_e4m3fn_x4
+ALU = mybir.AluOpType
+ACT = mybir.ActivationFunctionType
+
+P = 128
+T, M, N, D, HOPS, CO = 16, 256, 512, 256, 3, 1024
+C = (HOPS + 1) * D
+FLOPS = 2 * T * HOPS * M * N * D + 2 * M * T * CO * C
+
+NB = HOPS * M * 4 // P
+VEC_SHARE = 4
+
+
+def tile_graphaggregation_pa_t_kernel(tc, feat_context, feat_target, adj, missing_mask_context, W_mlp, b_mlp, out):
+    nc = tc.nc
+    fc_v = feat_context.rearrange("o (j p) d t -> p (o j) (d t)", p=P)
+    ft_v = feat_target.rearrange("o m (e d) t -> (o m e) (d t)", e=2).rearrange("(a q) x -> q a x", q=P)
+    adj_v = adj.rearrange("o i m (j p) -> (o i m j) p", p=P).rearrange("(b q) p -> q b p", q=P)
+    mask_v = missing_mask_context.rearrange("o t n -> (o t) n")
+    w_v = W_mlp.rearrange("o (r p) -> (o r) p", p=P).rearrange("(b q) p -> q b p", q=P)
+    out_v = out.rearrange("o (a m) c t -> m (o a) (c t)", m=P)
+
+    with ExitStack() as top:
+        const = top.enter_context(tc.tile_pool(name="const", bufs=1))
+
+        ident = const.tile([P, P], BF16)
+        make_identity(nc, ident[:])
+        adj_r = const.tile([P, NB, P], BF16)
+        nc.sync.dma_start(out=adj_r[:], in_=adj_v)
+        mask_pad = const.tile([P, N], BF16)
+        nc.vector.memset(mask_pad[:], 0.0)
+        nc.sync.dma_start(out=mask_pad[0:T, :], in_=mask_v)
+        bias_bc = const.tile([P, CO], BF16)
+
+        fcq = const.tile([P, T, D], U32, align_bytes=64)
+        fcs = const.tile([P, T, D], U8, align_bytes=64)
+        catq = const.tile([P, T, 2, M], U32, align_bytes=64)
+        cats = const.tile([P, T, 2, M], U8, align_bytes=64)
+        wq = const.tile([P, 2, CO], U32, align_bytes=64)
+        ws = const.tile([P, 2, CO], U8, align_bytes=64)
+
+        with ExitStack() as ph1:
+            big = ph1.enter_context(tc.tile_pool(name="big", bufs=1))
+            loop = ph1.enter_context(tc.tile_pool(name="loop", bufs=2))
+            ps_t = ph1.enter_context(tc.psum_pool(name="ps_t", bufs=3))
+            ps_s = ph1.enter_context(tc.psum_pool(name="ps_s", bufs=3))
+            ps_x = ph1.enter_context(tc.psum_pool(name="ps_x", bufs=2))
+
+            fc_raw = big.tile([P, 4, D * T], BF16)
+            for j in range(4):
+                nc.sync.dma_start(out=fc_raw[:, j, :], in_=fc_v[:, j, :])
+            ft_r = big.tile([P, 4, P * T], BF16)
+            nc.sync.dma_start(out=ft_r[:], in_=ft_v)
+            w_r = big.tile([P, 64, P], BF16)
+            nc.sync.dma_start(out=w_r[:], in_=w_v)
+            nc.sync.dma_start(out=bias_bc[:], in_=b_mlp.partition_broadcast(P))
+
+            adj_t = const.tile([P, 4, HOPS * M], BF16)
+            for k in range(HOPS):
+                pa = ps_x.tile([P, 1024], BF16, tag="x")
+                for bb in range(8):
+                    nc.tensor.transpose(out=pa[:, bb * P : (bb + 1) * P], in_=adj_r[:, 8 * k + bb, :], identity=ident[:])
+                nc.scalar.copy(out=adj_t[:, :, k * M : (k + 1) * M], in_=pa[:].rearrange("p (c j) -> p j c", j=4))
+            pm = ps_x.tile([P, 1024], BF16, tag="x")
+            for j in range(4):
+                nc.tensor.transpose(out=pm[:, j * P : (j + 1) * P], in_=mask_pad[:, j * P : (j + 1) * P], identity=ident[:])
+            keep_t = const.tile([P, 4, 32], BF16)
+            nc.vector.tensor_scalar(
+                out=keep_t[:], in0=pm[:, 0:N].rearrange("p (j t) -> p j t", j=4)[:, :, 0:32],
+                scalar1=-1.0, scalar2=1.0, op0=ALU.mult, op1=ALU.add,
+            )
+            keep_g = const.tile([P, T, 16, 4], BF16)
+            nc.vector.tensor_scalar(
+                out=keep_g[:],
+                in0=pm[:, 0:N].rearrange("p (j t) -> p t j", j=4)[:, 0:T, :].unsqueeze(2).to_broadcast([P, T, 16, 4]),
+                scalar1=-1.0, scalar2=1.0, op0=ALU.mult, op1=ALU.add,
+            )
+            psum_s = ps_x.tile([P, 6, 32], F32, tag="x")
+            for g in range(6):
+                for j in range(4):
+                    nc.tensor.matmul(
+                        out=psum_s[:, g, :], lhsT=adj_t[:, j, g * P : (g + 1) * P], rhs=keep_t[:, j, :],
+                        start=(j == 0), stop=(j == 3),
+                    )
+            s1 = const.tile([P, 6, T], F32)
+            nc.vector.tensor_scalar_add(out=s1[:], in0=psum_s[:, :, 0:T], scalar1=1.0)
+            rcp = const.tile([P, 6, T], F32)
+            nc.vector.reciprocal(out=rcp[:], in_=s1[:])
+            spread = const.tile([P, 4, 32, 4], F32)
+            for b4 in range(4):
+                nc.vector.tensor_copy(
+                    out=spread[:, b4, :, :], in_=ident[:, 32 * b4 : 32 * b4 + 32].unsqueeze(2).to_broadcast([P, 32, 4])
+                )
+            pr = ps_x.tile([P, 4, 6 * T], F32, tag="x")
+            for b4 in range(4):
+                nc.tensor.matmul(
+                    out=pr[:, b4, :], lhsT=spread[:, b4, :, :].rearrange("p a b -> p (a b)"),
+                    rhs=rcp[:].rearrange("p g t -> p (g t)"), start=True, stop=True,
+                )
+            r_rep = const.tile([P, 4, 6 * T], F32)
+            nc.vector.tensor_copy(out=r_rep[:], in_=pr[:])
+
+            fc_view = fc_raw[:].rearrange("p j (d t) -> p t d j", t=T)
+
+            def do_weights():
+                wtg = big.tile([P, 2, CO, 4], BF16, align_bytes=64)
+                for k in range(8):
+                    pw = ps_x.tile([P, 1024], BF16, tag="x")
+                    for bb in range(8):
+                        nc.tensor.transpose(out=pw[:, bb * P : (bb + 1) * P], in_=w_r[:, 8 * k + bb, :], identity=ident[:])
+                    pw_v = pw[:].rearrange("p (o g j) -> p g o j", g=2, j=4)
+                    for g in range(2):
+                        nc.scalar.copy(out=wtg[:, g, k * P : (k + 1) * P, :], in_=pw_v[:, g])
+                for g in range(2):
+                    nc.vector.quantize_mx(
+                        out=wq[:, g, :].bitcast(FP8X4), scales=ws[:, g, :],
+                        in_=wtg[:, g, :, :].rearrange("p o j -> p (o j)"),
+                    )
+
+            for t in range(T):
+                u = loop.tile([P, NB, P], BF16, bufs=3)
+                for b in range(NB):
+                    sc = r_rep[:, b % 4, (b // 4) * T + t : (b // 4) * T + t + 1]
+                    if b % VEC_SHARE == VEC_SHARE - 1:
+                        nc.vector.tensor_scalar(out=u[:, b, :], in0=adj_r[:, b, :], scalar1=sc, scalar2=None, op0=ALU.mult)
+                    else:
+                        nc.scalar.activation(out=u[:, b, :], in_=adj_r[:, b, :], func=ACT.Copy, scale=sc)
+                ng = loop.tile([P, HOPS * 1024], BF16, align_bytes=64)
+                nq = loop.tile([P, HOPS * M], U32, align_bytes=64)
+                ns = loop.tile([P, HOPS * M], U8, align_bytes=64)
+                keep_b = keep_g[:, t, :, :].rearrange("p r j -> p (r j)").unsqueeze(1).to_broadcast([P, 16, 64])
+                pts = []
+                for k in range(HOPS):
+                    pt = ps_t.tile([P, 1024], BF16, tag="t")
+                    for bb in range(8):
+                        nc.tensor.transpose(out=pt[:, bb * P : (bb + 1) * P], in_=u[:, 8 * k + bb, :], identity=ident[:])
+                    pts.append(pt)
+                pf = ps_x.tile([P, 1024], BF16, tag="x")
+                for a in range(4):
+                    nc.tensor.transpose(
+                        out=pf[:, a * P : (a + 1) * P],
+                        in_=ft_r[:, a, :].rearrange("p (d t) -> p t d", t=T)[:, t, :], identity=ident[:],
+                    )
+                cg0 = loop.tile([P, M, 4], BF16, align_bytes=64)
+                cg1 = loop.tile([P, M, 4], BF16, align_bytes=64)
+                nc.scalar.copy(out=cg0[:, :, 0:2], in_=pf[:, 0 : 2 * M].rearrange("p (m e) -> p m e", e=2))
+                for k in range(HOPS):
+                    nc.vector.tensor_tensor(
+                        out=ng[:, k * 1024 : (k + 1) * 1024].rearrange("p (r c) -> p r c", c=64),
+                        in0=pts[k][:].rearrange("p (r c) -> p r c", c=64), in1=keep_b, op=ALU.mult,
+                    )
+                fcg = loop.tile([P, D, 4], BF16, align_bytes=64)
+                nc.vector.tensor_copy(out=fcg[:], in_=fc_view[:, t])
+                for k in range(HOPS):
+                    nc.vector.quantize_mx(
+                        out=nq[:, k * M : (k + 1) * M].bitcast(FP8X4), scales=ns[:, k * M : (k + 1) * M],
+                        in_=ng[:, k * 1024 : (k + 1) * 1024],
+                    )
+                nc.vector.quantize_mx(
+                    out=fcq[:, t, :].bitcast(FP8X4), scales=fcs[:, t, :], in_=fcg[:].rearrange("p d j -> p (d j)")
+                )
+
+                def hop_pass(dst, i, a, e):
+                    nc.tensor.matmul_mx(
+                        out=dst,
+                        lhsT=fcq[:, t, e * P : (e + 1) * P].bitcast(FP8X4), lhsT_scale=fcs[:, t, e * P : (e + 1) * P],
+                        rhs=nq[:, i * M + a * P : i * M + (a + 1) * P].bitcast(FP8X4),
+                        rhs_scale=ns[:, i * M + a * P : i * M + (a + 1) * P],
+                        start=True, stop=True,
+                    )
+
+                p0 = ps_s.tile([P, 4, P], F32, tag="s")
+                for a in range(2):
+                    for e in range(2):
+                        hop_pass(p0[:, a * 2 + e, :], 0, a, e)
+                p1 = []
+                for a in range(2):
+                    pp = ps_s.tile([P, 4, P], F32, tag="s")
+                    for i in (1, 2):
+                        for e in range(2):
+                            hop_pass(pp[:, (i - 1) * 2 + e, :], i, a, e)
+                    p1.append(pp)
+                nc.vector.tensor_tensor(
+                    out=cg0[:, :, 2:4].rearrange("p (a m) e -> p a m e", a=2),
+                    in0=p0[:].rearrange("p (a e) m -> p a m e", a=2),
+                    in1=cg0[:, :, 0:2].rearrange("p (a m) e -> p a m e", a=2), op=ALU.add,
+                )
+                for a in range(2):
+                    nc.vector.tensor_tensor(
+                        out=cg1[:, a * P : (a + 1) * P, :].rearrange("p m (h e) -> p m h e", h=2),
+                        in0=p1[a][:].rearrange("p (h e) m -> p m h e", h=2),
+                        in1=cg0[:, a * P : (a + 1) * P, 0:2].unsqueeze(2).to_broadcast([P, P, 2, 2]), op=ALU.add,
+                    )
+                nc.vector.quantize_mx(
+                    out=catq[:, t, 0, :].bitcast(FP8X4), scales=cats[:, t, 0, :], in_=cg0[:].rearrange("p m j -> p (m j)")
+                )
+                nc.vector.quantize_mx(
+                    out=catq[:, t, 1, :].bitcast(FP8X4), scales=cats[:, t, 1, :], in_=cg1[:].rearrange("p m j -> p (m j)")
+                )
+                if t == 5:
+                    do_weights()
+
+        with ExitStack() as ph2:
+            opool = ph2.enter_context(tc.tile_pool(name="opool", bufs=4))
+            ps_o = ph2.enter_context(tc.psum_pool(name="ps_o", bufs=6))
+            for a in range(2):
+                for ob in range(8):
+                    ot = opool.tile([P, P, T], F32)
+                    for tq in range(4):
+                        pb = ps_o.tile([P, 4, P], F32)
+                        for tt in range(4):
+                            t = 4 * tq + tt
+                            for g in range(2):
+                                nc.tensor.matmul_mx(
+                                    out=pb[:, tt, :],
+                                    lhsT=catq[:, t, g, a * P : (a + 1) * P].bitcast(FP8X4),
+                                    lhsT_scale=cats[:, t, g, a * P : (a + 1) * P],
+                                    rhs=wq[:, g, ob * P : (ob + 1) * P].bitcast(FP8X4),
+                                    rhs_scale=ws[:, g, ob * P : (ob + 1) * P],
+                                    start=(g == 0), stop=(g == 1),
+                                )
+                        nc.vector.tensor_tensor(
+                            out=ot[:, :, 4 * tq : 4 * tq + 4], in0=pb[:].rearrange("p t o -> p o t"),
+                            in1=bias_bc[:, ob * P : (ob + 1) * P].unsqueeze(2).to_broadcast([P, P, 4]), op=ALU.add,
+                        )
+                    flat = ot[:].rearrange("p o t -> p (o t)")
+                    nc.scalar.activation(out=flat, in_=flat, func=ACT.Relu)
+                    nc.sync.dma_start(out=out_v[:, a, ob * P * T : (ob + 1) * P * T], in_=flat)

@@ -17,7 +17,9 @@ C = (HOPS + 1) * D
 FLOPS = 2 * T * HOPS * M * N * D + 2 * M * T * CO * C
 
 NB = HOPS * M * 4 // P
-VEC_SHARE = 4
+VEC_SHARE = 6
+FC_AHEAD = 6
+PLAIN_HOPS = 2
 
 
 def tile_graphaggregation_pa_t_kernel(tc, feat_context, feat_target, adj, missing_mask_context, W_mlp, b_mlp, out):
@@ -34,6 +36,8 @@ def tile_graphaggregation_pa_t_kernel(tc, feat_context, feat_target, adj, missin
 
         ident = const.tile([P, P], BF16)
         make_identity(nc, ident[:])
+        ident_f = const.tile([P, P], F32)
+        make_identity(nc, ident_f[:])
         adj_r = const.tile([P, NB, P], BF16)
         nc.sync.dma_start(out=adj_r[:], in_=adj_v)
         mask_pad = const.tile([P, N], BF16)
@@ -98,7 +102,7 @@ def tile_graphaggregation_pa_t_kernel(tc, feat_context, feat_target, adj, missin
             spread = const.tile([P, 4, 32, 4], F32)
             for b4 in range(4):
                 nc.vector.tensor_copy(
-                    out=spread[:, b4, :, :], in_=ident[:, 32 * b4 : 32 * b4 + 32].unsqueeze(2).to_broadcast([P, 32, 4])
+                    out=spread[:, b4, :, :], in_=ident_f[:, 32 * b4 : 32 * b4 + 32].unsqueeze(2).to_broadcast([P, 32, 4])
                 )
             pr = ps_x.tile([P, 4, 6 * T], F32, tag="x")
             for b4 in range(4):
@@ -110,6 +114,18 @@ def tile_graphaggregation_pa_t_kernel(tc, feat_context, feat_target, adj, missin
             nc.vector.tensor_copy(out=r_rep[:], in_=pr[:])
 
             fc_view = fc_raw[:].rearrange("p j (d t) -> p t d j", t=T)
+            ft_words = ft_r[:].bitcast(F32).rearrange("p a (d w) -> p a w d", w=T // 2)
+
+            def do_context(t):
+                fcg = loop.tile([P, D, 4], BF16, align_bytes=64)
+                nc.vector.tensor_copy(out=fcg[:], in_=fc_view[:, t])
+                nc.vector.quantize_mx(
+                    out=fcq[:, t, :].bitcast(FP8X4), scales=fcs[:, t, :], in_=fcg[:].rearrange("p d j -> p (d j)")
+                )
+
+            for t in range(FC_AHEAD):
+                do_context(t)
+            cg0s = {}
 
             def do_weights():
                 wtg = big.tile([P, 2, CO, 4], BF16, align_bytes=64)
@@ -142,32 +158,36 @@ def tile_graphaggregation_pa_t_kernel(tc, feat_context, feat_target, adj, missin
                 for k in range(HOPS):
                     pt = ps_t.tile([P, 1024], BF16, tag="t")
                     for bb in range(8):
-                        nc.tensor.transpose(out=pt[:, bb * P : (bb + 1) * P], in_=u[:, 8 * k + bb, :], identity=ident[:])
+                        if k < PLAIN_HOPS:
+                            nc.tensor.matmul(
+                                out=pt[:, bb * P : (bb + 1) * P], lhsT=u[:, 8 * k + bb, :], rhs=ident[:], start=True, stop=True
+                            )
+                        else:
+                            nc.tensor.transpose(out=pt[:, bb * P : (bb + 1) * P], in_=u[:, 8 * k + bb, :], identity=ident[:])
                     pts.append(pt)
-                pf = ps_x.tile([P, 1024], BF16, tag="x")
-                for a in range(4):
-                    nc.tensor.transpose(
-                        out=pf[:, a * P : (a + 1) * P],
-                        in_=ft_r[:, a, :].rearrange("p (d t) -> p t d", t=T)[:, t, :], identity=ident[:],
-                    )
-                cg0 = loop.tile([P, M, 4], BF16, align_bytes=64)
+                if t % 2 == 0:
+                    pf = ps_x.tile([P, 512], F32, tag="x")
+                    for a in range(4):
+                        nc.tensor.transpose(out=pf[:, a * P : (a + 1) * P], in_=ft_words[:, a, t // 2, :], identity=ident_f[:])
+                    pf_v = pf[:].bitcast(BF16).rearrange("p (m c e) -> p e m c", c=2, e=2)
+                    for e in range(2):
+                        cg = loop.tile([P, M, 4], BF16, align_bytes=64, tag="cg0", name="cg0", bufs=4)
+                        nc.scalar.copy(out=cg[:, :, 0:2], in_=pf_v[:, e])
+                        cg0s[t + e] = cg
+                cg0 = cg0s[t]
                 cg1 = loop.tile([P, M, 4], BF16, align_bytes=64)
-                nc.scalar.copy(out=cg0[:, :, 0:2], in_=pf[:, 0 : 2 * M].rearrange("p (m e) -> p m e", e=2))
                 for k in range(HOPS):
                     nc.vector.tensor_tensor(
                         out=ng[:, k * 1024 : (k + 1) * 1024].rearrange("p (r c) -> p r c", c=64),
                         in0=pts[k][:].rearrange("p (r c) -> p r c", c=64), in1=keep_b, op=ALU.mult,
                     )
-                fcg = loop.tile([P, D, 4], BF16, align_bytes=64)
-                nc.vector.tensor_copy(out=fcg[:], in_=fc_view[:, t])
+                if t + FC_AHEAD < T:
+                    do_context(t + FC_AHEAD)
                 for k in range(HOPS):
                     nc.vector.quantize_mx(
                         out=nq[:, k * M : (k + 1) * M].bitcast(FP8X4), scales=ns[:, k * M : (k + 1) * M],
                         in_=ng[:, k * 1024 : (k + 1) * 1024],
                     )
-                nc.vector.quantize_mx(
-                    out=fcq[:, t, :].bitcast(FP8X4), scales=fcs[:, t, :], in_=fcg[:].rearrange("p d j -> p (d j)")
-                )
 
                 def hop_pass(dst, i, a, e):
                     nc.tensor.matmul_mx(

@@ -17,9 +17,10 @@ C = (HOPS + 1) * D
 FLOPS = 2 * T * HOPS * M * N * D + 2 * M * T * CO * C
 
 NB = HOPS * M * 4 // P
-VEC_SHARE = 6
-FC_AHEAD = 6
+VEC_SHARE = 4
+FC_AHEAD = 4
 PLAIN_HOPS = 2
+W_FIRST = 4
 
 
 def tile_graphaggregation_pa_t_kernel(tc, feat_context, feat_target, adj, missing_mask_context, W_mlp, b_mlp, out):
@@ -32,17 +33,18 @@ def tile_graphaggregation_pa_t_kernel(tc, feat_context, feat_target, adj, missin
     out_v = out.rearrange("o (a m) c t -> m (o a) (c t)", m=P)
 
     with ExitStack() as top:
+        top.enter_context(tc.manual_schedule())
         const = top.enter_context(tc.tile_pool(name="const", bufs=1))
 
+        mask_pad = const.tile([P, N], BF16)
+        nc.vector.memset(mask_pad[:], 0.0)
+        nc.sync.dma_start(out=mask_pad[0:T, :], in_=mask_v)
+        adj_r = const.tile([P, NB, P], BF16)
+        nc.sync.dma_start(out=adj_r[:], in_=adj_v)
         ident = const.tile([P, P], BF16)
         make_identity(nc, ident[:])
         ident_f = const.tile([P, P], F32)
         make_identity(nc, ident_f[:])
-        adj_r = const.tile([P, NB, P], BF16)
-        nc.sync.dma_start(out=adj_r[:], in_=adj_v)
-        mask_pad = const.tile([P, N], BF16)
-        nc.vector.memset(mask_pad[:], 0.0)
-        nc.sync.dma_start(out=mask_pad[0:T, :], in_=mask_v)
         bias_bc = const.tile([P, CO], BF16)
 
         fcq = const.tile([P, T, D], U32, align_bytes=64)
@@ -67,13 +69,13 @@ def tile_graphaggregation_pa_t_kernel(tc, feat_context, feat_target, adj, missin
             w_r = big.tile([P, 64, P], BF16)
             nc.sync.dma_start(out=w_r[:], in_=w_v)
             nc.sync.dma_start(out=bias_bc[:], in_=b_mlp.partition_broadcast(P))
+            wtg = big.tile([P, 2, CO, 4], BF16, align_bytes=64)
 
-            adj_t = const.tile([P, 4, HOPS * M], BF16)
-            for k in range(HOPS):
-                pa = ps_x.tile([P, 1024], BF16, tag="x")
-                for bb in range(8):
-                    nc.tensor.transpose(out=pa[:, bb * P : (bb + 1) * P], in_=adj_r[:, 8 * k + bb, :], identity=ident[:])
-                nc.scalar.copy(out=adj_t[:, :, k * M : (k + 1) * M], in_=pa[:].rearrange("p (c j) -> p j c", j=4))
+            spread = const.tile([P, 4, 32, 4], F32)
+            for b4 in range(4):
+                nc.vector.tensor_copy(
+                    out=spread[:, b4, :, :], in_=ident_f[:, 32 * b4 : 32 * b4 + 32].unsqueeze(2).to_broadcast([P, 32, 4])
+                )
             pm = ps_x.tile([P, 1024], BF16, tag="x")
             for j in range(4):
                 nc.tensor.transpose(out=pm[:, j * P : (j + 1) * P], in_=mask_pad[:, j * P : (j + 1) * P], identity=ident[:])
@@ -88,6 +90,12 @@ def tile_graphaggregation_pa_t_kernel(tc, feat_context, feat_target, adj, missin
                 in0=pm[:, 0:N].rearrange("p (j t) -> p t j", j=4)[:, 0:T, :].unsqueeze(2).to_broadcast([P, T, 16, 4]),
                 scalar1=-1.0, scalar2=1.0, op0=ALU.mult, op1=ALU.add,
             )
+            adj_t = const.tile([P, 4, HOPS * M], BF16)
+            for k in range(HOPS):
+                pa = ps_t.tile([P, 1024], BF16, tag="t")
+                for bb in range(8):
+                    nc.tensor.transpose(out=pa[:, bb * P : (bb + 1) * P], in_=adj_r[:, 8 * k + bb, :], identity=ident[:])
+                nc.scalar.copy(out=adj_t[:, :, k * M : (k + 1) * M], in_=pa[:].rearrange("p (c j) -> p j c", j=4))
             psum_s = ps_x.tile([P, 6, 32], F32, tag="x")
             for g in range(6):
                 for j in range(4):
@@ -99,12 +107,7 @@ def tile_graphaggregation_pa_t_kernel(tc, feat_context, feat_target, adj, missin
             nc.vector.tensor_scalar_add(out=s1[:], in0=psum_s[:, :, 0:T], scalar1=1.0)
             rcp = const.tile([P, 6, T], F32)
             nc.vector.reciprocal(out=rcp[:], in_=s1[:])
-            spread = const.tile([P, 4, 32, 4], F32)
-            for b4 in range(4):
-                nc.vector.tensor_copy(
-                    out=spread[:, b4, :, :], in_=ident_f[:, 32 * b4 : 32 * b4 + 32].unsqueeze(2).to_broadcast([P, 32, 4])
-                )
-            pr = ps_x.tile([P, 4, 6 * T], F32, tag="x")
+            pr = ps_s.tile([P, 4, 6 * T], F32, tag="s")
             for b4 in range(4):
                 nc.tensor.matmul(
                     out=pr[:, b4, :], lhsT=spread[:, b4, :, :].rearrange("p a b -> p (a b)"),
@@ -115,123 +118,170 @@ def tile_graphaggregation_pa_t_kernel(tc, feat_context, feat_target, adj, missin
 
             fc_view = fc_raw[:].rearrange("p j (d t) -> p t d j", t=T)
             ft_words = ft_r[:].bitcast(F32).rearrange("p a (d w) -> p a w d", w=T // 2)
+            us, pts, ngs, nqs, nss, cg0s, cg1s, fcgs, p0s, p1s = {}, {}, {}, {}, {}, {}, {}, {}, {}, {}
 
-            def do_context(t):
-                fcg = loop.tile([P, D, 4], BF16, align_bytes=64)
-                nc.vector.tensor_copy(out=fcg[:], in_=fc_view[:, t])
-                nc.vector.quantize_mx(
-                    out=fcq[:, t, :].bitcast(FP8X4), scales=fcs[:, t, :], in_=fcg[:].rearrange("p d j -> p (d j)")
-                )
-
-            for t in range(FC_AHEAD):
-                do_context(t)
-            cg0s = {}
-
-            def do_weights():
-                wtg = big.tile([P, 2, CO, 4], BF16, align_bytes=64)
-                for k in range(8):
-                    pw = ps_x.tile([P, 1024], BF16, tag="x")
-                    for bb in range(8):
-                        nc.tensor.transpose(out=pw[:, bb * P : (bb + 1) * P], in_=w_r[:, 8 * k + bb, :], identity=ident[:])
-                    pw_v = pw[:].rearrange("p (o g j) -> p g o j", g=2, j=4)
-                    for g in range(2):
-                        nc.scalar.copy(out=wtg[:, g, k * P : (k + 1) * P, :], in_=pw_v[:, g])
-                for g in range(2):
-                    nc.vector.quantize_mx(
-                        out=wq[:, g, :].bitcast(FP8X4), scales=ws[:, g, :],
-                        in_=wtg[:, g, :, :].rearrange("p o j -> p (o j)"),
-                    )
-
-            for t in range(T):
-                u = loop.tile([P, NB, P], BF16, bufs=3)
+            def scale_blocks(t):
+                u = loop.tile([P, NB, P], BF16, bufs=3, name="u")
                 for b in range(NB):
                     sc = r_rep[:, b % 4, (b // 4) * T + t : (b // 4) * T + t + 1]
                     if b % VEC_SHARE == VEC_SHARE - 1:
                         nc.vector.tensor_scalar(out=u[:, b, :], in0=adj_r[:, b, :], scalar1=sc, scalar2=None, op0=ALU.mult)
                     else:
                         nc.scalar.activation(out=u[:, b, :], in_=adj_r[:, b, :], func=ACT.Copy, scale=sc)
-                ng = loop.tile([P, HOPS * 1024], BF16, align_bytes=64)
-                nq = loop.tile([P, HOPS * M], U32, align_bytes=64)
-                ns = loop.tile([P, HOPS * M], U8, align_bytes=64)
-                keep_b = keep_g[:, t, :, :].rearrange("p r j -> p (r j)").unsqueeze(1).to_broadcast([P, 16, 64])
-                pts = []
+                us[t] = u
+
+            def turn_blocks(t):
+                pts[t] = []
                 for k in range(HOPS):
                     pt = ps_t.tile([P, 1024], BF16, tag="t")
                     for bb in range(8):
                         if k < PLAIN_HOPS:
                             nc.tensor.matmul(
-                                out=pt[:, bb * P : (bb + 1) * P], lhsT=u[:, 8 * k + bb, :], rhs=ident[:], start=True, stop=True
+                                out=pt[:, bb * P : (bb + 1) * P], lhsT=us[t][:, 8 * k + bb, :], rhs=ident[:], start=True, stop=True
                             )
                         else:
-                            nc.tensor.transpose(out=pt[:, bb * P : (bb + 1) * P], in_=u[:, 8 * k + bb, :], identity=ident[:])
-                    pts.append(pt)
-                if t % 2 == 0:
-                    pf = ps_x.tile([P, 512], F32, tag="x")
-                    for a in range(4):
-                        nc.tensor.transpose(out=pf[:, a * P : (a + 1) * P], in_=ft_words[:, a, t // 2, :], identity=ident_f[:])
-                    pf_v = pf[:].bitcast(BF16).rearrange("p (m c e) -> p e m c", c=2, e=2)
-                    for e in range(2):
-                        cg = loop.tile([P, M, 4], BF16, align_bytes=64, tag="cg0", name="cg0", bufs=4)
-                        nc.scalar.copy(out=cg[:, :, 0:2], in_=pf_v[:, e])
-                        cg0s[t + e] = cg
-                cg0 = cg0s[t]
-                cg1 = loop.tile([P, M, 4], BF16, align_bytes=64)
+                            nc.tensor.transpose(out=pt[:, bb * P : (bb + 1) * P], in_=us[t][:, 8 * k + bb, :], identity=ident[:])
+                    pts[t].append(pt)
+
+            def mask_blocks(t):
+                ng = loop.tile([P, HOPS * 1024], BF16, align_bytes=64, name="ng")
+                keep_b = keep_g[:, t, :, :].rearrange("p r j -> p (r j)").unsqueeze(1).to_broadcast([P, 16, 64])
                 for k in range(HOPS):
                     nc.vector.tensor_tensor(
                         out=ng[:, k * 1024 : (k + 1) * 1024].rearrange("p (r c) -> p r c", c=64),
-                        in0=pts[k][:].rearrange("p (r c) -> p r c", c=64), in1=keep_b, op=ALU.mult,
+                        in0=pts[t][k][:].rearrange("p (r c) -> p r c", c=64), in1=keep_b, op=ALU.mult,
                     )
-                if t + FC_AHEAD < T:
-                    do_context(t + FC_AHEAD)
+                ngs[t] = ng
+
+            def quantise_norm(t):
+                nq = loop.tile([P, HOPS * M], U32, align_bytes=64, name="nq")
+                ns = loop.tile([P, HOPS * M], U8, align_bytes=64, name="ns")
                 for k in range(HOPS):
                     nc.vector.quantize_mx(
                         out=nq[:, k * M : (k + 1) * M].bitcast(FP8X4), scales=ns[:, k * M : (k + 1) * M],
-                        in_=ng[:, k * 1024 : (k + 1) * 1024],
+                        in_=ngs[t][:, k * 1024 : (k + 1) * 1024],
                     )
+                nqs[t] = nq
+                nss[t] = ns
 
-                def hop_pass(dst, i, a, e):
-                    nc.tensor.matmul_mx(
-                        out=dst,
-                        lhsT=fcq[:, t, e * P : (e + 1) * P].bitcast(FP8X4), lhsT_scale=fcs[:, t, e * P : (e + 1) * P],
-                        rhs=nq[:, i * M + a * P : i * M + (a + 1) * P].bitcast(FP8X4),
-                        rhs_scale=ns[:, i * M + a * P : i * M + (a + 1) * P],
-                        start=True, stop=True,
-                    )
+            def regroup_context(t):
+                fcg = loop.tile([P, D, 4], BF16, align_bytes=64, name="fcg", bufs=3)
+                if t % 2 == 1:
+                    nc.scalar.copy(out=fcg[:], in_=fc_view[:, t])
+                else:
+                    nc.vector.tensor_copy(out=fcg[:], in_=fc_view[:, t])
+                fcgs[t] = fcg
 
+            def quantise_context(t):
+                nc.vector.quantize_mx(
+                    out=fcq[:, t, :].bitcast(FP8X4), scales=fcs[:, t, :], in_=fcgs[t][:].rearrange("p d j -> p (d j)")
+                )
+
+            def turn_target(t):
+                pf = ps_x.tile([P, 512], F32, tag="x")
+                for a in range(4):
+                    nc.tensor.transpose(out=pf[:, a * P : (a + 1) * P], in_=ft_words[:, a, t // 2, :], identity=ident_f[:])
+                pf_v = pf[:].bitcast(BF16).rearrange("p (m c e) -> p e m c", c=2, e=2)
+                for e in range(2):
+                    cg = loop.tile([P, M, 4], BF16, align_bytes=64, name="cg0", bufs=4)
+                    nc.scalar.copy(out=cg[:, :, 0:2], in_=pf_v[:, e])
+                    cg0s[t + e] = cg
+
+            def hop_pass(dst, t, i, a, e):
+                nc.tensor.matmul_mx(
+                    out=dst,
+                    lhsT=fcq[:, t, e * P : (e + 1) * P].bitcast(FP8X4), lhsT_scale=fcs[:, t, e * P : (e + 1) * P],
+                    rhs=nqs[t][:, i * M + a * P : i * M + (a + 1) * P].bitcast(FP8X4),
+                    rhs_scale=nss[t][:, i * M + a * P : i * M + (a + 1) * P],
+                    start=True, stop=True,
+                )
+
+            def neighbour_sums(t):
                 p0 = ps_s.tile([P, 4, P], F32, tag="s")
                 for a in range(2):
                     for e in range(2):
-                        hop_pass(p0[:, a * 2 + e, :], 0, a, e)
-                p1 = []
+                        hop_pass(p0[:, a * 2 + e, :], t, 0, a, e)
+                p0s[t] = p0
+                p1s[t] = []
                 for a in range(2):
                     pp = ps_s.tile([P, 4, P], F32, tag="s")
                     for i in (1, 2):
                         for e in range(2):
-                            hop_pass(pp[:, (i - 1) * 2 + e, :], i, a, e)
-                    p1.append(pp)
+                            hop_pass(pp[:, (i - 1) * 2 + e, :], t, i, a, e)
+                    p1s[t].append(pp)
+
+            def add_target(t):
+                cg0 = cg0s[t]
+                cg1 = loop.tile([P, M, 4], BF16, align_bytes=64, name="cg1")
                 nc.vector.tensor_tensor(
                     out=cg0[:, :, 2:4].rearrange("p (a m) e -> p a m e", a=2),
-                    in0=p0[:].rearrange("p (a e) m -> p a m e", a=2),
+                    in0=p0s[t][:].rearrange("p (a e) m -> p a m e", a=2),
                     in1=cg0[:, :, 0:2].rearrange("p (a m) e -> p a m e", a=2), op=ALU.add,
                 )
                 for a in range(2):
                     nc.vector.tensor_tensor(
                         out=cg1[:, a * P : (a + 1) * P, :].rearrange("p m (h e) -> p m h e", h=2),
-                        in0=p1[a][:].rearrange("p (h e) m -> p m h e", h=2),
+                        in0=p1s[t][a][:].rearrange("p (h e) m -> p m h e", h=2),
                         in1=cg0[:, a * P : (a + 1) * P, 0:2].unsqueeze(2).to_broadcast([P, P, 2, 2]), op=ALU.add,
                     )
+                cg1s[t] = cg1
+
+            def quantise_cat(t):
                 nc.vector.quantize_mx(
-                    out=catq[:, t, 0, :].bitcast(FP8X4), scales=cats[:, t, 0, :], in_=cg0[:].rearrange("p m j -> p (m j)")
+                    out=catq[:, t, 0, :].bitcast(FP8X4), scales=cats[:, t, 0, :], in_=cg0s[t][:].rearrange("p m j -> p (m j)")
                 )
                 nc.vector.quantize_mx(
-                    out=catq[:, t, 1, :].bitcast(FP8X4), scales=cats[:, t, 1, :], in_=cg1[:].rearrange("p m j -> p (m j)")
+                    out=catq[:, t, 1, :].bitcast(FP8X4), scales=cats[:, t, 1, :], in_=cg1s[t][:].rearrange("p m j -> p (m j)")
                 )
-                if t == 5:
-                    do_weights()
+
+            def turn_weights(k):
+                pw = ps_x.tile([P, 1024], BF16, tag="x")
+                for bb in range(8):
+                    nc.tensor.transpose(out=pw[:, bb * P : (bb + 1) * P], in_=w_r[:, 8 * k + bb, :], identity=ident[:])
+                pw_v = pw[:].rearrange("p (o g j) -> p g o j", g=2, j=4)
+                for g in range(2):
+                    nc.scalar.copy(out=wtg[:, g, k * P : (k + 1) * P, :], in_=pw_v[:, g])
+
+            scale_blocks(0)
+            turn_blocks(0)
+            scale_blocks(1)
+            turn_target(0)
+            for t in range(FC_AHEAD):
+                regroup_context(t)
+            mask_blocks(0)
+            for t in range(FC_AHEAD):
+                quantise_context(t)
+            quantise_norm(0)
+            for t in range(T):
+                if t + 2 < T:
+                    scale_blocks(t + 2)
+                if t + 1 < T:
+                    turn_blocks(t + 1)
+                if t % 2 == 0 and t + 2 < T:
+                    turn_target(t + 2)
+                neighbour_sums(t)
+                if W_FIRST <= t < W_FIRST + 8:
+                    turn_weights(t - W_FIRST)
+                if t + FC_AHEAD < T:
+                    regroup_context(t + FC_AHEAD)
+                if t + 1 < T:
+                    mask_blocks(t + 1)
+                add_target(t)
+                if t + 1 < T:
+                    quantise_norm(t + 1)
+                quantise_cat(t)
+                if t + FC_AHEAD < T:
+                    quantise_context(t + FC_AHEAD)
+                if t == W_FIRST + 8:
+                    for g in range(2):
+                        nc.vector.quantize_mx(
+                            out=wq[:, g, :].bitcast(FP8X4), scales=ws[:, g, :],
+                            in_=wtg[:, g, :, :].rearrange("p o j -> p (o j)"),
+                        )
 
         with ExitStack() as ph2:
             opool = ph2.enter_context(tc.tile_pool(name="opool", bufs=4))
-            ps_o = ph2.enter_context(tc.psum_pool(name="ps_o", bufs=6))
+            ps_o = ph2.enter_context(tc.psum_pool(name="ps_o", bufs=8))
             for a in range(2):
                 for ob in range(8):
                     ot = opool.tile([P, P, T], F32)

@@ -17,8 +17,7 @@ C = (HOPS + 1) * D
 FLOPS = 2 * T * HOPS * M * N * D + 2 * M * T * CO * C
 
 NB = HOPS * M * 4 // P
-VEC_SHARE = 4
-FC_AHEAD = 4
+SHARE = 6
 PLAIN_HOPS = 2
 W_FIRST = 4
 
@@ -116,7 +115,7 @@ def tile_graphaggregation_pa_t_kernel(tc, feat_context, feat_target, adj, missin
             r_rep = const.tile([P, 4, 6 * T], F32)
             nc.vector.tensor_copy(out=r_rep[:], in_=pr[:])
 
-            fc_view = fc_raw[:].rearrange("p j (d t) -> p t d j", t=T)
+            fc_view = fc_raw[:].rearrange("p j (d q t) -> p q d j t", q=4, t=4)
             ft_words = ft_r[:].bitcast(F32).rearrange("p a (d w) -> p a w d", w=T // 2)
             us, pts, ngs, nqs, nss, cg0s, cg1s, fcgs, p0s, p1s = {}, {}, {}, {}, {}, {}, {}, {}, {}, {}
 
@@ -124,8 +123,12 @@ def tile_graphaggregation_pa_t_kernel(tc, feat_context, feat_target, adj, missin
                 u = loop.tile([P, NB, P], BF16, bufs=3, name="u")
                 for b in range(NB):
                     sc = r_rep[:, b % 4, (b // 4) * T + t : (b // 4) * T + t + 1]
-                    if b % VEC_SHARE == VEC_SHARE - 1:
+                    if b % SHARE == SHARE - 1:
                         nc.vector.tensor_scalar(out=u[:, b, :], in0=adj_r[:, b, :], scalar1=sc, scalar2=None, op0=ALU.mult)
+                    elif b % SHARE == 2:
+                        nc.gpsimd.tensor_scalar(
+                            out=u[:, b, :], in0=adj_r[:, b, :], scalar1=sc, scalar2=0.0, op0=ALU.mult, op1=ALU.add
+                        )
                     else:
                         nc.scalar.activation(out=u[:, b, :], in_=adj_r[:, b, :], func=ACT.Copy, scale=sc)
                 us[t] = u
@@ -164,17 +167,19 @@ def tile_graphaggregation_pa_t_kernel(tc, feat_context, feat_target, adj, missin
                 nqs[t] = nq
                 nss[t] = ns
 
-            def regroup_context(t):
-                fcg = loop.tile([P, D, 4], BF16, align_bytes=64, name="fcg", bufs=3)
-                if t % 2 == 1:
-                    nc.scalar.copy(out=fcg[:], in_=fc_view[:, t])
+            def regroup_context(q):
+                fcg = loop.tile([P, 4, D, 4], BF16, align_bytes=64, name="fcg", bufs=1)
+                if q < 2:
+                    nc.vector.tensor_copy(out=fcg[:].rearrange("p t d j -> p d j t"), in_=fc_view[:, q])
                 else:
-                    nc.vector.tensor_copy(out=fcg[:], in_=fc_view[:, t])
-                fcgs[t] = fcg
+                    nc.scalar.copy(out=fcg[:].rearrange("p t d j -> p d j t"), in_=fc_view[:, q])
+                fcgs[q] = fcg
 
-            def quantise_context(t):
+            def quantise_context(q):
                 nc.vector.quantize_mx(
-                    out=fcq[:, t, :].bitcast(FP8X4), scales=fcs[:, t, :], in_=fcgs[t][:].rearrange("p d j -> p (d j)")
+                    out=fcq[:, 4 * q : 4 * q + 4, :].rearrange("p t d -> p (t d)").bitcast(FP8X4),
+                    scales=fcs[:, 4 * q : 4 * q + 4, :].rearrange("p t d -> p (t d)"),
+                    in_=fcgs[q][:].rearrange("p t d j -> p (t d j)"),
                 )
 
             def turn_target(t):
@@ -246,11 +251,9 @@ def tile_graphaggregation_pa_t_kernel(tc, feat_context, feat_target, adj, missin
             turn_blocks(0)
             scale_blocks(1)
             turn_target(0)
-            for t in range(FC_AHEAD):
-                regroup_context(t)
+            regroup_context(0)
             mask_blocks(0)
-            for t in range(FC_AHEAD):
-                quantise_context(t)
+            quantise_context(0)
             quantise_norm(0)
             for t in range(T):
                 if t + 2 < T:
@@ -262,16 +265,16 @@ def tile_graphaggregation_pa_t_kernel(tc, feat_context, feat_target, adj, missin
                 neighbour_sums(t)
                 if W_FIRST <= t < W_FIRST + 8:
                     turn_weights(t - W_FIRST)
-                if t + FC_AHEAD < T:
-                    regroup_context(t + FC_AHEAD)
+                if t % 4 == 0 and t + 4 < T:
+                    regroup_context(t // 4 + 1)
                 if t + 1 < T:
                     mask_blocks(t + 1)
                 add_target(t)
                 if t + 1 < T:
                     quantise_norm(t + 1)
                 quantise_cat(t)
-                if t + FC_AHEAD < T:
-                    quantise_context(t + FC_AHEAD)
+                if t % 4 == 1 and t + 3 < T:
+                    quantise_context(t // 4 + 1)
                 if t == W_FIRST + 8:
                     for g in range(2):
                         nc.vector.quantize_mx(
@@ -303,5 +306,12 @@ def tile_graphaggregation_pa_t_kernel(tc, feat_context, feat_target, adj, missin
                             in1=bias_bc[:, ob * P : (ob + 1) * P].unsqueeze(2).to_broadcast([P, P, 4]), op=ALU.add,
                         )
                     flat = ot[:].rearrange("p o t -> p (o t)")
-                    nc.scalar.activation(out=flat, in_=flat, func=ACT.Relu)
-                    nc.sync.dma_start(out=out_v[:, a, ob * P * T : (ob + 1) * P * T], in_=flat)
+                    half = P * T // 2
+                    nc.scalar.activation(out=flat[:, 0:half], in_=flat[:, 0:half], func=ACT.Relu)
+                    nc.gpsimd.tensor_scalar(
+                        out=flat[:, half : 2 * half], in0=flat[:, half : 2 * half], scalar1=0.0, scalar2=0.0, op0=ALU.max, op1=ALU.add
+                    )
+                    for h in range(2):
+                        nc.sync.dma_start(
+                            out=out_v[:, a, (2 * ob + h) * half : (2 * ob + h + 1) * half], in_=flat[:, h * half : (h + 1) * half]
+                        )

@@ -17,7 +17,7 @@ C = (HOPS + 1) * D
 FLOPS = 2 * T * HOPS * M * N * D + 2 * M * T * CO * C
 
 NB = HOPS * M * 4 // P
-SHARE = 6
+VEC_SHARE = 3
 PLAIN_HOPS = 2
 W_FIRST = 4
 
@@ -123,12 +123,8 @@ def tile_graphaggregation_pa_t_kernel(tc, feat_context, feat_target, adj, missin
                 u = loop.tile([P, NB, P], BF16, bufs=3, name="u")
                 for b in range(NB):
                     sc = r_rep[:, b % 4, (b // 4) * T + t : (b // 4) * T + t + 1]
-                    if b % SHARE == SHARE - 1:
+                    if b % VEC_SHARE == VEC_SHARE - 1:
                         nc.vector.tensor_scalar(out=u[:, b, :], in0=adj_r[:, b, :], scalar1=sc, scalar2=None, op0=ALU.mult)
-                    elif b % SHARE == 2:
-                        nc.gpsimd.tensor_scalar(
-                            out=u[:, b, :], in0=adj_r[:, b, :], scalar1=sc, scalar2=0.0, op0=ALU.mult, op1=ALU.add
-                        )
                     else:
                         nc.scalar.activation(out=u[:, b, :], in_=adj_r[:, b, :], func=ACT.Copy, scale=sc)
                 us[t] = u
@@ -307,11 +303,8 @@ def tile_graphaggregation_pa_t_kernel(tc, feat_context, feat_target, adj, missin
                         )
                     flat = ot[:].rearrange("p o t -> p (o t)")
                     half = P * T // 2
-                    nc.scalar.activation(out=flat[:, 0:half], in_=flat[:, 0:half], func=ACT.Relu)
-                    nc.gpsimd.tensor_scalar(
-                        out=flat[:, half : 2 * half], in0=flat[:, half : 2 * half], scalar1=0.0, scalar2=0.0, op0=ALU.max, op1=ALU.add
-                    )
                     for h in range(2):
+                        nc.scalar.activation(out=flat[:, h * half : (h + 1) * half], in_=flat[:, h * half : (h + 1) * half], func=ACT.Relu)
                         nc.sync.dma_start(
                             out=out_v[:, a, (2 * ob + h) * half : (2 * ob + h + 1) * half], in_=flat[:, h * half : (h + 1) * half]
                         )

@@ -35,11 +35,7 @@ def tile_graphaggregation_pa_t_kernel(tc, feat_context, feat_target, adj, missin
         top.enter_context(tc.manual_schedule())
         const = top.enter_context(tc.tile_pool(name="const", bufs=1))
 
-        mask_pad = const.tile([P, N], BF16)
-        nc.vector.memset(mask_pad[:], 0.0)
-        nc.sync.dma_start(out=mask_pad[0:T, :], in_=mask_v)
         adj_r = const.tile([P, NB, P], BF16)
-        nc.sync.dma_start(out=adj_r[:], in_=adj_v)
         ident = const.tile([P, P], BF16)
         make_identity(nc, ident[:])
         ident_f = const.tile([P, P], F32)
@@ -55,75 +51,81 @@ def tile_graphaggregation_pa_t_kernel(tc, feat_context, feat_target, adj, missin
 
         with ExitStack() as ph1:
             big = ph1.enter_context(tc.tile_pool(name="big", bufs=1))
-            loop = ph1.enter_context(tc.tile_pool(name="loop", bufs=2))
             ps_t = ph1.enter_context(tc.psum_pool(name="ps_t", bufs=3))
             ps_s = ph1.enter_context(tc.psum_pool(name="ps_s", bufs=3))
             ps_x = ph1.enter_context(tc.psum_pool(name="ps_x", bufs=2))
 
-            fc_raw = big.tile([P, 4, D * T], BF16)
-            for j in range(4):
-                nc.sync.dma_start(out=fc_raw[:, j, :], in_=fc_v[:, j, :])
-            ft_r = big.tile([P, 4, P * T], BF16)
-            nc.sync.dma_start(out=ft_r[:], in_=ft_v)
-            w_r = big.tile([P, 64, P], BF16)
-            nc.sync.dma_start(out=w_r[:], in_=w_v)
-            nc.sync.dma_start(out=bias_bc[:], in_=b_mlp.partition_broadcast(P))
-            wtg = big.tile([P, 2, CO, 4], BF16, align_bytes=64)
-
-            spread = const.tile([P, 4, 32, 4], F32)
-            for b4 in range(4):
-                nc.vector.tensor_copy(
-                    out=spread[:, b4, :, :], in_=ident_f[:, 32 * b4 : 32 * b4 + 32].unsqueeze(2).to_broadcast([P, 32, 4])
-                )
-            pm = ps_x.tile([P, 1024], BF16, tag="x")
-            for j in range(4):
-                nc.tensor.transpose(out=pm[:, j * P : (j + 1) * P], in_=mask_pad[:, j * P : (j + 1) * P], identity=ident[:])
-            keep_t = const.tile([P, 4, 32], BF16)
-            nc.vector.tensor_scalar(
-                out=keep_t[:], in0=pm[:, 0:N].rearrange("p (j t) -> p j t", j=4)[:, :, 0:32],
-                scalar1=-1.0, scalar2=1.0, op0=ALU.mult, op1=ALU.add,
-            )
-            keep_g = const.tile([P, T, 16, 4], BF16)
-            nc.vector.tensor_scalar(
-                out=keep_g[:],
-                in0=pm[:, 0:N].rearrange("p (j t) -> p t j", j=4)[:, 0:T, :].unsqueeze(2).to_broadcast([P, T, 16, 4]),
-                scalar1=-1.0, scalar2=1.0, op0=ALU.mult, op1=ALU.add,
-            )
-            adj_t = const.tile([P, 4, HOPS * M], BF16)
-            for k in range(HOPS):
-                pa = ps_t.tile([P, 1024], BF16, tag="t")
-                for bb in range(8):
-                    nc.tensor.transpose(out=pa[:, bb * P : (bb + 1) * P], in_=adj_r[:, 8 * k + bb, :], identity=ident[:])
-                nc.scalar.copy(out=adj_t[:, :, k * M : (k + 1) * M], in_=pa[:].rearrange("p (c j) -> p j c", j=4))
-            psum_s = ps_x.tile([P, 6, 32], F32, tag="x")
-            for g in range(6):
+            with tc.tile_pool(name="pre", bufs=1) as pre:
+                mask_pad = pre.tile([P, N], BF16)
+                nc.vector.memset(mask_pad[:], 0.0)
+                nc.sync.dma_start(out=mask_pad[0:T, :], in_=mask_v)
+                for k in range(HOPS):
+                    nc.sync.dma_start(out=adj_r[:, 8 * k : 8 * k + 8, :], in_=adj_v[:, 8 * k : 8 * k + 8, :])
+                fc_raw = big.tile([P, 4, D * T], BF16)
                 for j in range(4):
-                    nc.tensor.matmul(
-                        out=psum_s[:, g, :], lhsT=adj_t[:, j, g * P : (g + 1) * P], rhs=keep_t[:, j, :],
-                        start=(j == 0), stop=(j == 3),
+                    nc.sync.dma_start(out=fc_raw[:, j, :], in_=fc_v[:, j, :])
+                ft_r = big.tile([P, 4, P * T], BF16)
+                nc.sync.dma_start(out=ft_r[:], in_=ft_v)
+                w_r = big.tile([P, 64, P], BF16)
+                nc.sync.dma_start(out=w_r[:], in_=w_v)
+                nc.sync.dma_start(out=bias_bc[:], in_=b_mlp.partition_broadcast(P))
+                wtg = big.tile([P, 2, CO, 4], BF16, align_bytes=64)
+
+                spread = pre.tile([P, 4, 32, 4], F32)
+                for b4 in range(4):
+                    nc.vector.tensor_copy(
+                        out=spread[:, b4, :, :], in_=ident_f[:, 32 * b4 : 32 * b4 + 32].unsqueeze(2).to_broadcast([P, 32, 4])
                     )
-            s1 = const.tile([P, 6, T], F32)
-            nc.vector.tensor_scalar_add(out=s1[:], in0=psum_s[:, :, 0:T], scalar1=1.0)
-            rcp = const.tile([P, 6, T], F32)
-            nc.vector.reciprocal(out=rcp[:], in_=s1[:])
-            pr = ps_s.tile([P, 4, 6 * T], F32, tag="s")
-            for b4 in range(4):
-                nc.tensor.matmul(
-                    out=pr[:, b4, :], lhsT=spread[:, b4, :, :].rearrange("p a b -> p (a b)"),
-                    rhs=rcp[:].rearrange("p g t -> p (g t)"), start=True, stop=True,
+                pm = ps_x.tile([P, 1024], BF16, tag="x")
+                for j in range(4):
+                    nc.tensor.transpose(out=pm[:, j * P : (j + 1) * P], in_=mask_pad[:, j * P : (j + 1) * P], identity=ident[:])
+                keep_t = const.tile([P, 4, 32], BF16)
+                nc.vector.tensor_scalar(
+                    out=keep_t[:], in0=pm[:, 0:N].rearrange("p (j t) -> p j t", j=4)[:, :, 0:32],
+                    scalar1=-1.0, scalar2=1.0, op0=ALU.mult, op1=ALU.add,
                 )
-            r_rep = const.tile([P, 4, 6 * T], F32)
-            nc.vector.tensor_copy(out=r_rep[:], in_=pr[:])
+                keep_g = const.tile([P, T, 16, 4], BF16)
+                nc.vector.tensor_scalar(
+                    out=keep_g[:],
+                    in0=pm[:, 0:N].rearrange("p (j t) -> p t j", j=4)[:, 0:T, :].unsqueeze(2).to_broadcast([P, T, 16, 4]),
+                    scalar1=-1.0, scalar2=1.0, op0=ALU.mult, op1=ALU.add,
+                )
+                adj_t = pre.tile([P, 4, HOPS * M], BF16)
+                for k in range(HOPS):
+                    pa = ps_t.tile([P, 1024], BF16, tag="t")
+                    for bb in range(8):
+                        nc.tensor.transpose(out=pa[:, bb * P : (bb + 1) * P], in_=adj_r[:, 8 * k + bb, :], identity=ident[:])
+                    nc.scalar.copy(out=adj_t[:, :, k * M : (k + 1) * M], in_=pa[:].rearrange("p (c j) -> p j c", j=4))
+                psum_s = ps_x.tile([P, 6, 32], F32, tag="x")
+                for g in range(6):
+                    for j in range(4):
+                        nc.tensor.matmul(
+                            out=psum_s[:, g, :], lhsT=adj_t[:, j, g * P : (g + 1) * P], rhs=keep_t[:, j, :],
+                            start=(j == 0), stop=(j == 3),
+                        )
+                s1 = pre.tile([P, 6, T], F32)
+                nc.vector.tensor_scalar_add(out=s1[:], in0=psum_s[:, :, 0:T], scalar1=1.0)
+                rcp = pre.tile([P, 6, T], F32)
+                nc.vector.reciprocal(out=rcp[:], in_=s1[:])
+                pr = ps_s.tile([P, 4, 6 * T], F32, tag="s")
+                for b4 in range(4):
+                    nc.tensor.matmul(
+                        out=pr[:, b4, :], lhsT=spread[:, b4, :, :].rearrange("p a b -> p (a b)"),
+                        rhs=rcp[:].rearrange("p g t -> p (g t)"), start=True, stop=True,
+                    )
+                r_rep = const.tile([P, 4, 6 * T], F32)
+                nc.vector.tensor_copy(out=r_rep[:], in_=pr[:])
+            loop = ph1.enter_context(tc.tile_pool(name="loop", bufs=2))
 
             fc_view = fc_raw[:].rearrange("p j (d q t) -> p q d j t", q=4, t=4)
             ft_words = ft_r[:].bitcast(F32).rearrange("p a (d w) -> p a w d", w=T // 2)
-            us, pts, ngs, nqs, nss, cg0s, cg1s, fcgs, p0s, p1s = {}, {}, {}, {}, {}, {}, {}, {}, {}, {}
+            us, pts, ngs, nqs, nss, cg0s, fcgs, p0s, p1s = {}, {}, {}, {}, {}, {}, {}, {}, {}
 
             def scale_blocks(t):
                 u = loop.tile([P, NB, P], BF16, bufs=3, name="u")
                 for b in range(NB):
                     sc = r_rep[:, b % 4, (b // 4) * T + t : (b // 4) * T + t + 1]
-                    if b % VEC_SHARE == VEC_SHARE - 1:
+                    if (b % VEC_SHARE != 0) if t == 0 else (b % VEC_SHARE == VEC_SHARE - 1):
                         nc.vector.tensor_scalar(out=u[:, b, :], in0=adj_r[:, b, :], scalar1=sc, scalar2=None, op0=ALU.mult)
                     else:
                         nc.scalar.activation(out=u[:, b, :], in_=adj_r[:, b, :], func=ACT.Copy, scale=sc)
@@ -155,10 +157,10 @@ def tile_graphaggregation_pa_t_kernel(tc, feat_context, feat_target, adj, missin
             def quantise_norm(t):
                 nq = loop.tile([P, HOPS * M], U32, align_bytes=64, name="nq")
                 ns = loop.tile([P, HOPS * M], U8, align_bytes=64, name="ns")
-                for k in range(HOPS):
+                for lo, hi in ((0, 2), (2, 3)):
                     nc.vector.quantize_mx(
-                        out=nq[:, k * M : (k + 1) * M].bitcast(FP8X4), scales=ns[:, k * M : (k + 1) * M],
-                        in_=ngs[t][:, k * 1024 : (k + 1) * 1024],
+                        out=nq[:, lo * M : hi * M].bitcast(FP8X4), scales=ns[:, lo * M : hi * M],
+                        in_=ngs[t][:, lo * 1024 : hi * 1024],
                     )
                 nqs[t] = nq
                 nss[t] = ns
@@ -184,8 +186,8 @@ def tile_graphaggregation_pa_t_kernel(tc, feat_context, feat_target, adj, missin
                     nc.tensor.transpose(out=pf[:, a * P : (a + 1) * P], in_=ft_words[:, a, t // 2, :], identity=ident_f[:])
                 pf_v = pf[:].bitcast(BF16).rearrange("p (m c e) -> p e m c", c=2, e=2)
                 for e in range(2):
-                    cg = loop.tile([P, M, 4], BF16, align_bytes=64, name="cg0", bufs=4)
-                    nc.scalar.copy(out=cg[:, :, 0:2], in_=pf_v[:, e])
+                    cg = loop.tile([P, 2, M, 4], BF16, align_bytes=64, name="cg", bufs=4)
+                    nc.scalar.copy(out=cg[:, 0, :, 0:2], in_=pf_v[:, e])
                     cg0s[t + e] = cg
 
             def hop_pass(dst, t, i, a, e):
@@ -212,8 +214,8 @@ def tile_graphaggregation_pa_t_kernel(tc, feat_context, feat_target, adj, missin
                     p1s[t].append(pp)
 
             def add_target(t):
-                cg0 = cg0s[t]
-                cg1 = loop.tile([P, M, 4], BF16, align_bytes=64, name="cg1")
+                cg0 = cg0s[t][:, 0]
+                cg1 = cg0s[t][:, 1]
                 nc.vector.tensor_tensor(
                     out=cg0[:, :, 2:4].rearrange("p (a m) e -> p a m e", a=2),
                     in0=p0s[t][:].rearrange("p (a e) m -> p a m e", a=2),
@@ -225,14 +227,12 @@ def tile_graphaggregation_pa_t_kernel(tc, feat_context, feat_target, adj, missin
                         in0=p1s[t][a][:].rearrange("p (h e) m -> p m h e", h=2),
                         in1=cg0[:, a * P : (a + 1) * P, 0:2].unsqueeze(2).to_broadcast([P, P, 2, 2]), op=ALU.add,
                     )
-                cg1s[t] = cg1
 
             def quantise_cat(t):
                 nc.vector.quantize_mx(
-                    out=catq[:, t, 0, :].bitcast(FP8X4), scales=cats[:, t, 0, :], in_=cg0s[t][:].rearrange("p m j -> p (m j)")
-                )
-                nc.vector.quantize_mx(
-                    out=catq[:, t, 1, :].bitcast(FP8X4), scales=cats[:, t, 1, :], in_=cg1s[t][:].rearrange("p m j -> p (m j)")
+                    out=catq[:, t, :, :].rearrange("p g m -> p (g m)").bitcast(FP8X4),
+                    scales=cats[:, t, :, :].rearrange("p g m -> p (g m)"),
+                    in_=cg0s[t][:].rearrange("p g m j -> p (g m j)"),
                 )
 
             def turn_weights(k):
@@ -279,8 +279,8 @@ def tile_graphaggregation_pa_t_kernel(tc, feat_context, feat_target, adj, missin
                         )
 
         with ExitStack() as ph2:
-            opool = ph2.enter_context(tc.tile_pool(name="opool", bufs=4))
-            ps_o = ph2.enter_context(tc.psum_pool(name="ps_o", bufs=8))
+            opool = ph2.enter_context(tc.tile_pool(name="opool", bufs=4, reuse_waits="tile"))
+            ps_o = ph2.enter_context(tc.psum_pool(name="ps_o", bufs=8, reuse_waits="tile"))
             for a in range(2):
                 for ob in range(8):
                     ot = opool.tile([P, P, T], F32)

@@ -16,295 +16,394 @@ T, M, N, D, HOPS, CO = 16, 256, 512, 256, 3, 1024
 C = (HOPS + 1) * D
 FLOPS = 2 * T * HOPS * M * N * D + 2 * M * T * CO * C
 
-NB = HOPS * M * 4 // P
-VEC_SHARE = 3
-PLAIN_HOPS = 2
-W_FIRST = 4
+TP = T // 2
+STEPS = 2 * TP
+KO = CO // P
+SHARE = [3, 3, 3, 3, 3, 3, 2, 2, 6, 6, 6, 6]
 
 
 def tile_graphaggregation_pa_t_kernel(tc, feat_context, feat_target, adj, missing_mask_context, W_mlp, b_mlp, out):
     nc = tc.nc
-    fc_v = feat_context.rearrange("o (j p) d t -> p (o j) (d t)", p=P)
-    ft_v = feat_target.rearrange("o m (e d) t -> (o m e) (d t)", e=2).rearrange("(a q) x -> q a x", q=P)
-    adj_v = adj.rearrange("o i m (j p) -> (o i m j) p", p=P).rearrange("(b q) p -> q b p", q=P)
+    fc_v = feat_context.rearrange("o (u p e) d t -> p (o u) e (d t)", p=P, e=2)
+    ft_v = feat_target.rearrange("o (a m) d t -> m (o a) (d t)", m=P)
+    adj_v = adj.rearrange("o i (a m) n -> m a (o i) n", m=P)
     mask_v = missing_mask_context.rearrange("o t n -> (o t) n")
-    w_v = W_mlp.rearrange("o (r p) -> (o r) p", p=P).rearrange("(b q) p -> q b p", q=P)
-    out_v = out.rearrange("o (a m) c t -> m (o a) (c t)", m=P)
+    w_v = W_mlp.rearrange("(p k) c -> p k c", k=KO)
+    wn_v = W_mlp.rearrange("(b q) c -> q b c", q=P)
+    out_o = out.rearrange("o (a m) (p k) t -> p (o a) m (k t)", m=P, k=KO)
+    out_m = out.rearrange("o (a m) c t -> m (o a) (c t)", m=P)
 
     with ExitStack() as top:
         top.enter_context(tc.manual_schedule())
         const = top.enter_context(tc.tile_pool(name="const", bufs=1))
 
-        adj_r = const.tile([P, NB, P], BF16)
-        ident = const.tile([P, P], BF16)
-        make_identity(nc, ident[:])
-        ident_f = const.tile([P, P], F32)
-        make_identity(nc, ident_f[:])
+        adj_r = const.tile([P, 2, HOPS, N], BF16)
+        ident = const.tile([P, P], F32)
         bias_bc = const.tile([P, CO], BF16)
-
+        bias_col = const.tile([P, KO], BF16)
+        keep_t = const.tile([P, 4, T], BF16)
+        keep_g = const.tile([P, T, 4], BF16)
+        rcp = const.tile([P, 2, HOPS, T], F32)
         fcq = const.tile([P, T, D], U32, align_bytes=64)
         fcs = const.tile([P, T, D], U8, align_bytes=64)
-        catq = const.tile([P, T, 2, M], U32, align_bytes=64)
-        cats = const.tile([P, T, 2, M], U8, align_bytes=64)
-        wq = const.tile([P, 2, CO], U32, align_bytes=64)
-        ws = const.tile([P, 2, CO], U8, align_bytes=64)
+        catq = const.tile([P, 2, TP, 512], U32, align_bytes=64)
+        cats = const.tile([P, 2, TP, 512], U8, align_bytes=64)
+        wqk = const.tile([P, 2, CO], U32, align_bytes=64)
+        wsk = const.tile([P, 2, CO], U8, align_bytes=64)
+        wqn = const.tile([P, KO, 2, P], U32, align_bytes=64)
+        wsn = const.tile([P, KO, 2, P], U8, align_bytes=64)
 
         with ExitStack() as ph1:
-            big = ph1.enter_context(tc.tile_pool(name="big", bufs=1))
+            loop = ph1.enter_context(tc.tile_pool(name="loop", bufs=2))
             ps_t = ph1.enter_context(tc.psum_pool(name="ps_t", bufs=3))
             ps_s = ph1.enter_context(tc.psum_pool(name="ps_s", bufs=3))
             ps_x = ph1.enter_context(tc.psum_pool(name="ps_x", bufs=2))
+            ft_r = loop.tile([P, 2, D * T], BF16, bufs=1)
+            with tc.tile_pool(name="big", bufs=1) as big:
 
-            with tc.tile_pool(name="pre", bufs=1) as pre:
-                mask_pad = pre.tile([P, N], BF16)
+                mask_pad = big.tile([P, N], BF16)
                 nc.vector.memset(mask_pad[:], 0.0)
+                make_identity(nc, ident[:])
                 nc.sync.dma_start(out=mask_pad[0:T, :], in_=mask_v)
-                for k in range(HOPS):
-                    nc.sync.dma_start(out=adj_r[:, 8 * k : 8 * k + 8, :], in_=adj_v[:, 8 * k : 8 * k + 8, :])
+                nc.sync.dma_start(out=adj_r[:, 0], in_=adj_v[:, 0])
                 fc_raw = big.tile([P, 4, D * T], BF16)
-                for j in range(4):
-                    nc.sync.dma_start(out=fc_raw[:, j, :], in_=fc_v[:, j, :])
-                ft_r = big.tile([P, 4, P * T], BF16)
-                nc.sync.dma_start(out=ft_r[:], in_=ft_v)
-                w_r = big.tile([P, 64, P], BF16)
+                for h in range(2):
+                    for u in range(2):
+                        nc.sync.dma_start(
+                            out=fc_raw[:, 2 * u : 2 * u + 2, h * 2048 : (h + 1) * 2048], in_=fc_v[:, u, :, h * 2048 : (h + 1) * 2048]
+                        )
+                nc.sync.dma_start(out=ft_r[:, 0, :], in_=ft_v[:, 0, :])
+                nc.sync.dma_start(out=adj_r[:, 1], in_=adj_v[:, 1])
+                w_r = big.tile([P, KO, C], BF16, tag="w", align_bytes=64)
                 nc.sync.dma_start(out=w_r[:], in_=w_v)
+                nc.sync.dma_start(out=ft_r[:, 1, :], in_=ft_v[:, 1, :])
+                nc.sync.dma_start(out=bias_col[:], in_=b_mlp.rearrange("(p k) -> p k", k=KO))
                 nc.sync.dma_start(out=bias_bc[:], in_=b_mlp.partition_broadcast(P))
                 wtg = big.tile([P, 2, CO, 4], BF16, align_bytes=64)
 
-                spread = pre.tile([P, 4, 32, 4], F32)
-                for b4 in range(4):
-                    nc.vector.tensor_copy(
-                        out=spread[:, b4, :, :], in_=ident_f[:, 32 * b4 : 32 * b4 + 32].unsqueeze(2).to_broadcast([P, 32, 4])
-                    )
-                pm = ps_x.tile([P, 1024], BF16, tag="x")
-                for j in range(4):
-                    nc.tensor.transpose(out=pm[:, j * P : (j + 1) * P], in_=mask_pad[:, j * P : (j + 1) * P], identity=ident[:])
-                keep_t = const.tile([P, 4, 32], BF16)
+                adj_w = adj_r[:].rearrange("p a i n -> p (a i n)").bitcast(F32).rearrange("p (a i u q) -> p a i u q", a=2, i=HOPS, u=2)
+                mask_w = mask_pad[:].bitcast(F32)
+                ft_w = ft_r[:].rearrange("p a x -> p (a x)").bitcast(F32).rearrange("p (a d e w) -> p a e w d", a=2, e=2, w=TP)
+                w_w = w_r[:].rearrange("p k c -> p (k c)").bitcast(F32).rearrange("p (k h q) -> p k h q", k=KO, q=P)
+
+                pm = ps_x.tile([P, 512], F32, tag="x")
+                for u in range(2):
+                    nc.tensor.transpose(out=pm[:, u * P : (u + 1) * P], in_=mask_w[:, u * P : (u + 1) * P], identity=ident[:])
+                pm_v = pm[:].bitcast(BF16)[:, 0 : 4 * P].rearrange("p (u q e) -> p u e q", u=2, e=2)[:, :, :, 0:T]
                 nc.vector.tensor_scalar(
-                    out=keep_t[:], in0=pm[:, 0:N].rearrange("p (j t) -> p j t", j=4)[:, :, 0:32],
-                    scalar1=-1.0, scalar2=1.0, op0=ALU.mult, op1=ALU.add,
+                    out=keep_t[:].rearrange("p (u e) t -> p u e t", u=2), in0=pm_v, scalar1=-1.0, scalar2=1.0, op0=ALU.mult, op1=ALU.add
                 )
-                keep_g = const.tile([P, T, 16, 4], BF16)
                 nc.vector.tensor_scalar(
-                    out=keep_g[:],
-                    in0=pm[:, 0:N].rearrange("p (j t) -> p t j", j=4)[:, 0:T, :].unsqueeze(2).to_broadcast([P, T, 16, 4]),
-                    scalar1=-1.0, scalar2=1.0, op0=ALU.mult, op1=ALU.add,
+                    out=keep_g[:].rearrange("p t (u e) -> p u e t", u=2), in0=pm_v, scalar1=-1.0, scalar2=1.0, op0=ALU.mult, op1=ALU.add
                 )
-                adj_t = pre.tile([P, 4, HOPS * M], BF16)
-                for k in range(HOPS):
-                    pa = ps_t.tile([P, 1024], BF16, tag="t")
-                    for bb in range(8):
-                        nc.tensor.transpose(out=pa[:, bb * P : (bb + 1) * P], in_=adj_r[:, 8 * k + bb, :], identity=ident[:])
-                    nc.scalar.copy(out=adj_t[:, :, k * M : (k + 1) * M], in_=pa[:].rearrange("p (c j) -> p j c", j=4))
-                psum_s = ps_x.tile([P, 6, 32], F32, tag="x")
-                for g in range(6):
-                    for j in range(4):
-                        nc.tensor.matmul(
-                            out=psum_s[:, g, :], lhsT=adj_t[:, j, g * P : (g + 1) * P], rhs=keep_t[:, j, :],
-                            start=(j == 0), stop=(j == 3),
-                        )
-                s1 = pre.tile([P, 6, T], F32)
-                nc.vector.tensor_scalar_add(out=s1[:], in0=psum_s[:, :, 0:T], scalar1=1.0)
-                rcp = pre.tile([P, 6, T], F32)
-                nc.vector.reciprocal(out=rcp[:], in_=s1[:])
-                pr = ps_s.tile([P, 4, 6 * T], F32, tag="s")
-                for b4 in range(4):
-                    nc.tensor.matmul(
-                        out=pr[:, b4, :], lhsT=spread[:, b4, :, :].rearrange("p a b -> p (a b)"),
-                        rhs=rcp[:].rearrange("p g t -> p (g t)"), start=True, stop=True,
-                    )
-                r_rep = const.tile([P, 4, 6 * T], F32)
-                nc.vector.tensor_copy(out=r_rep[:], in_=pr[:])
-            loop = ph1.enter_context(tc.tile_pool(name="loop", bufs=2))
 
-            fc_view = fc_raw[:].rearrange("p j (d q t) -> p q d j t", q=4, t=4)
-            ft_words = ft_r[:].bitcast(F32).rearrange("p a (d w) -> p a w d", w=T // 2)
-            us, pts, ngs, nqs, nss, cg0s, fcgs, p0s, p1s = {}, {}, {}, {}, {}, {}, {}, {}, {}
+                adj_ts, sums = {}, {}
 
-            def scale_blocks(t):
-                u = loop.tile([P, NB, P], BF16, bufs=3, name="u")
-                for b in range(NB):
-                    sc = r_rep[:, b % 4, (b // 4) * T + t : (b // 4) * T + t + 1]
-                    if (b % VEC_SHARE != 0) if t == 0 else (b % VEC_SHARE == VEC_SHARE - 1):
-                        nc.vector.tensor_scalar(out=u[:, b, :], in0=adj_r[:, b, :], scalar1=sc, scalar2=None, op0=ALU.mult)
-                    else:
-                        nc.scalar.activation(out=u[:, b, :], in_=adj_r[:, b, :], func=ACT.Copy, scale=sc)
-                us[t] = u
-
-            def turn_blocks(t):
-                pts[t] = []
-                for k in range(HOPS):
-                    pt = ps_t.tile([P, 1024], BF16, tag="t")
-                    for bb in range(8):
-                        if k < PLAIN_HOPS:
-                            nc.tensor.matmul(
-                                out=pt[:, bb * P : (bb + 1) * P], lhsT=us[t][:, 8 * k + bb, :], rhs=ident[:], start=True, stop=True
-                            )
+                def turn_adj(a):
+                    adj_t = big.tile([P, 2, HOPS * P], F32, name="adj_t")
+                    for u in range(2):
+                        pa = ps_x.tile([P, 512], F32, tag="x")
+                        for i in range(HOPS):
+                            nc.tensor.transpose(out=pa[:, i * P : (i + 1) * P], in_=adj_w[:, a, i, u, :], identity=ident[:])
+                        if u == 0:
+                            nc.vector.tensor_copy(out=adj_t[:, u, :], in_=pa[:, 0 : HOPS * P])
                         else:
-                            nc.tensor.transpose(out=pt[:, bb * P : (bb + 1) * P], in_=us[t][:, 8 * k + bb, :], identity=ident[:])
-                    pts[t].append(pt)
+                            nc.scalar.copy(out=adj_t[:, u, :], in_=pa[:, 0 : HOPS * P])
+                    adj_ts[a] = adj_t
 
-            def mask_blocks(t):
-                ng = loop.tile([P, HOPS * 1024], BF16, align_bytes=64, name="ng")
-                keep_b = keep_g[:, t, :, :].rearrange("p r j -> p (r j)").unsqueeze(1).to_broadcast([P, 16, 64])
-                for k in range(HOPS):
-                    nc.vector.tensor_tensor(
-                        out=ng[:, k * 1024 : (k + 1) * 1024].rearrange("p (r c) -> p r c", c=64),
-                        in0=pts[t][k][:].rearrange("p (r c) -> p r c", c=64), in1=keep_b, op=ALU.mult,
-                    )
-                ngs[t] = ng
+                def row_sums(a):
+                    adj_b = adj_ts[a][:].rearrange("p u c -> p (u c)").bitcast(BF16).rearrange("p (u i c e) -> p u i e c", u=2, i=HOPS, e=2)
+                    psum_s = ps_x.tile([P, 512], F32, tag="x")
+                    for i in range(HOPS):
+                        for j in range(4):
+                            nc.tensor.matmul(
+                                out=psum_s[:, i * T : (i + 1) * T], lhsT=adj_b[:, j // 2, i, j % 2, :], rhs=keep_t[:, j, :],
+                                start=(j == 0), stop=(j == 3),
+                            )
+                    sums[a] = psum_s
 
-            def quantise_norm(t):
-                nq = loop.tile([P, HOPS * M], U32, align_bytes=64, name="nq")
-                ns = loop.tile([P, HOPS * M], U8, align_bytes=64, name="ns")
-                for lo, hi in ((0, 2), (2, 3)):
-                    nc.vector.quantize_mx(
-                        out=nq[:, lo * M : hi * M].bitcast(FP8X4), scales=ns[:, lo * M : hi * M],
-                        in_=ngs[t][:, lo * 1024 : hi * 1024],
-                    )
-                nqs[t] = nq
-                nss[t] = ns
+                def invert_sums(a):
+                    s1 = big.tile([P, HOPS * T], F32, name="s1")
+                    nc.vector.tensor_scalar_add(out=s1[:], in0=sums[a][:, 0 : HOPS * T], scalar1=1.0)
+                    nc.vector.reciprocal(out=rcp[:, a].rearrange("p i t -> p (i t)"), in_=s1[:])
 
-            def regroup_context(q):
-                fcg = loop.tile([P, 4, D, 4], BF16, align_bytes=64, name="fcg", bufs=1)
-                if q < 2:
-                    nc.vector.tensor_copy(out=fcg[:].rearrange("p t d j -> p d j t"), in_=fc_view[:, q])
-                else:
-                    nc.scalar.copy(out=fcg[:].rearrange("p t d j -> p d j t"), in_=fc_view[:, q])
-                fcgs[q] = fcg
+                fc_view = fc_raw[:].rearrange("p j (d e q t) -> p q e d j t", e=2, q=4, t=4)
+                us, pts, ngs, nqs, nss, cgs, fcgs, p0s, p1s = {}, {}, {}, {}, {}, {}, {}, {}, {}
 
-            def quantise_context(q):
-                nc.vector.quantize_mx(
-                    out=fcq[:, 4 * q : 4 * q + 4, :].rearrange("p t d -> p (t d)").bitcast(FP8X4),
-                    scales=fcs[:, 4 * q : 4 * q + 4, :].rearrange("p t d -> p (t d)"),
-                    in_=fcgs[q][:].rearrange("p t d j -> p (t d j)"),
-                )
+                def scale_blocks(s, vec):
+                    a, tp = s // TP, s % TP
+                    u = loop.tile([P, 2, HOPS, N], BF16, name="u")
+                    us[s] = u
+                    for n in range(2 * HOPS):
+                        tt, i = n % 2, n // 2
+                        sc = rcp[:, a, i, 2 * tp + tt : 2 * tp + tt + 1]
+                        if n < vec:
+                            nc.vector.tensor_scalar(out=u[:, tt, i, :], in0=adj_r[:, a, i, :], scalar1=sc, scalar2=None, op0=ALU.mult)
+                        else:
+                            nc.scalar.activation(out=u[:, tt, i, :], in_=adj_r[:, a, i, :], func=ACT.Copy, scale=sc)
 
-            def turn_target(t):
-                pf = ps_x.tile([P, 512], F32, tag="x")
-                for a in range(4):
-                    nc.tensor.transpose(out=pf[:, a * P : (a + 1) * P], in_=ft_words[:, a, t // 2, :], identity=ident_f[:])
-                pf_v = pf[:].bitcast(BF16).rearrange("p (m c e) -> p e m c", c=2, e=2)
-                for e in range(2):
-                    cg = loop.tile([P, 2, M, 4], BF16, align_bytes=64, name="cg", bufs=4)
-                    nc.scalar.copy(out=cg[:, 0, :, 0:2], in_=pf_v[:, e])
-                    cg0s[t + e] = cg
+                def turn_blocks(s):
+                    u_w = us[s][:].rearrange("p t i n -> p (t i n)").bitcast(F32).rearrange("p (t i u q) -> p t i u q", t=2, i=HOPS, u=2)
+                    pts[s] = []
+                    for pair in (((0, 0), (1, 0)), ((0, 1), (0, 2)), ((1, 1), (1, 2))):
+                        pt = ps_t.tile([P, 2, 2, P], F32, tag="t")
+                        for u in range(2):
+                            for n, (tt, i) in enumerate(pair):
+                                nc.tensor.transpose(out=pt[:, u, n, :], in_=u_w[:, tt, i, u, :], identity=ident[:])
+                        pts[s].append(pt)
 
-            def hop_pass(dst, t, i, a, e):
-                nc.tensor.matmul_mx(
-                    out=dst,
-                    lhsT=fcq[:, t, e * P : (e + 1) * P].bitcast(FP8X4), lhsT_scale=fcs[:, t, e * P : (e + 1) * P],
-                    rhs=nqs[t][:, i * M + a * P : i * M + (a + 1) * P].bitcast(FP8X4),
-                    rhs_scale=nss[t][:, i * M + a * P : i * M + (a + 1) * P],
-                    start=True, stop=True,
-                )
+                def mask_blocks(s):
+                    tp = s % TP
+                    ng = loop.tile([P, 2 * HOPS * P, 4], BF16, align_bytes=64, name="ng")
+                    ngs[s] = ng
 
-            def neighbour_sums(t):
-                p0 = ps_s.tile([P, 4, P], F32, tag="s")
-                for a in range(2):
-                    for e in range(2):
-                        hop_pass(p0[:, a * 2 + e, :], t, 0, a, e)
-                p0s[t] = p0
-                p1s[t] = []
-                for a in range(2):
-                    pp = ps_s.tile([P, 4, P], F32, tag="s")
-                    for i in (1, 2):
-                        for e in range(2):
-                            hop_pass(pp[:, (i - 1) * 2 + e, :], t, i, a, e)
-                    p1s[t].append(pp)
-
-            def add_target(t):
-                cg0 = cg0s[t][:, 0]
-                cg1 = cg0s[t][:, 1]
-                nc.vector.tensor_tensor(
-                    out=cg0[:, :, 2:4].rearrange("p (a m) e -> p a m e", a=2),
-                    in0=p0s[t][:].rearrange("p (a e) m -> p a m e", a=2),
-                    in1=cg0[:, :, 0:2].rearrange("p (a m) e -> p a m e", a=2), op=ALU.add,
-                )
-                for a in range(2):
-                    nc.vector.tensor_tensor(
-                        out=cg1[:, a * P : (a + 1) * P, :].rearrange("p m (h e) -> p m h e", h=2),
-                        in0=p1s[t][a][:].rearrange("p (h e) m -> p m h e", h=2),
-                        in1=cg0[:, a * P : (a + 1) * P, 0:2].unsqueeze(2).to_broadcast([P, P, 2, 2]), op=ALU.add,
-                    )
-
-            def quantise_cat(t):
-                nc.vector.quantize_mx(
-                    out=catq[:, t, :, :].rearrange("p g m -> p (g m)").bitcast(FP8X4),
-                    scales=cats[:, t, :, :].rearrange("p g m -> p (g m)"),
-                    in_=cg0s[t][:].rearrange("p g m j -> p (g m j)"),
-                )
-
-            def turn_weights(k):
-                pw = ps_x.tile([P, 1024], BF16, tag="x")
-                for bb in range(8):
-                    nc.tensor.transpose(out=pw[:, bb * P : (bb + 1) * P], in_=w_r[:, 8 * k + bb, :], identity=ident[:])
-                pw_v = pw[:].rearrange("p (o g j) -> p g o j", g=2, j=4)
-                for g in range(2):
-                    nc.scalar.copy(out=wtg[:, g, k * P : (k + 1) * P, :], in_=pw_v[:, g])
-
-            scale_blocks(0)
-            turn_blocks(0)
-            scale_blocks(1)
-            turn_target(0)
-            regroup_context(0)
-            mask_blocks(0)
-            quantise_context(0)
-            quantise_norm(0)
-            for t in range(T):
-                if t + 2 < T:
-                    scale_blocks(t + 2)
-                if t + 1 < T:
-                    turn_blocks(t + 1)
-                if t % 2 == 0 and t + 2 < T:
-                    turn_target(t + 2)
-                neighbour_sums(t)
-                if W_FIRST <= t < W_FIRST + 8:
-                    turn_weights(t - W_FIRST)
-                if t % 4 == 0 and t + 4 < T:
-                    regroup_context(t // 4 + 1)
-                if t + 1 < T:
-                    mask_blocks(t + 1)
-                add_target(t)
-                if t + 1 < T:
-                    quantise_norm(t + 1)
-                quantise_cat(t)
-                if t % 4 == 1 and t + 3 < T:
-                    quantise_context(t // 4 + 1)
-                if t == W_FIRST + 8:
-                    for g in range(2):
-                        nc.vector.quantize_mx(
-                            out=wq[:, g, :].bitcast(FP8X4), scales=ws[:, g, :],
-                            in_=wtg[:, g, :, :].rearrange("p o j -> p (o j)"),
+                    def masked(dst, pt, n0, n1, t):
+                        width = (n1 - n0) * P
+                        nc.vector.tensor_tensor(
+                            out=ng[:, dst : dst + width, :].rearrange("p c (u e) -> p c u e", u=2),
+                            in0=pt[:].rearrange("p u n m -> p (u n m)").bitcast(BF16).rearrange("p (u c e) -> p c u e", u=2, e=2)[:, n0 * P : n1 * P],
+                            in1=keep_g[:, t, :].rearrange("p (u e) -> p u e", u=2).unsqueeze(1).to_broadcast([P, width, 2, 2]),
+                            op=ALU.mult,
                         )
+
+                    p0, p1, p2 = pts[s]
+                    masked(4 * P, p0, 0, 1, 2 * tp)
+                    masked(5 * P, p0, 1, 2, 2 * tp + 1)
+                    masked(0, p1, 0, 2, 2 * tp)
+                    masked(2 * P, p2, 0, 2, 2 * tp + 1)
+
+                def quantise_norm(s):
+                    nq = loop.tile([P, 2 * HOPS * P], U32, align_bytes=64, name="nq")
+                    ns = loop.tile([P, 2 * HOPS * P], U8, align_bytes=64, name="ns")
+                    for lo, hi in ((4 * P, 6 * P), (0, 4 * P)):
+                        nc.vector.quantize_mx(
+                            out=nq[:, lo:hi].bitcast(FP8X4), scales=ns[:, lo:hi], in_=ngs[s][:, lo:hi, :].rearrange("p c j -> p (c j)")
+                        )
+                    nqs[s] = nq
+                    nss[s] = ns
+
+                def regroup_context(q, e, h, vec):
+                    if q not in fcgs:
+                        fcg = big.tile([P, 4, 2, P, 4], BF16, align_bytes=64, name="fcg")
+                        fcgs[q] = fcg
+                    lo, hi = h
+                    dst = fcgs[q][:, :, e, lo:hi, :].rearrange("p t d j -> p d j t")
+                    if vec:
+                        nc.vector.tensor_copy(out=dst, in_=fc_view[:, q, e, lo:hi])
+                    else:
+                        nc.scalar.copy(out=dst, in_=fc_view[:, q, e, lo:hi])
+
+                def quantise_context(q):
+                    nc.vector.quantize_mx(
+                        out=fcq[:, 4 * q : 4 * q + 4, :].rearrange("p t d -> p (t d)").bitcast(FP8X4),
+                        scales=fcs[:, 4 * q : 4 * q + 4, :].rearrange("p t d -> p (t d)"),
+                        in_=fcgs[q][:].rearrange("p t e d j -> p (t e d j)"),
+                    )
+
+                def turn_target(s):
+                    a, tp = s // TP, s % TP
+                    pf = ps_x.tile([P, 512], F32, tag="x")
+                    for e in range(2):
+                        nc.tensor.transpose(out=pf[:, e * P : (e + 1) * P], in_=ft_w[:, a, e, tp, :], identity=ident[:])
+                    cg = loop.tile([P, 2, 2, P, 4], BF16, align_bytes=64, name="cg", bufs=3)
+                    nc.scalar.copy(
+                        out=cg[:, 0, :, :, 0:2], in_=pf[:].bitcast(BF16)[:, 0 : 4 * P].rearrange("p (e m t) -> p t m e", e=2, t=2)
+                    )
+                    cgs[s] = cg
+
+                def hop_pass(dst, s, t, e, lo, hi):
+                    nc.tensor.matmul_mx(
+                        out=dst,
+                        lhsT=fcq[:, t, e * P : (e + 1) * P].bitcast(FP8X4), lhsT_scale=fcs[:, t, e * P : (e + 1) * P],
+                        rhs=nqs[s][:, lo:hi].bitcast(FP8X4), rhs_scale=nss[s][:, lo:hi],
+                        start=True, stop=True,
+                    )
+
+                def neighbour_sums(s):
+                    tp = s % TP
+                    p0 = ps_s.tile([P, 2, 2, P], F32, tag="s")
+                    for tt in range(2):
+                        for e in range(2):
+                            hop_pass(p0[:, tt, e, :], s, 2 * tp + tt, e, (4 + tt) * P, (5 + tt) * P)
+                    p0s[s] = p0
+                    p1s[s] = []
+                    for tt in range(2):
+                        pp = ps_s.tile([P, 2, 2, P], F32, tag="s")
+                        for e in range(2):
+                            hop_pass(pp[:, e].rearrange("p h m -> p (h m)"), s, 2 * tp + tt, e, 2 * tt * P, 2 * (tt + 1) * P)
+                        p1s[s].append(pp)
+
+                def add_target(s):
+                    cg = cgs[s]
+                    nc.vector.tensor_tensor(
+                        out=cg[:, 0, :, :, 2:4], in0=p0s[s][:].rearrange("p t e m -> p t m e"), in1=cg[:, 0, :, :, 0:2], op=ALU.add
+                    )
+                    for tt in range(2):
+                        nc.vector.tensor_tensor(
+                            out=cg[:, 1, tt].rearrange("p m (h e) -> p m h e", h=2),
+                            in0=p1s[s][tt][:].rearrange("p e h m -> p m h e"),
+                            in1=cg[:, 0, tt, :, 0:2].unsqueeze(2).to_broadcast([P, P, 2, 2]), op=ALU.add,
+                        )
+
+                def quantise_cat(s):
+                    a, tp = s // TP, s % TP
+                    nc.vector.quantize_mx(
+                        out=catq[:, a, tp, :].bitcast(FP8X4), scales=cats[:, a, tp, :], in_=cgs[s][:].rearrange("p g t m j -> p (g t m j)")
+                    )
+
+                def turn_weights(k):
+                    pw = ps_x.tile([P, 512], F32, tag="x")
+                    for h in range(4):
+                        nc.tensor.transpose(out=pw[:, h * P : (h + 1) * P], in_=w_w[:, k, h, :], identity=ident[:])
+                    wtg_w = wtg[:].rearrange("p g o j -> p (g o j)").bitcast(F32).rearrange("p (g o h) -> p g o h", g=2, h=2)
+                    nc.scalar.copy(out=wtg_w[:, :, k * P : (k + 1) * P, :], in_=pw[:].rearrange("p (g h o) -> p g o h", g=2, h=2))
+
+                def quantise_weights(g):
+                    nc.vector.quantize_mx(
+                        out=wqk[:, g, :].bitcast(FP8X4), scales=wsk[:, g, :], in_=wtg[:, g].rearrange("p o j -> p (o j)")
+                    )
+
+                wns = {}
+
+                def turn_natural(late, wr2, b):
+                    w2_w = wr2[:].rearrange("p k c -> p (k c)").bitcast(F32).rearrange("p (k h q) -> p k h q", k=KO, q=P)
+                    wt2 = late.tile([P, 2, 2, P, 4], BF16, align_bytes=64, name="wt2")
+                    wt2_w = wt2[:].rearrange("p k g o j -> p (k g o j)").bitcast(F32).rearrange("p (k g o h) -> p k g o h", k=2, g=2, h=2)
+                    for k in range(2):
+                        pw = ps_x.tile([P, 512], F32, tag="x")
+                        for h in range(4):
+                            nc.tensor.transpose(out=pw[:, h * P : (h + 1) * P], in_=w2_w[:, 2 * b + k, h, :], identity=ident[:])
+                        nc.scalar.copy(out=wt2_w[:, k], in_=pw[:].rearrange("p (g h o) -> p g o h", g=2, h=2))
+                    wns[b] = wt2
+
+                def quantise_natural(b):
+                    nc.vector.quantize_mx(
+                        out=wqn[:, 2 * b : 2 * b + 2].rearrange("p k g o -> p (k g o)").bitcast(FP8X4),
+                        scales=wsn[:, 2 * b : 2 * b + 2].rearrange("p k g o -> p (k g o)"),
+                        in_=wns[b][:].rearrange("p k g o j -> p (k g o j)"),
+                    )
+
+                def mix_first(k, tq, ot):
+                    pb = ps_x.tile([P, 4, P], F32, tag="x")
+                    for h in range(2):
+                        for g in range(2):
+                            nc.tensor.matmul_mx(
+                                out=pb[:, 2 * h : 2 * h + 2, :].rearrange("p t m -> p (t m)"),
+                                lhsT=wqk[:, g, k * P : (k + 1) * P].bitcast(FP8X4), lhsT_scale=wsk[:, g, k * P : (k + 1) * P],
+                                rhs=catq[:, 0, 2 * tq + h, g * 256 : (g + 1) * 256].bitcast(FP8X4),
+                                rhs_scale=cats[:, 0, 2 * tq + h, g * 256 : (g + 1) * 256],
+                                start=(g == 0), stop=(g == 1),
+                            )
+                    nc.scalar.activation(
+                        out=ot[:, :, k, 4 * tq : 4 * tq + 4], in_=pb[:].rearrange("p t m -> p m t"), func=ACT.Relu, bias=bias_col[:, k : k + 1]
+                    )
+
+                whole, low, high = (0, P), (0, P // 2), (P // 2, P)
+                turn_adj(0)
+                row_sums(0)
+                invert_sums(0)
+                scale_blocks(0, 4)
+                turn_blocks(0)
+                scale_blocks(1, 2)
+                mask_blocks(0)
+                turn_blocks(1)
+                scale_blocks(2, 2)
+                quantise_norm(0)
+                mask_blocks(1)
+                turn_blocks(2)
+                quantise_norm(1)
+                regroup_context(0, 0, low, False)
+                regroup_context(0, 1, low, True)
+                turn_target(0)
+                regroup_context(0, 0, high, True)
+                regroup_context(0, 1, high, True)
+                scale_blocks(3, 2)
+                quantise_context(0)
+                neighbour_sums(0)
+
+                mixes = [(k, tq) for k in range(KO) for tq in range(4)]
+
+                def step(s, late, ot, wr2):
+                    if s + 1 < STEPS:
+                        turn_target(s + 1)
+                    if s == 1:
+                        turn_adj(1)
+                    if s == 2:
+                        row_sums(1)
+                    if s >= TP:
+                        for k, tq in mixes[8 * (s - TP) : 8 * (s - TP) + 4]:
+                            mix_first(k, tq, ot)
+                    if s + 2 < STEPS:
+                        mask_blocks(s + 2)
+                    if s + 3 < STEPS:
+                        turn_blocks(s + 3)
+                    if 2 <= s < 6:
+                        turn_weights(2 * (s - 2))
+                        turn_weights(2 * (s - 2) + 1)
+                    if s < 6:
+                        regroup_context(s // 2 + 1, s % 2, whole, False)
+                    if s + 4 < STEPS:
+                        scale_blocks(s + 4, SHARE[s])
+                    if s >= TP:
+                        for k, tq in mixes[8 * (s - TP) + 4 : 8 * (s - TP) + 8]:
+                            mix_first(k, tq, ot)
+                    if s >= TP + 3 and s < TP + 7:
+                        turn_natural(late, wr2, s - TP - 3)
+                    add_target(s)
+                    if s == 3:
+                        invert_sums(1)
+                    if s + 2 < STEPS:
+                        quantise_norm(s + 2)
+                    quantise_cat(s)
+                    if s < 6 and s % 2 == 1:
+                        quantise_context(s // 2 + 1)
+                    if 6 <= s < 8:
+                        quantise_weights(s - 6)
+                    if s >= TP + 4 and s < TP + 8:
+                        quantise_natural(s - TP - 4)
+                    if s + 1 < STEPS:
+                        neighbour_sums(s + 1)
+                    if s == TP + 3:
+                        for b in range(4):
+                            nc.sync.dma_start(
+                                out=out_o[:, 0, 32 * b : 32 * b + 32, :], in_=ot[:, 32 * b : 32 * b + 32].rearrange("p m k t -> p m (k t)")
+                            )
+
+                for s in range(TP):
+                    step(s, None, None, None)
+            with tc.tile_pool(name="late", bufs=1) as late:
+                ot0 = late.tile([P, P, KO, T], F32)
+                wr2 = late.tile([P, KO, C], BF16, align_bytes=64)
+                nc.sync.dma_start(out=wr2[:], in_=wn_v)
+                for s in range(TP, STEPS):
+                    step(s, late, ot0, wr2)
 
         with ExitStack() as ph2:
             opool = ph2.enter_context(tc.tile_pool(name="opool", bufs=4, reuse_waits="tile"))
             ps_o = ph2.enter_context(tc.psum_pool(name="ps_o", bufs=8, reuse_waits="tile"))
-            for a in range(2):
-                for ob in range(8):
-                    ot = opool.tile([P, P, T], F32)
-                    for tq in range(4):
-                        pb = ps_o.tile([P, 4, P], F32)
-                        for tt in range(4):
-                            t = 4 * tq + tt
-                            for g in range(2):
-                                nc.tensor.matmul_mx(
-                                    out=pb[:, tt, :],
-                                    lhsT=catq[:, t, g, a * P : (a + 1) * P].bitcast(FP8X4),
-                                    lhsT_scale=cats[:, t, g, a * P : (a + 1) * P],
-                                    rhs=wq[:, g, ob * P : (ob + 1) * P].bitcast(FP8X4),
-                                    rhs_scale=ws[:, g, ob * P : (ob + 1) * P],
-                                    start=(g == 0), stop=(g == 1),
-                                )
-                        nc.vector.tensor_tensor(
-                            out=ot[:, :, 4 * tq : 4 * tq + 4], in0=pb[:].rearrange("p t o -> p o t"),
-                            in1=bias_bc[:, ob * P : (ob + 1) * P].unsqueeze(2).to_broadcast([P, P, 4]), op=ALU.add,
-                        )
-                    flat = ot[:].rearrange("p o t -> p (o t)")
-                    half = P * T // 2
-                    for h in range(2):
-                        nc.scalar.activation(out=flat[:, h * half : (h + 1) * half], in_=flat[:, h * half : (h + 1) * half], func=ACT.Relu)
-                        nc.sync.dma_start(
-                            out=out_v[:, a, (2 * ob + h) * half : (2 * ob + h + 1) * half], in_=flat[:, h * half : (h + 1) * half]
-                        )
+            for ob in range(8):
+                ot = opool.tile([P, P, T], F32)
+                for tq in range(4):
+                    pb = ps_o.tile([P, 4, P], F32)
+                    for tt in range(4):
+                        tp, at = 2 * tq + tt // 2, (tt % 2) * P
+                        for g in range(2):
+                            nc.tensor.matmul_mx(
+                                out=pb[:, tt, :],
+                                lhsT=catq[:, 1, tp, g * 256 + at : g * 256 + at + P].bitcast(FP8X4),
+                                lhsT_scale=cats[:, 1, tp, g * 256 + at : g * 256 + at + P],
+                                rhs=wqn[:, ob, g, :].bitcast(FP8X4),
+                                rhs_scale=wsn[:, ob, g, :],
+                                start=(g == 0), stop=(g == 1),
+                            )
+                    nc.vector.tensor_tensor(
+                        out=ot[:, :, 4 * tq : 4 * tq + 4], in0=pb[:].rearrange("p t o -> p o t"),
+                        in1=bias_bc[:, ob * P : (ob + 1) * P].unsqueeze(2).to_broadcast([P, P, 4]), op=ALU.add,
+                    )
+                flat = ot[:].rearrange("p o t -> p (o t)")
+                half = P * T // 2
+                for h in range(2):
+                    nc.scalar.activation(out=flat[:, h * half : (h + 1) * half], in_=flat[:, h * half : (h + 1) * half], func=ACT.Relu)
+                    nc.sync.dma_start(
+                        out=out_m[:, 1, (2 * ob + h) * half : (2 * ob + h + 1) * half], in_=flat[:, h * half : (h + 1) * half]
+                    )

@@ -19,7 +19,9 @@ FLOPS = 2 * T * HOPS * M * N * D + 2 * M * T * CO * C
 TP = T // 2
 STEPS = 2 * TP
 KO = CO // P
-SHARE = [3, 3, 3, 3, 3, 3, 2, 2, 6, 6, 6, 6]
+VEC_SHARE = 4
+LATE = 6
+MIX_STEPS = 6
 
 
 def tile_graphaggregation_pa_t_kernel(tc, feat_context, feat_target, adj, missing_mask_context, W_mlp, b_mlp, out):
@@ -55,17 +57,17 @@ def tile_graphaggregation_pa_t_kernel(tc, feat_context, feat_target, adj, missin
 
         with ExitStack() as ph1:
             loop = ph1.enter_context(tc.tile_pool(name="loop", bufs=2))
-            ps_t = ph1.enter_context(tc.psum_pool(name="ps_t", bufs=3))
+            ps_t = ph1.enter_context(tc.psum_pool(name="ps_t", bufs=2))
             ps_s = ph1.enter_context(tc.psum_pool(name="ps_s", bufs=3))
-            ps_x = ph1.enter_context(tc.psum_pool(name="ps_x", bufs=2))
+            ps_x = ph1.enter_context(tc.psum_pool(name="ps_x", bufs=3))
             ft_r = loop.tile([P, 2, D * T], BF16, bufs=1)
             with tc.tile_pool(name="big", bufs=1) as big:
 
                 mask_pad = big.tile([P, N], BF16)
                 nc.vector.memset(mask_pad[:], 0.0)
                 make_identity(nc, ident[:])
-                nc.sync.dma_start(out=mask_pad[0:T, :], in_=mask_v)
                 nc.sync.dma_start(out=adj_r[:, 0], in_=adj_v[:, 0])
+                nc.sync.dma_start(out=mask_pad[0:T, :], in_=mask_v)
                 fc_raw = big.tile([P, 4, D * T], BF16)
                 for h in range(2):
                     for u in range(2):
@@ -130,47 +132,47 @@ def tile_graphaggregation_pa_t_kernel(tc, feat_context, feat_target, adj, missin
                 fc_view = fc_raw[:].rearrange("p j (d e q t) -> p q e d j t", e=2, q=4, t=4)
                 us, pts, ngs, nqs, nss, cgs, fcgs, p0s, p1s = {}, {}, {}, {}, {}, {}, {}, {}, {}
 
-                def scale_blocks(s, vec):
+                def scale_block(s, n, vec):
                     a, tp = s // TP, s % TP
-                    u = loop.tile([P, 2, HOPS, N], BF16, name="u")
-                    us[s] = u
+                    if n == 0:
+                        u = loop.tile([P, 2, HOPS, N], BF16, name="u")
+                        us[s] = u
+                    tt, i = n % 2, n // 2
+                    dst, src, sc = us[s][:, tt, i, :], adj_r[:, a, i, :], rcp[:, a, i, 2 * tp + tt : 2 * tp + tt + 1]
+                    if n < vec:
+                        nc.vector.tensor_scalar(out=dst, in0=src, scalar1=sc, scalar2=None, op0=ALU.mult)
+                    else:
+                        nc.scalar.activation(out=dst, in_=src, func=ACT.Copy, scale=sc)
+
+                def scale_blocks(s, vec):
                     for n in range(2 * HOPS):
-                        tt, i = n % 2, n // 2
-                        sc = rcp[:, a, i, 2 * tp + tt : 2 * tp + tt + 1]
-                        if n < vec:
-                            nc.vector.tensor_scalar(out=u[:, tt, i, :], in0=adj_r[:, a, i, :], scalar1=sc, scalar2=None, op0=ALU.mult)
-                        else:
-                            nc.scalar.activation(out=u[:, tt, i, :], in_=adj_r[:, a, i, :], func=ACT.Copy, scale=sc)
+                        scale_block(s, n, vec)
 
-                def turn_blocks(s):
+                PAIRS = (((0, 0), (1, 0)), ((0, 1), (0, 2)), ((1, 1), (1, 2)))
+
+                def turn_blocks(s, b):
                     u_w = us[s][:].rearrange("p t i n -> p (t i n)").bitcast(F32).rearrange("p (t i u q) -> p t i u q", t=2, i=HOPS, u=2)
-                    pts[s] = []
-                    for pair in (((0, 0), (1, 0)), ((0, 1), (0, 2)), ((1, 1), (1, 2))):
-                        pt = ps_t.tile([P, 2, 2, P], F32, tag="t")
-                        for u in range(2):
-                            for n, (tt, i) in enumerate(pair):
-                                nc.tensor.transpose(out=pt[:, u, n, :], in_=u_w[:, tt, i, u, :], identity=ident[:])
-                        pts[s].append(pt)
+                    pt = ps_t.tile([P, 2, 2, P], F32, tag="t")
+                    for u in range(2):
+                        for n, (tt, i) in enumerate(PAIRS[b]):
+                            nc.tensor.transpose(out=pt[:, u, n, :], in_=u_w[:, tt, i, u, :], identity=ident[:])
+                    pts[s, b] = pt
 
-                def mask_blocks(s):
+                def mask_blocks(s, b):
                     tp = s % TP
-                    ng = loop.tile([P, 2 * HOPS * P, 4], BF16, align_bytes=64, name="ng")
-                    ngs[s] = ng
-
-                    def masked(dst, pt, n0, n1, t):
+                    if b == 0:
+                        ng = loop.tile([P, 2 * HOPS * P, 4], BF16, align_bytes=64, name="ng")
+                        ngs[s] = ng
+                    parts = ((4, 0, 1, 0), (5, 1, 2, 1)) if b == 0 else ((2 * (b - 1), 0, 2, b - 1),)
+                    pt_v = pts[s, b][:].rearrange("p u n m -> p (u n m)").bitcast(BF16).rearrange("p (u c e) -> p c u e", u=2, e=2)
+                    for at, n0, n1, tt in parts:
                         width = (n1 - n0) * P
                         nc.vector.tensor_tensor(
-                            out=ng[:, dst : dst + width, :].rearrange("p c (u e) -> p c u e", u=2),
-                            in0=pt[:].rearrange("p u n m -> p (u n m)").bitcast(BF16).rearrange("p (u c e) -> p c u e", u=2, e=2)[:, n0 * P : n1 * P],
-                            in1=keep_g[:, t, :].rearrange("p (u e) -> p u e", u=2).unsqueeze(1).to_broadcast([P, width, 2, 2]),
+                            out=ngs[s][:, at * P : at * P + width, :].rearrange("p c (u e) -> p c u e", u=2),
+                            in0=pt_v[:, n0 * P : n1 * P],
+                            in1=keep_g[:, 2 * tp + tt, :].rearrange("p (u e) -> p u e", u=2).unsqueeze(1).to_broadcast([P, width, 2, 2]),
                             op=ALU.mult,
                         )
-
-                    p0, p1, p2 = pts[s]
-                    masked(4 * P, p0, 0, 1, 2 * tp)
-                    masked(5 * P, p0, 1, 2, 2 * tp + 1)
-                    masked(0, p1, 0, 2, 2 * tp)
-                    masked(2 * P, p2, 0, 2, 2 * tp + 1)
 
                 def quantise_norm(s):
                     nq = loop.tile([P, 2 * HOPS * P], U32, align_bytes=64, name="nq")
@@ -303,80 +305,98 @@ def tile_graphaggregation_pa_t_kernel(tc, feat_context, feat_target, adj, missin
                 row_sums(0)
                 invert_sums(0)
                 scale_blocks(0, 4)
-                turn_blocks(0)
+                turn_blocks(0, 0)
+                turn_blocks(0, 1)
                 scale_blocks(1, 2)
-                mask_blocks(0)
-                turn_blocks(1)
+                mask_blocks(0, 0)
+                mask_blocks(0, 1)
+                turn_blocks(0, 2)
+                turn_blocks(1, 0)
                 scale_blocks(2, 2)
+                mask_blocks(0, 2)
+                mask_blocks(1, 0)
+                turn_blocks(1, 1)
+                turn_blocks(1, 2)
                 quantise_norm(0)
-                mask_blocks(1)
-                turn_blocks(2)
+                mask_blocks(1, 1)
+                mask_blocks(1, 2)
+                turn_blocks(2, 0)
+                turn_blocks(2, 1)
                 quantise_norm(1)
                 regroup_context(0, 0, low, False)
                 regroup_context(0, 1, low, True)
-                turn_target(0)
                 regroup_context(0, 0, high, True)
                 regroup_context(0, 1, high, True)
+                turn_target(0)
                 scale_blocks(3, 2)
                 quantise_context(0)
                 neighbour_sums(0)
 
-                mixes = [(k, tq) for k in range(KO) for tq in range(4)]
+                mixes = [(k, tq) for tq in range(4) for k in range(KO)]
 
                 def step(s, late, ot, wr2):
+                    lo, hi = (max(0, min(MIX_STEPS, x)) * len(mixes) // MIX_STEPS for x in (s - LATE, s - LATE + 1))
+                    todo = mixes[lo:hi]
+                    first = len(todo) // 2
+                    if s < 6:
+                        regroup_context(s // 2 + 1, s % 2, whole, False)
+                    if s + 2 < STEPS:
+                        mask_blocks(s + 2, 0)
+                        turn_blocks(s + 2, 2)
+                        mask_blocks(s + 2, 1)
+                    if s + 3 < STEPS:
+                        turn_blocks(s + 3, 0)
                     if s + 1 < STEPS:
                         turn_target(s + 1)
+                    if s > 0:
+                        quantise_cat(s - 1)
+                    if s + 4 < STEPS:
+                        scale_blocks(s + 4, VEC_SHARE)
                     if s == 1:
                         turn_adj(1)
                     if s == 2:
                         row_sums(1)
-                    if s >= TP:
-                        for k, tq in mixes[8 * (s - TP) : 8 * (s - TP) + 4]:
-                            mix_first(k, tq, ot)
-                    if s + 2 < STEPS:
-                        mask_blocks(s + 2)
-                    if s + 3 < STEPS:
-                        turn_blocks(s + 3)
-                    if 2 <= s < 6:
-                        turn_weights(2 * (s - 2))
-                        turn_weights(2 * (s - 2) + 1)
-                    if s < 6:
-                        regroup_context(s // 2 + 1, s % 2, whole, False)
-                    if s + 4 < STEPS:
-                        scale_blocks(s + 4, SHARE[s])
-                    if s >= TP:
-                        for k, tq in mixes[8 * (s - TP) + 4 : 8 * (s - TP) + 8]:
-                            mix_first(k, tq, ot)
-                    if s >= TP + 3 and s < TP + 7:
-                        turn_natural(late, wr2, s - TP - 3)
+                    for k, tq in todo[:first]:
+                        mix_first(k, tq, ot)
+                    if s < 6 and s % 2 == 1:
+                        quantise_context(s // 2 + 1)
                     add_target(s)
+                    if s + 1 < STEPS:
+                        neighbour_sums(s + 1)
+                    if s + 2 < STEPS:
+                        mask_blocks(s + 2, 2)
+                    if s + 3 < STEPS:
+                        turn_blocks(s + 3, 1)
+                    if s < 4:
+                        turn_weights(2 * s)
+                        turn_weights(2 * s + 1)
+                    for k, tq in todo[first:]:
+                        mix_first(k, tq, ot)
                     if s == 3:
                         invert_sums(1)
                     if s + 2 < STEPS:
                         quantise_norm(s + 2)
-                    quantise_cat(s)
-                    if s < 6 and s % 2 == 1:
-                        quantise_context(s // 2 + 1)
-                    if 6 <= s < 8:
-                        quantise_weights(s - 6)
                     if s >= TP + 4 and s < TP + 8:
                         quantise_natural(s - TP - 4)
-                    if s + 1 < STEPS:
-                        neighbour_sums(s + 1)
-                    if s == TP + 3:
+                    if s >= TP + 3 and s < TP + 7:
+                        turn_natural(late, wr2, s - TP - 3)
+                    if 4 <= s < 6:
+                        quantise_weights(s - 4)
+                    if s == LATE + MIX_STEPS - 1:
                         for b in range(4):
                             nc.sync.dma_start(
                                 out=out_o[:, 0, 32 * b : 32 * b + 32, :], in_=ot[:, 32 * b : 32 * b + 32].rearrange("p m k t -> p m (k t)")
                             )
 
-                for s in range(TP):
+                for s in range(LATE):
                     step(s, None, None, None)
             with tc.tile_pool(name="late", bufs=1) as late:
                 ot0 = late.tile([P, P, KO, T], F32)
                 wr2 = late.tile([P, KO, C], BF16, align_bytes=64)
                 nc.sync.dma_start(out=wr2[:], in_=wn_v)
-                for s in range(TP, STEPS):
+                for s in range(LATE, STEPS):
                     step(s, late, ot0, wr2)
+                quantise_cat(STEPS - 1)
 
         with ExitStack() as ph2:
             opool = ph2.enter_context(tc.tile_pool(name="opool", bufs=4, reuse_waits="tile"))

@@ -16,12 +16,13 @@ T, M, N, D, HOPS, CO = 16, 256, 512, 256, 3, 1024
 C = (HOPS + 1) * D
 FLOPS = 2 * T * HOPS * M * N * D + 2 * M * T * CO * C
 
+MH = 64
 TP = T // 2
 STEPS = 2 * TP
 KO = CO // P
 VEC_SHARE = 4
 LATE = 6
-MIX_STEPS = 6
+MIX_RATE = 6
 
 
 def tile_graphaggregation_pa_t_kernel(tc, feat_context, feat_target, adj, missing_mask_context, W_mlp, b_mlp, out):
@@ -41,6 +42,8 @@ def tile_graphaggregation_pa_t_kernel(tc, feat_context, feat_target, adj, missin
 
         adj_r = const.tile([P, 2, HOPS, N], BF16)
         ident = const.tile([P, P], F32)
+        ones_l = const.tile([P, P], BF16)
+        ones_r = const.tile([P, T], BF16)
         bias_bc = const.tile([P, CO], BF16)
         bias_col = const.tile([P, KO], BF16)
         keep_t = const.tile([P, 4, T], BF16)
@@ -66,6 +69,8 @@ def tile_graphaggregation_pa_t_kernel(tc, feat_context, feat_target, adj, missin
                 mask_pad = big.tile([P, N], BF16)
                 nc.vector.memset(mask_pad[:], 0.0)
                 make_identity(nc, ident[:])
+                nc.gpsimd.memset(ones_l[:], 1.0 / P)
+                nc.gpsimd.memset(ones_r[:], 1.0)
                 nc.sync.dma_start(out=adj_r[:, 0], in_=adj_v[:, 0])
                 nc.sync.dma_start(out=mask_pad[0:T, :], in_=mask_v)
                 fc_raw = big.tile([P, 4, D * T], BF16)
@@ -88,16 +93,17 @@ def tile_graphaggregation_pa_t_kernel(tc, feat_context, feat_target, adj, missin
                 ft_w = ft_r[:].rearrange("p a x -> p (a x)").bitcast(F32).rearrange("p (a d e w) -> p a e w d", a=2, e=2, w=TP)
                 w_w = w_r[:].rearrange("p k c -> p (k c)").bitcast(F32).rearrange("p (k h q) -> p k h q", k=KO, q=P)
 
-                pm = ps_x.tile([P, 512], F32, tag="x")
-                for u in range(2):
-                    nc.tensor.transpose(out=pm[:, u * P : (u + 1) * P], in_=mask_w[:, u * P : (u + 1) * P], identity=ident[:])
-                pm_v = pm[:].bitcast(BF16)[:, 0 : 4 * P].rearrange("p (u q e) -> p u e q", u=2, e=2)[:, :, :, 0:T]
-                nc.vector.tensor_scalar(
-                    out=keep_t[:].rearrange("p (u e) t -> p u e t", u=2), in0=pm_v, scalar1=-1.0, scalar2=1.0, op0=ALU.mult, op1=ALU.add
-                )
-                nc.vector.tensor_scalar(
-                    out=keep_g[:].rearrange("p t (u e) -> p u e t", u=2), in0=pm_v, scalar1=-1.0, scalar2=1.0, op0=ALU.mult, op1=ALU.add
-                )
+                def turn_mask():
+                    pm = ps_x.tile([P, 512], F32, tag="x")
+                    for u in range(2):
+                        nc.tensor.transpose(out=pm[:, u * P : (u + 1) * P], in_=mask_w[:, u * P : (u + 1) * P], identity=ident[:])
+                    pm_v = pm[:].bitcast(BF16)[:, 0 : 4 * P].rearrange("p (u q e) -> p u e q", u=2, e=2)[:, :, :, 0:T]
+                    nc.vector.tensor_scalar(
+                        out=keep_t[:].rearrange("p (u e) t -> p u e t", u=2), in0=pm_v, scalar1=-1.0, scalar2=1.0, op0=ALU.mult, op1=ALU.add
+                    )
+                    nc.vector.tensor_scalar(
+                        out=keep_g[:].rearrange("p t (u e) -> p u e t", u=2), in0=pm_v, scalar1=-1.0, scalar2=1.0, op0=ALU.mult, op1=ALU.add
+                    )
 
                 adj_ts, sums = {}, {}
 
@@ -107,7 +113,7 @@ def tile_graphaggregation_pa_t_kernel(tc, feat_context, feat_target, adj, missin
                         pa = ps_x.tile([P, 512], F32, tag="x")
                         for i in range(HOPS):
                             nc.tensor.transpose(out=pa[:, i * P : (i + 1) * P], in_=adj_w[:, a, i, u, :], identity=ident[:])
-                        if u == 0:
+                        if (a, u) == (0, 0):
                             nc.vector.tensor_copy(out=adj_t[:, u, :], in_=pa[:, 0 : HOPS * P])
                         else:
                             nc.scalar.copy(out=adj_t[:, u, :], in_=pa[:, 0 : HOPS * P])
@@ -117,20 +123,17 @@ def tile_graphaggregation_pa_t_kernel(tc, feat_context, feat_target, adj, missin
                     adj_b = adj_ts[a][:].rearrange("p u c -> p (u c)").bitcast(BF16).rearrange("p (u i c e) -> p u i e c", u=2, i=HOPS, e=2)
                     psum_s = ps_x.tile([P, 512], F32, tag="x")
                     for i in range(HOPS):
+                        dst = psum_s[:, i * T : (i + 1) * T]
+                        nc.tensor.matmul(out=dst, lhsT=ones_l[:], rhs=ones_r[:], start=True, stop=False)
                         for j in range(4):
-                            nc.tensor.matmul(
-                                out=psum_s[:, i * T : (i + 1) * T], lhsT=adj_b[:, j // 2, i, j % 2, :], rhs=keep_t[:, j, :],
-                                start=(j == 0), stop=(j == 3),
-                            )
+                            nc.tensor.matmul(out=dst, lhsT=adj_b[:, j // 2, i, j % 2, :], rhs=keep_t[:, j, :], start=False, stop=(j == 3))
                     sums[a] = psum_s
 
                 def invert_sums(a):
-                    s1 = big.tile([P, HOPS * T], F32, name="s1")
-                    nc.vector.tensor_scalar_add(out=s1[:], in0=sums[a][:, 0 : HOPS * T], scalar1=1.0)
-                    nc.vector.reciprocal(out=rcp[:, a].rearrange("p i t -> p (i t)"), in_=s1[:])
+                    nc.vector.reciprocal(out=rcp[:, a].rearrange("p i t -> p (i t)"), in_=sums[a][:, 0 : HOPS * T])
 
                 fc_view = fc_raw[:].rearrange("p j (d e q t) -> p q e d j t", e=2, q=4, t=4)
-                us, pts, ngs, nqs, nss, cgs, fcgs, p0s, p1s = {}, {}, {}, {}, {}, {}, {}, {}, {}
+                us, pts, ngs, nqs, nss, cgs, fcgs, p0s, p1s, flats, ots = {}, {}, {}, {}, {}, {}, {}, {}, {}, {}, {}
 
                 def scale_block(s, n, vec):
                     a, tp = s // TP, s % TP
@@ -207,11 +210,14 @@ def tile_graphaggregation_pa_t_kernel(tc, feat_context, feat_target, adj, missin
                     pf = ps_x.tile([P, 512], F32, tag="x")
                     for e in range(2):
                         nc.tensor.transpose(out=pf[:, e * P : (e + 1) * P], in_=ft_w[:, a, e, tp, :], identity=ident[:])
-                    cg = loop.tile([P, 2, 2, P, 4], BF16, align_bytes=64, name="cg", bufs=3)
-                    nc.scalar.copy(
-                        out=cg[:, 0, :, :, 0:2], in_=pf[:].bitcast(BF16)[:, 0 : 4 * P].rearrange("p (e m t) -> p t m e", e=2, t=2)
-                    )
-                    cgs[s] = cg
+                    cg = loop.tile([P, 2048], BF16, align_bytes=64, name="cg", bufs=3)
+                    w = P if a else MH
+                    cg_v = cg[:].rearrange("p (h g t m j) -> p h g t m j", g=2, t=2, m=w, j=4)
+                    pf_v = pf[:].bitcast(BF16)[:, 0 : 4 * P].rearrange("p (e h m t) -> p h t m e", e=2, m=w, t=2)
+                    for h in range(P // w):
+                        nc.scalar.copy(out=cg_v[:, h, 0, :, :, 0:2], in_=pf_v[:, h])
+                    cgs[s] = cg_v
+                    flats[s] = cg
 
                 def hop_pass(dst, s, t, e, lo, hi):
                     nc.tensor.matmul_mx(
@@ -237,20 +243,26 @@ def tile_graphaggregation_pa_t_kernel(tc, feat_context, feat_target, adj, missin
 
                 def add_target(s):
                     cg = cgs[s]
-                    nc.vector.tensor_tensor(
-                        out=cg[:, 0, :, :, 2:4], in0=p0s[s][:].rearrange("p t e m -> p t m e"), in1=cg[:, 0, :, :, 0:2], op=ALU.add
-                    )
-                    for tt in range(2):
+                    w = P if s >= TP else MH
+                    for h in range(P // w):
+                        at = slice(h * w, (h + 1) * w)
                         nc.vector.tensor_tensor(
-                            out=cg[:, 1, tt].rearrange("p m (h e) -> p m h e", h=2),
-                            in0=p1s[s][tt][:].rearrange("p e h m -> p m h e"),
-                            in1=cg[:, 0, tt, :, 0:2].unsqueeze(2).to_broadcast([P, P, 2, 2]), op=ALU.add,
+                            out=cg[:, h, 0, :, :, 2:4], in0=p0s[s][:].rearrange("p t e m -> p t m e")[:, :, at],
+                            in1=cg[:, h, 0, :, :, 0:2], op=ALU.add,
                         )
+                    for tt in range(2):
+                        for h in range(P // w):
+                            at = slice(h * w, (h + 1) * w)
+                            nc.vector.tensor_tensor(
+                                out=cg[:, h, 1, tt].rearrange("p m (i e) -> p m i e", i=2),
+                                in0=p1s[s][tt][:].rearrange("p e i m -> p m i e")[:, at],
+                                in1=cg[:, h, 0, tt, :, 0:2].unsqueeze(2).to_broadcast([P, w, 2, 2]), op=ALU.add,
+                            )
 
                 def quantise_cat(s):
                     a, tp = s // TP, s % TP
                     nc.vector.quantize_mx(
-                        out=catq[:, a, tp, :].bitcast(FP8X4), scales=cats[:, a, tp, :], in_=cgs[s][:].rearrange("p g t m j -> p (g t m j)")
+                        out=catq[:, a, tp, :].bitcast(FP8X4), scales=cats[:, a, tp, :], in_=flats[s][:]
                     )
 
                 def turn_weights(k):
@@ -285,23 +297,34 @@ def tile_graphaggregation_pa_t_kernel(tc, feat_context, feat_target, adj, missin
                         in_=wns[b][:].rearrange("p k g o j -> p (k g o j)"),
                     )
 
-                def mix_first(k, tq, ot):
+                def mix_first(late, h, t8, k):
+                    if h not in ots:
+                        ot = late.tile([P, MH, KO, T], F32, name="ot", bufs=2)
+                        ots[h] = ot
                     pb = ps_x.tile([P, 4, P], F32, tag="x")
-                    for h in range(2):
+                    for b in range(4):
                         for g in range(2):
+                            at = (2 * h + g) * P
                             nc.tensor.matmul_mx(
-                                out=pb[:, 2 * h : 2 * h + 2, :].rearrange("p t m -> p (t m)"),
+                                out=pb[:, b, :],
                                 lhsT=wqk[:, g, k * P : (k + 1) * P].bitcast(FP8X4), lhsT_scale=wsk[:, g, k * P : (k + 1) * P],
-                                rhs=catq[:, 0, 2 * tq + h, g * 256 : (g + 1) * 256].bitcast(FP8X4),
-                                rhs_scale=cats[:, 0, 2 * tq + h, g * 256 : (g + 1) * 256],
+                                rhs=catq[:, 0, 4 * t8 + b, at : at + P].bitcast(FP8X4), rhs_scale=cats[:, 0, 4 * t8 + b, at : at + P],
                                 start=(g == 0), stop=(g == 1),
                             )
                     nc.scalar.activation(
-                        out=ot[:, :, k, 4 * tq : 4 * tq + 4], in_=pb[:].rearrange("p t m -> p m t"), func=ACT.Relu, bias=bias_col[:, k : k + 1]
+                        out=ots[h][:, :, k, 8 * t8 : 8 * t8 + 8], in_=pb[:].rearrange("p b (t m) -> p m (b t)", t=2),
+                        func=ACT.Relu, bias=bias_col[:, k : k + 1],
                     )
+                    if (t8, k) == (1, KO - 1):
+                        for b in range(2):
+                            nc.sync.dma_start(
+                                out=out_o[:, 0, h * MH + 32 * b : h * MH + 32 * b + 32, :],
+                                in_=ots[h][:, 32 * b : 32 * b + 32].rearrange("p m k t -> p m (k t)"),
+                            )
 
                 whole, low, high = (0, P), (0, P // 2), (P // 2, P)
                 turn_adj(0)
+                turn_mask()
                 row_sums(0)
                 invert_sums(0)
                 scale_blocks(0, 4)
@@ -332,11 +355,10 @@ def tile_graphaggregation_pa_t_kernel(tc, feat_context, feat_target, adj, missin
                 quantise_context(0)
                 neighbour_sums(0)
 
-                mixes = [(k, tq) for tq in range(4) for k in range(KO)]
+                mixes = [(h, t8, k) for t8 in range(2) for h in range(2) for k in range(KO)]
 
-                def step(s, late, ot, wr2):
-                    lo, hi = (max(0, min(MIX_STEPS, x)) * len(mixes) // MIX_STEPS for x in (s - LATE, s - LATE + 1))
-                    todo = mixes[lo:hi]
+                def step(s, late, wr2):
+                    todo = mixes[max(0, s - LATE) * MIX_RATE : max(0, s + 1 - LATE) * MIX_RATE]
                     first = len(todo) // 2
                     if s < 6:
                         regroup_context(s // 2 + 1, s % 2, whole, False)
@@ -348,30 +370,30 @@ def tile_graphaggregation_pa_t_kernel(tc, feat_context, feat_target, adj, missin
                         turn_blocks(s + 3, 0)
                     if s + 1 < STEPS:
                         turn_target(s + 1)
-                    if s > 0:
-                        quantise_cat(s - 1)
-                    if s + 4 < STEPS:
-                        scale_blocks(s + 4, VEC_SHARE)
                     if s == 1:
                         turn_adj(1)
                     if s == 2:
                         row_sums(1)
-                    for k, tq in todo[:first]:
-                        mix_first(k, tq, ot)
-                    if s < 6 and s % 2 == 1:
-                        quantise_context(s // 2 + 1)
+                    for h, t8, k in todo[:first]:
+                        mix_first(late, h, t8, k)
                     add_target(s)
-                    if s + 1 < STEPS:
-                        neighbour_sums(s + 1)
                     if s + 2 < STEPS:
                         mask_blocks(s + 2, 2)
+                    if s > 0:
+                        quantise_cat(s - 1)
+                    if s + 4 < STEPS:
+                        scale_blocks(s + 4, VEC_SHARE)
+                    if s < 6 and s % 2 == 1:
+                        quantise_context(s // 2 + 1)
+                    if s + 1 < STEPS:
+                        neighbour_sums(s + 1)
                     if s + 3 < STEPS:
                         turn_blocks(s + 3, 1)
                     if s < 4:
                         turn_weights(2 * s)
                         turn_weights(2 * s + 1)
-                    for k, tq in todo[first:]:
-                        mix_first(k, tq, ot)
+                    for h, t8, k in todo[first:]:
+                        mix_first(late, h, t8, k)
                     if s == 3:
                         invert_sums(1)
                     if s + 2 < STEPS:
@@ -382,20 +404,14 @@ def tile_graphaggregation_pa_t_kernel(tc, feat_context, feat_target, adj, missin
                         turn_natural(late, wr2, s - TP - 3)
                     if 4 <= s < 6:
                         quantise_weights(s - 4)
-                    if s == LATE + MIX_STEPS - 1:
-                        for b in range(4):
-                            nc.sync.dma_start(
-                                out=out_o[:, 0, 32 * b : 32 * b + 32, :], in_=ot[:, 32 * b : 32 * b + 32].rearrange("p m k t -> p m (k t)")
-                            )
 
                 for s in range(LATE):
-                    step(s, None, None, None)
+                    step(s, None, None)
             with tc.tile_pool(name="late", bufs=1) as late:
-                ot0 = late.tile([P, P, KO, T], F32)
                 wr2 = late.tile([P, KO, C], BF16, align_bytes=64)
                 nc.sync.dma_start(out=wr2[:], in_=wn_v)
                 for s in range(LATE, STEPS):
-                    step(s, late, ot0, wr2)
+                    step(s, late, wr2)
                 quantise_cat(STEPS - 1)
 
         with ExitStack() as ph2:

@@ -20,8 +20,9 @@ MH = 64
 TP = T // 2
 STEPS = 2 * TP
 KO = CO // P
-VEC_SHARE = 4
+SHARE = 4
 LATE = 6
+MIX_FIRST = 2
 MIX_RATE = 6
 
 
@@ -135,21 +136,23 @@ def tile_graphaggregation_pa_t_kernel(tc, feat_context, feat_target, adj, missin
                 fc_view = fc_raw[:].rearrange("p j (d e q t) -> p q e d j t", e=2, q=4, t=4)
                 us, pts, ngs, nqs, nss, cgs, fcgs, p0s, p1s, flats, ots = {}, {}, {}, {}, {}, {}, {}, {}, {}, {}, {}
 
-                def scale_block(s, n, vec):
+                def scale_block(s, n, share, gp):
                     a, tp = s // TP, s % TP
                     if n == 0:
                         u = loop.tile([P, 2, HOPS, N], BF16, name="u")
                         us[s] = u
                     tt, i = n % 2, n // 2
                     dst, src, sc = us[s][:, tt, i, :], adj_r[:, a, i, :], rcp[:, a, i, 2 * tp + tt : 2 * tp + tt + 1]
-                    if n < vec:
+                    if n < share and gp:
+                        nc.gpsimd.tensor_scalar(out=dst, in0=src, scalar1=sc, scalar2=0.0, op0=ALU.mult, op1=ALU.add)
+                    elif n < share:
                         nc.vector.tensor_scalar(out=dst, in0=src, scalar1=sc, scalar2=None, op0=ALU.mult)
                     else:
                         nc.scalar.activation(out=dst, in_=src, func=ACT.Copy, scale=sc)
 
-                def scale_blocks(s, vec):
+                def scale_blocks(s, share, gp=False):
                     for n in range(2 * HOPS):
-                        scale_block(s, n, vec)
+                        scale_block(s, n, share, gp)
 
                 PAIRS = (((0, 0), (1, 0)), ((0, 1), (0, 2)), ((1, 1), (1, 2)))
 
@@ -166,16 +169,14 @@ def tile_graphaggregation_pa_t_kernel(tc, feat_context, feat_target, adj, missin
                     if b == 0:
                         ng = loop.tile([P, 2 * HOPS * P, 4], BF16, align_bytes=64, name="ng")
                         ngs[s] = ng
-                    parts = ((4, 0, 1, 0), (5, 1, 2, 1)) if b == 0 else ((2 * (b - 1), 0, 2, b - 1),)
-                    pt_v = pts[s, b][:].rearrange("p u n m -> p (u n m)").bitcast(BF16).rearrange("p (u c e) -> p c u e", u=2, e=2)
-                    for at, n0, n1, tt in parts:
-                        width = (n1 - n0) * P
-                        nc.vector.tensor_tensor(
-                            out=ngs[s][:, at * P : at * P + width, :].rearrange("p c (u e) -> p c u e", u=2),
-                            in0=pt_v[:, n0 * P : n1 * P],
-                            in1=keep_g[:, 2 * tp + tt, :].rearrange("p (u e) -> p u e", u=2).unsqueeze(1).to_broadcast([P, width, 2, 2]),
-                            op=ALU.mult,
-                        )
+                    at, lo, hi = ((4, 0, 2), (0, 0, 1), (2, 1, 2))[b]
+                    w = 2 * P // (hi - lo)
+                    keep = keep_g[:, 2 * tp + lo : 2 * tp + hi].rearrange("p t (u e) -> p t u e", u=2)
+                    nc.vector.tensor_tensor(
+                        out=ngs[s][:, at * P : (at + 2) * P, :].rearrange("p (t m) (u e) -> p t m u e", m=w, u=2),
+                        in0=pts[s, b][:].rearrange("p u n m -> p (u n m)").bitcast(BF16).rearrange("p (u t m e) -> p t m u e", u=2, m=w, e=2),
+                        in1=keep.unsqueeze(2).to_broadcast([P, hi - lo, w, 2, 2]), op=ALU.mult,
+                    )
 
                 def quantise_norm(s):
                     nq = loop.tile([P, 2 * HOPS * P], U32, align_bytes=64, name="nq")
@@ -359,7 +360,7 @@ def tile_graphaggregation_pa_t_kernel(tc, feat_context, feat_target, adj, missin
 
                 def step(s, late, wr2):
                     todo = mixes[max(0, s - LATE) * MIX_RATE : max(0, s + 1 - LATE) * MIX_RATE]
-                    first = len(todo) // 2
+                    first = min(MIX_FIRST, len(todo))
                     if s < 6:
                         regroup_context(s // 2 + 1, s % 2, whole, False)
                     if s + 2 < STEPS:
@@ -382,7 +383,7 @@ def tile_graphaggregation_pa_t_kernel(tc, feat_context, feat_target, adj, missin
                     if s > 0:
                         quantise_cat(s - 1)
                     if s + 4 < STEPS:
-                        scale_blocks(s + 4, VEC_SHARE)
+                        scale_blocks(s + 4, SHARE, True)
                     if s < 6 and s % 2 == 1:
                         quantise_context(s // 2 + 1)
                     if s + 1 < STEPS:

@@ -21,9 +21,9 @@ TP = T // 2
 STEPS = 2 * TP
 KO = CO // P
 SHARE = 4
-LATE = 6
+LATE = 5
 MIX_FIRST = 2
-MIX_RATE = 6
+MIX_RATE = 15
 
 
 def tile_graphaggregation_pa_t_kernel(tc, feat_context, feat_target, adj, missing_mask_context, W_mlp, b_mlp, out):
@@ -52,8 +52,8 @@ def tile_graphaggregation_pa_t_kernel(tc, feat_context, feat_target, adj, missin
         rcp = const.tile([P, 2, HOPS, T], F32)
         fcq = const.tile([P, T, D], U32, align_bytes=64)
         fcs = const.tile([P, T, D], U8, align_bytes=64)
-        catq = const.tile([P, 2, TP, 512], U32, align_bytes=64)
-        cats = const.tile([P, 2, TP, 512], U8, align_bytes=64)
+        catq = const.tile([P, TP, 1024], U32, align_bytes=64)
+        cats = const.tile([P, TP, 1024], U8, align_bytes=64)
         wqk = const.tile([P, 2, CO], U32, align_bytes=64)
         wsk = const.tile([P, 2, CO], U8, align_bytes=64)
         wqn = const.tile([P, KO, 2, P], U32, align_bytes=64)
@@ -138,8 +138,8 @@ def tile_graphaggregation_pa_t_kernel(tc, feat_context, feat_target, adj, missin
 
                 def scale_block(s, n, share, gp):
                     a, tp = s // TP, s % TP
-                    if n == 0:
-                        u = loop.tile([P, 2, HOPS, N], BF16, name="u")
+                    if n == 0 and s not in us:
+                        u = loop.tile([P, 2, HOPS, N], BF16, bufs=3, name="u")
                         us[s] = u
                     tt, i = n % 2, n // 2
                     dst, src, sc = us[s][:, tt, i, :], adj_r[:, a, i, :], rcp[:, a, i, 2 * tp + tt : 2 * tp + tt + 1]
@@ -211,14 +211,18 @@ def tile_graphaggregation_pa_t_kernel(tc, feat_context, feat_target, adj, missin
                     pf = ps_x.tile([P, 512], F32, tag="x")
                     for e in range(2):
                         nc.tensor.transpose(out=pf[:, e * P : (e + 1) * P], in_=ft_w[:, a, e, tp, :], identity=ident[:])
-                    cg = loop.tile([P, 2048], BF16, align_bytes=64, name="cg", bufs=3)
+                    if s % 2 == 0:
+                        cg = loop.tile([P, 4096], BF16, align_bytes=64, name="cg")
+                        flats[s // 2] = cg
                     w = P if a else MH
-                    cg_v = cg[:].rearrange("p (h g t m j) -> p h g t m j", g=2, t=2, m=w, j=4)
+                    if a:
+                        cg_v = flats[s // 2][:].rearrange("p (b h g t m j) -> p b h g t m j", b=2, g=2, t=2, m=w, j=4)[:, s % 2]
+                    else:
+                        cg_v = flats[s // 2][:].rearrange("p (h g b t m j) -> p b h g t m j", b=2, g=2, t=2, m=w, j=4)[:, s % 2]
                     pf_v = pf[:].bitcast(BF16)[:, 0 : 4 * P].rearrange("p (e h m t) -> p h t m e", e=2, m=w, t=2)
                     for h in range(P // w):
                         nc.scalar.copy(out=cg_v[:, h, 0, :, :, 0:2], in_=pf_v[:, h])
                     cgs[s] = cg_v
-                    flats[s] = cg
 
                 def hop_pass(dst, s, t, e, lo, hi):
                     nc.tensor.matmul_mx(
@@ -261,9 +265,12 @@ def tile_graphaggregation_pa_t_kernel(tc, feat_context, feat_target, adj, missin
                             )
 
                 def quantise_cat(s):
-                    a, tp = s // TP, s % TP
+                    if s < TP and s % 2 == 0:
+                        return
+                    lo, hi = (0, 2) if s < TP else (s % 2, s % 2 + 1)
                     nc.vector.quantize_mx(
-                        out=catq[:, a, tp, :].bitcast(FP8X4), scales=cats[:, a, tp, :], in_=flats[s][:]
+                        out=catq[:, s // 2, 512 * lo : 512 * hi].bitcast(FP8X4), scales=cats[:, s // 2, 512 * lo : 512 * hi],
+                        in_=flats[s // 2][:, 2048 * lo : 2048 * hi],
                     )
 
                 def turn_weights(k):
@@ -280,14 +287,19 @@ def tile_graphaggregation_pa_t_kernel(tc, feat_context, feat_target, adj, missin
 
                 wns = {}
 
-                def turn_natural(late, wr2, b):
-                    w2_w = wr2[:].rearrange("p k c -> p (k c)").bitcast(F32).rearrange("p (k h q) -> p k h q", k=KO, q=P)
+                wns_w = []
+
+                def load_natural(dst, b):
+                    nc.sync.dma_start(out=dst, in_=wn_v[:, 4 * b : 4 * b + 4, :])
+                    wns_w.append(dst.rearrange("p k c -> p (k c)").bitcast(F32).rearrange("p (k h q) -> p k h q", k=4, q=P))
+
+                def turn_natural(late, b):
                     wt2 = late.tile([P, 2, 2, P, 4], BF16, align_bytes=64, name="wt2")
                     wt2_w = wt2[:].rearrange("p k g o j -> p (k g o j)").bitcast(F32).rearrange("p (k g o h) -> p k g o h", k=2, g=2, h=2)
                     for k in range(2):
                         pw = ps_x.tile([P, 512], F32, tag="x")
                         for h in range(4):
-                            nc.tensor.transpose(out=pw[:, h * P : (h + 1) * P], in_=w2_w[:, 2 * b + k, h, :], identity=ident[:])
+                            nc.tensor.transpose(out=pw[:, h * P : (h + 1) * P], in_=wns_w[b // 2][:, 2 * (b % 2) + k, h, :], identity=ident[:])
                         nc.scalar.copy(out=wt2_w[:, k], in_=pw[:].rearrange("p (g h o) -> p g o h", g=2, h=2))
                     wns[b] = wt2
 
@@ -302,18 +314,18 @@ def tile_graphaggregation_pa_t_kernel(tc, feat_context, feat_target, adj, missin
                     if h not in ots:
                         ot = late.tile([P, MH, KO, T], F32, name="ot", bufs=2)
                         ots[h] = ot
-                    pb = ps_x.tile([P, 4, P], F32, tag="x")
-                    for b in range(4):
+                    pb = ps_x.tile([P, 2, 256], F32, tag="x")
+                    for b in range(2):
                         for g in range(2):
-                            at = (2 * h + g) * P
+                            at = (2 * h + g) * 256
                             nc.tensor.matmul_mx(
                                 out=pb[:, b, :],
                                 lhsT=wqk[:, g, k * P : (k + 1) * P].bitcast(FP8X4), lhsT_scale=wsk[:, g, k * P : (k + 1) * P],
-                                rhs=catq[:, 0, 4 * t8 + b, at : at + P].bitcast(FP8X4), rhs_scale=cats[:, 0, 4 * t8 + b, at : at + P],
+                                rhs=catq[:, 2 * t8 + b, at : at + 256].bitcast(FP8X4), rhs_scale=cats[:, 2 * t8 + b, at : at + 256],
                                 start=(g == 0), stop=(g == 1),
                             )
                     nc.scalar.activation(
-                        out=ots[h][:, :, k, 8 * t8 : 8 * t8 + 8], in_=pb[:].rearrange("p b (t m) -> p m (b t)", t=2),
+                        out=ots[h][:, :, k, 8 * t8 : 8 * t8 + 8], in_=pb[:].rearrange("p b (t m) -> p m (b t)", t=4),
                         func=ACT.Relu, bias=bias_col[:, k : k + 1],
                     )
                     if (t8, k) == (1, KO - 1):
@@ -336,7 +348,7 @@ def tile_graphaggregation_pa_t_kernel(tc, feat_context, feat_target, adj, missin
                 mask_blocks(0, 1)
                 turn_blocks(0, 2)
                 turn_blocks(1, 0)
-                scale_blocks(2, 2)
+                scale_blocks(2, 6, True)
                 mask_blocks(0, 2)
                 mask_blocks(1, 0)
                 turn_blocks(1, 1)
@@ -348,21 +360,26 @@ def tile_graphaggregation_pa_t_kernel(tc, feat_context, feat_target, adj, missin
                 turn_blocks(2, 1)
                 quantise_norm(1)
                 regroup_context(0, 0, low, False)
-                regroup_context(0, 1, low, True)
-                regroup_context(0, 0, high, True)
+                regroup_context(0, 1, low, False)
+                regroup_context(0, 0, high, False)
                 regroup_context(0, 1, high, True)
+                scale_blocks(3, 6, True)
                 turn_target(0)
-                scale_blocks(3, 2)
                 quantise_context(0)
+                regroup_context(1, 0, whole, False)
                 neighbour_sums(0)
 
                 mixes = [(h, t8, k) for t8 in range(2) for h in range(2) for k in range(KO)]
 
-                def step(s, late, wr2):
-                    todo = mixes[max(0, s - LATE) * MIX_RATE : max(0, s + 1 - LATE) * MIX_RATE]
-                    first = min(MIX_FIRST, len(todo))
-                    if s < 6:
-                        regroup_context(s // 2 + 1, s % 2, whole, False)
+                def step(s, late):
+                    todo = mixes[max(0, s - LATE) * MIX_RATE // 3 : max(0, s + 1 - LATE) * MIX_RATE // 3]
+                    first = min(MIX_FIRST, len(todo) if s > TP else max(0, 16 - max(0, s - LATE) * MIX_RATE // 3))
+                    if s < 5:
+                        regroup_context((s + 3) // 2, (s + 1) % 2, whole, False)
+                    if s + 4 < STEPS:
+                        u = loop.tile([P, 2, HOPS, N], BF16, bufs=3, name="u")
+                        us[s + 4] = u
+                        nc.vector.memset(u[:, 0, 0, 0:2], 0.0)
                     if s + 2 < STEPS:
                         mask_blocks(s + 2, 0)
                         turn_blocks(s + 2, 2)
@@ -384,7 +401,7 @@ def tile_graphaggregation_pa_t_kernel(tc, feat_context, feat_target, adj, missin
                         quantise_cat(s - 1)
                     if s + 4 < STEPS:
                         scale_blocks(s + 4, SHARE, True)
-                    if s < 6 and s % 2 == 1:
+                    if s < 5 and s % 2 == 0:
                         quantise_context(s // 2 + 1)
                     if s + 1 < STEPS:
                         neighbour_sums(s + 1)
@@ -402,17 +419,20 @@ def tile_graphaggregation_pa_t_kernel(tc, feat_context, feat_target, adj, missin
                     if s >= TP + 4 and s < TP + 8:
                         quantise_natural(s - TP - 4)
                     if s >= TP + 3 and s < TP + 7:
-                        turn_natural(late, wr2, s - TP - 3)
-                    if 4 <= s < 6:
-                        quantise_weights(s - 4)
+                        turn_natural(late, s - TP - 3)
+                    if s == 4:
+                        quantise_weights(0)
+                        quantise_weights(1)
 
                 for s in range(LATE):
-                    step(s, None, None)
+                    step(s, None)
             with tc.tile_pool(name="late", bufs=1) as late:
-                wr2 = late.tile([P, KO, C], BF16, align_bytes=64)
-                nc.sync.dma_start(out=wr2[:], in_=wn_v)
+                wr2 = late.tile([P, 4, C], BF16, align_bytes=64)
+                load_natural(wr2[:], 0)
                 for s in range(LATE, STEPS):
-                    step(s, late, wr2)
+                    if s == TP:
+                        load_natural(ft_r[:, 0, :].rearrange("p (k c) -> p k c", k=4), 1)
+                    step(s, late)
                 quantise_cat(STEPS - 1)
 
         with ExitStack() as ph2:
@@ -423,12 +443,12 @@ def tile_graphaggregation_pa_t_kernel(tc, feat_context, feat_target, adj, missin
                 for tq in range(4):
                     pb = ps_o.tile([P, 4, P], F32)
                     for tt in range(4):
-                        tp, at = 2 * tq + tt // 2, (tt % 2) * P
+                        q, at = TP // 2 + tq, (tt // 2) * 512 + (tt % 2) * P
                         for g in range(2):
                             nc.tensor.matmul_mx(
                                 out=pb[:, tt, :],
-                                lhsT=catq[:, 1, tp, g * 256 + at : g * 256 + at + P].bitcast(FP8X4),
-                                lhsT_scale=cats[:, 1, tp, g * 256 + at : g * 256 + at + P],
+                                lhsT=catq[:, q, g * 256 + at : g * 256 + at + P].bitcast(FP8X4),
+                                lhsT_scale=cats[:, q, g * 256 + at : g * 256 + at + P],
                                 rhs=wqn[:, ob, g, :].bitcast(FP8X4),
                                 rhs_scale=wsn[:, ob, g, :],
                                 start=(g == 0), stop=(g == 1),

@@ -20,7 +20,7 @@ MH = 64
 TP = T // 2
 STEPS = 2 * TP
 KO = CO // P
-SHARE = 4
+SHARE = 5
 LATE = 5
 MIX_FIRST = 2
 MIX_RATE = 15
@@ -54,10 +54,9 @@ def tile_graphaggregation_pa_t_kernel(tc, feat_context, feat_target, adj, missin
         fcs = const.tile([P, T, D], U8, align_bytes=64)
         catq = const.tile([P, TP, 1024], U32, align_bytes=64)
         cats = const.tile([P, TP, 1024], U8, align_bytes=64)
-        wqk = const.tile([P, 2, CO], U32, align_bytes=64)
-        wsk = const.tile([P, 2, CO], U8, align_bytes=64)
-        wqn = const.tile([P, KO, 2, P], U32, align_bytes=64)
-        wsn = const.tile([P, KO, 2, P], U8, align_bytes=64)
+        wqk = const.tile([P, 2, CO], U32, tag="wq", align_bytes=64)
+        wsk = const.tile([P, 2, CO], U8, tag="ws", align_bytes=64)
+        natural = []
 
         with ExitStack() as ph1:
             loop = ph1.enter_context(tc.tile_pool(name="loop", bufs=2))
@@ -134,13 +133,18 @@ def tile_graphaggregation_pa_t_kernel(tc, feat_context, feat_target, adj, missin
                     nc.vector.reciprocal(out=rcp[:, a].rearrange("p i t -> p (i t)"), in_=sums[a][:, 0 : HOPS * T])
 
                 fc_view = fc_raw[:].rearrange("p j (d e q t) -> p q e d j t", e=2, q=4, t=4)
-                us, pts, ngs, nqs, nss, cgs, fcgs, p0s, p1s, flats, ots = {}, {}, {}, {}, {}, {}, {}, {}, {}, {}, {}
+                us, pts, ngs, nqs, nss, cgs, fcgs, p0s, p1s, flats, ots, pairs = {}, {}, {}, {}, {}, {}, {}, {}, {}, {}, {}, {}
+
+                def open_scalings(s):
+                    u = loop.tile([P, 2, HOPS, N], BF16, bufs=3, name="u")
+                    us[s] = u
+                    if s > 3:
+                        nc.vector.memset(u[:, 0, 0, 0:2], 0.0)
 
                 def scale_block(s, n, share, gp):
                     a, tp = s // TP, s % TP
-                    if n == 0 and s not in us:
-                        u = loop.tile([P, 2, HOPS, N], BF16, bufs=3, name="u")
-                        us[s] = u
+                    if s not in us:
+                        open_scalings(s)
                     tt, i = n % 2, n // 2
                     dst, src, sc = us[s][:, tt, i, :], adj_r[:, a, i, :], rcp[:, a, i, 2 * tp + tt : 2 * tp + tt + 1]
                     if n < share and gp:
@@ -211,6 +215,9 @@ def tile_graphaggregation_pa_t_kernel(tc, feat_context, feat_target, adj, missin
                     pf = ps_x.tile([P, 512], F32, tag="x")
                     for e in range(2):
                         nc.tensor.transpose(out=pf[:, e * P : (e + 1) * P], in_=ft_w[:, a, e, tp, :], identity=ident[:])
+                    pair = loop.tile([P, 2, 2, P, 2], BF16, name="pair", bufs=3)
+                    nc.scalar.copy(out=pair[:, 0], in_=pf[:].bitcast(BF16)[:, 0 : 4 * P].rearrange("p (e m t) -> p t m e", e=2, t=2))
+                    pairs[s] = pair
                     if s % 2 == 0:
                         cg = loop.tile([P, 4096], BF16, align_bytes=64, name="cg")
                         flats[s // 2] = cg
@@ -219,10 +226,18 @@ def tile_graphaggregation_pa_t_kernel(tc, feat_context, feat_target, adj, missin
                         cg_v = flats[s // 2][:].rearrange("p (b h g t m j) -> p b h g t m j", b=2, g=2, t=2, m=w, j=4)[:, s % 2]
                     else:
                         cg_v = flats[s // 2][:].rearrange("p (h g b t m j) -> p b h g t m j", b=2, g=2, t=2, m=w, j=4)[:, s % 2]
-                    pf_v = pf[:].bitcast(BF16)[:, 0 : 4 * P].rearrange("p (e h m t) -> p h t m e", e=2, m=w, t=2)
-                    for h in range(P // w):
-                        nc.scalar.copy(out=cg_v[:, h, 0, :, :, 0:2], in_=pf_v[:, h])
                     cgs[s] = cg_v
+
+                def interleave_target(s):
+                    w = P if s >= TP else MH
+                    words = pairs[s][:].rearrange("p x t m e -> p (x t m e)").bitcast(F32).rearrange("p (x t h m) -> p h t m x", x=2, t=2, m=w)
+                    flat_w = flats[s // 2][:].bitcast(F32)
+                    if s >= TP:
+                        dst = flat_w.rearrange("p (b h g t m x) -> p b h g t m x", b=2, g=2, t=2, m=w, x=2)[:, s % 2]
+                    else:
+                        dst = flat_w.rearrange("p (h g b t m x) -> p b h g t m x", b=2, g=2, t=2, m=w, x=2)[:, s % 2]
+                    for h in range(P // w):
+                        nc.scalar.copy(out=dst[:, h, 0], in_=words[:, h])
 
                 def hop_pass(dst, s, t, e, lo, hi):
                     nc.tensor.matmul_mx(
@@ -247,22 +262,15 @@ def tile_graphaggregation_pa_t_kernel(tc, feat_context, feat_target, adj, missin
                         p1s[s].append(pp)
 
                 def add_target(s):
-                    cg = cgs[s]
                     w = P if s >= TP else MH
-                    for h in range(P // w):
-                        at = slice(h * w, (h + 1) * w)
-                        nc.vector.tensor_tensor(
-                            out=cg[:, h, 0, :, :, 2:4], in0=p0s[s][:].rearrange("p t e m -> p t m e")[:, :, at],
-                            in1=cg[:, h, 0, :, :, 0:2], op=ALU.add,
-                        )
+                    ft = pairs[s][:, 0]
+                    nc.vector.tensor_tensor(out=pairs[s][:, 1], in0=p0s[s][:].rearrange("p t e m -> p t m e"), in1=ft, op=ALU.add)
                     for tt in range(2):
-                        for h in range(P // w):
-                            at = slice(h * w, (h + 1) * w)
-                            nc.vector.tensor_tensor(
-                                out=cg[:, h, 1, tt].rearrange("p m (i e) -> p m i e", i=2),
-                                in0=p1s[s][tt][:].rearrange("p e i m -> p m i e")[:, at],
-                                in1=cg[:, h, 0, tt, :, 0:2].unsqueeze(2).to_broadcast([P, w, 2, 2]), op=ALU.add,
-                            )
+                        nc.vector.tensor_tensor(
+                            out=cgs[s][:, :, 1, tt].rearrange("p h m (i e) -> p h m i e", i=2),
+                            in0=p1s[s][tt][:].rearrange("p e i (h m) -> p h m i e", m=w),
+                            in1=ft[:, tt].rearrange("p (h m) e -> p h m e", m=w).unsqueeze(3).to_broadcast([P, P // w, w, 2, 2]), op=ALU.add,
+                        )
 
                 def quantise_cat(s):
                     if s < TP and s % 2 == 0:
@@ -304,6 +312,11 @@ def tile_graphaggregation_pa_t_kernel(tc, feat_context, feat_target, adj, missin
                     wns[b] = wt2
 
                 def quantise_natural(b):
+                    if b == 0:
+                        wqn = const.tile([P, KO, 2, P], U32, tag="wq", align_bytes=64)
+                        wsn = const.tile([P, KO, 2, P], U8, tag="ws", align_bytes=64)
+                        natural.extend((wqn, wsn))
+                    wqn, wsn = natural
                     nc.vector.quantize_mx(
                         out=wqn[:, 2 * b : 2 * b + 2].rearrange("p k g o -> p (k g o)").bitcast(FP8X4),
                         scales=wsn[:, 2 * b : 2 * b + 2].rearrange("p k g o -> p (k g o)"),
@@ -377,9 +390,7 @@ def tile_graphaggregation_pa_t_kernel(tc, feat_context, feat_target, adj, missin
                     if s < 5:
                         regroup_context((s + 3) // 2, (s + 1) % 2, whole, False)
                     if s + 4 < STEPS:
-                        u = loop.tile([P, 2, HOPS, N], BF16, bufs=3, name="u")
-                        us[s + 4] = u
-                        nc.vector.memset(u[:, 0, 0, 0:2], 0.0)
+                        open_scalings(s + 4)
                     if s + 2 < STEPS:
                         mask_blocks(s + 2, 0)
                         turn_blocks(s + 2, 2)
@@ -401,8 +412,6 @@ def tile_graphaggregation_pa_t_kernel(tc, feat_context, feat_target, adj, missin
                         quantise_cat(s - 1)
                     if s + 4 < STEPS:
                         scale_blocks(s + 4, SHARE, True)
-                    if s < 5 and s % 2 == 0:
-                        quantise_context(s // 2 + 1)
                     if s + 1 < STEPS:
                         neighbour_sums(s + 1)
                     if s + 3 < STEPS:
@@ -410,12 +419,17 @@ def tile_graphaggregation_pa_t_kernel(tc, feat_context, feat_target, adj, missin
                     if s < 4:
                         turn_weights(2 * s)
                         turn_weights(2 * s + 1)
-                    for h, t8, k in todo[first:]:
+                    for h, t8, k in todo[first : first + 0]:
+                        mix_first(late, h, t8, k)
+                    interleave_target(s)
+                    for h, t8, k in todo[first + 0 :]:
                         mix_first(late, h, t8, k)
                     if s == 3:
                         invert_sums(1)
                     if s + 2 < STEPS:
                         quantise_norm(s + 2)
+                    if s < 5 and s % 2 == 0:
+                        quantise_context(s // 2 + 1)
                     if s >= TP + 4 and s < TP + 8:
                         quantise_natural(s - TP - 4)
                     if s >= TP + 3 and s < TP + 7:
@@ -438,6 +452,7 @@ def tile_graphaggregation_pa_t_kernel(tc, feat_context, feat_target, adj, missin
         with ExitStack() as ph2:
             opool = ph2.enter_context(tc.tile_pool(name="opool", bufs=4, reuse_waits="tile"))
             ps_o = ph2.enter_context(tc.psum_pool(name="ps_o", bufs=8, reuse_waits="tile"))
+            wqn, wsn = natural
             for ob in range(8):
                 ot = opool.tile([P, P, T], F32)
                 for tq in range(4):

@@ -361,7 +361,7 @@ def tile_graphaggregation_pa_t_kernel(tc, feat_context, feat_target, adj, missin
                 mask_blocks(0, 1)
                 turn_blocks(0, 2)
                 turn_blocks(1, 0)
-                scale_blocks(2, 6, True)
+                scale_blocks(2, 4, True)
                 mask_blocks(0, 2)
                 mask_blocks(1, 0)
                 turn_blocks(1, 1)
@@ -376,7 +376,7 @@ def tile_graphaggregation_pa_t_kernel(tc, feat_context, feat_target, adj, missin
                 regroup_context(0, 1, low, False)
                 regroup_context(0, 0, high, False)
                 regroup_context(0, 1, high, True)
-                scale_blocks(3, 6, True)
+                scale_blocks(3, 4, True)
                 turn_target(0)
                 quantise_context(0)
                 regroup_context(1, 0, whole, False)
@@ -450,7 +450,7 @@ def tile_graphaggregation_pa_t_kernel(tc, feat_context, feat_target, adj, missin
                 quantise_cat(STEPS - 1)
 
         with ExitStack() as ph2:
-            opool = ph2.enter_context(tc.tile_pool(name="opool", bufs=4, reuse_waits="tile"))
+            opool = ph2.enter_context(tc.tile_pool(name="opool", bufs=8, reuse_waits="tile"))
             ps_o = ph2.enter_context(tc.psum_pool(name="ps_o", bufs=8, reuse_waits="tile"))
             wqn, wsn = natural
             for ob in range(8):
@@ -473,9 +473,12 @@ def tile_graphaggregation_pa_t_kernel(tc, feat_context, feat_target, adj, missin
                         in1=bias_bc[:, ob * P : (ob + 1) * P].unsqueeze(2).to_broadcast([P, P, 4]), op=ALU.add,
                     )
                 flat = ot[:].rearrange("p o t -> p (o t)")
-                half = P * T // 2
-                for h in range(2):
-                    nc.scalar.activation(out=flat[:, h * half : (h + 1) * half], in_=flat[:, h * half : (h + 1) * half], func=ACT.Relu)
-                    nc.sync.dma_start(
-                        out=out_m[:, 1, (2 * ob + h) * half : (2 * ob + h + 1) * half], in_=flat[:, h * half : (h + 1) * half]
-                    )
+                pieces = 4 if ob == KO - 1 else 2
+                size = P * T // pieces
+                for h in range(pieces):
+                    part = flat[:, h * size : (h + 1) * size]
+                    if ob == KO - 1 and h % 2 == 1:
+                        nc.vector.tensor_scalar(out=part, in0=part, scalar1=0.0, scalar2=None, op0=ALU.max)
+                    else:
+                        nc.scalar.activation(out=part, in_=part, func=ACT.Relu)
+                    nc.sync.dma_start(out=out_m[:, 1, ob * P * T + h * size : ob * P * T + (h + 1) * size], in_=part)

@@ -71,8 +71,9 @@ def tile_graphaggregation_pa_t_kernel(tc, feat_context, feat_target, adj, missin
                 make_identity(nc, ident[:])
                 nc.gpsimd.memset(ones_l[:], 1.0 / P)
                 nc.gpsimd.memset(ones_r[:], 1.0)
-                nc.sync.dma_start(out=adj_r[:, 0], in_=adj_v[:, 0])
+                nc.sync.dma_start(out=adj_r[:, 0, 0], in_=adj_v[:, 0, 0])
                 nc.sync.dma_start(out=mask_pad[0:T, :], in_=mask_v)
+                nc.sync.dma_start(out=adj_r[:, 0, 1:HOPS], in_=adj_v[:, 0, 1:HOPS])
                 fc_raw = big.tile([P, 4, D * T], BF16)
                 for h in range(2):
                     for u in range(2):
@@ -107,30 +108,28 @@ def tile_graphaggregation_pa_t_kernel(tc, feat_context, feat_target, adj, missin
 
                 adj_ts, sums = {}, {}
 
-                def turn_adj(a):
-                    adj_t = big.tile([P, 2, HOPS * P], F32, name="adj_t")
-                    for u in range(2):
-                        pa = ps_x.tile([P, 512], F32, tag="x")
-                        for i in range(HOPS):
-                            nc.tensor.transpose(out=pa[:, i * P : (i + 1) * P], in_=adj_w[:, a, i, u, :], identity=ident[:])
-                        if (a, u) == (0, 0):
-                            nc.vector.tensor_copy(out=adj_t[:, u, :], in_=pa[:, 0 : HOPS * P])
-                        else:
-                            nc.scalar.copy(out=adj_t[:, u, :], in_=pa[:, 0 : HOPS * P])
-                    adj_ts[a] = adj_t
+                def turn_adj(a, blocks, engine):
+                    if a not in adj_ts:
+                        adj_t = big.tile([P, HOPS, 2, P], F32, name="adj_t")
+                        adj_ts[a] = adj_t
+                    pa = ps_x.tile([P, 4, P], F32, tag="x")
+                    for n, (i, u) in enumerate(blocks):
+                        nc.tensor.transpose(out=pa[:, n, :], in_=adj_w[:, a, i, u, :], identity=ident[:])
+                    i, u, n = blocks[0][0], blocks[0][1], len(blocks)
+                    dst = adj_ts[a][:, i] if n == 2 else adj_ts[a][:, :, u, :]
+                    engine(out=dst, in_=pa[:, 0:n, :])
 
-                def row_sums(a):
-                    adj_b = adj_ts[a][:].rearrange("p u c -> p (u c)").bitcast(BF16).rearrange("p (u i c e) -> p u i e c", u=2, i=HOPS, e=2)
-                    psum_s = ps_x.tile([P, 512], F32, tag="x")
-                    for i in range(HOPS):
-                        dst = psum_s[:, i * T : (i + 1) * T]
-                        nc.tensor.matmul(out=dst, lhsT=ones_l[:], rhs=ones_r[:], start=True, stop=False)
+                def row_sums(a, hops):
+                    adj_b = adj_ts[a][:].rearrange("p i u m -> p (i u m)").bitcast(BF16).rearrange("p (i u m e) -> p i u e m", i=HOPS, u=2, e=2)
+                    psum_s = ps_x.tile([P, HOPS, T], F32, tag="x")
+                    for n, i in enumerate(hops):
+                        nc.tensor.matmul(out=psum_s[:, n, :], lhsT=ones_l[:], rhs=ones_r[:], start=True, stop=False)
                         for j in range(4):
-                            nc.tensor.matmul(out=dst, lhsT=adj_b[:, j // 2, i, j % 2, :], rhs=keep_t[:, j, :], start=False, stop=(j == 3))
-                    sums[a] = psum_s
+                            nc.tensor.matmul(out=psum_s[:, n, :], lhsT=adj_b[:, i, j // 2, j % 2, :], rhs=keep_t[:, j, :], start=False, stop=(j == 3))
+                    sums[a, hops] = psum_s
 
-                def invert_sums(a):
-                    nc.vector.reciprocal(out=rcp[:, a].rearrange("p i t -> p (i t)"), in_=sums[a][:, 0 : HOPS * T])
+                def invert_sums(a, hops):
+                    nc.vector.reciprocal(out=rcp[:, a, hops[0] : hops[-1] + 1, :], in_=sums[a, hops][:, 0 : len(hops), :])
 
                 fc_view = fc_raw[:].rearrange("p j (d e q t) -> p q e d j t", e=2, q=4, t=4)
                 us, pts, ngs, nqs, nss, cgs, fcgs, p0s, p1s, flats, ots, pairs = {}, {}, {}, {}, {}, {}, {}, {}, {}, {}, {}, {}
@@ -349,12 +348,23 @@ def tile_graphaggregation_pa_t_kernel(tc, feat_context, feat_target, adj, missin
                             )
 
                 whole, low, high = (0, P), (0, P // 2), (P // 2, P)
-                turn_adj(0)
+                turn_adj(0, ((0, 0), (0, 1)), nc.vector.tensor_copy)
                 turn_mask()
-                row_sums(0)
-                invert_sums(0)
-                scale_blocks(0, 4)
+                row_sums(0, (0,))
+                turn_adj(0, ((1, 0), (1, 1)), nc.scalar.copy)
+                turn_adj(0, ((2, 0), (2, 1)), nc.scalar.copy)
+                invert_sums(0, (0,))
+                scale_block(0, 0, 4, False)
+                scale_block(0, 1, 4, False)
+                row_sums(0, (1,))
+                row_sums(0, (2,))
                 turn_blocks(0, 0)
+                invert_sums(0, (1,))
+                scale_block(0, 2, 4, False)
+                scale_block(0, 3, 4, False)
+                invert_sums(0, (2,))
+                scale_block(0, 4, 4, False)
+                scale_block(0, 5, 4, False)
                 turn_blocks(0, 1)
                 scale_blocks(1, 2)
                 mask_blocks(0, 0)
@@ -400,9 +410,10 @@ def tile_graphaggregation_pa_t_kernel(tc, feat_context, feat_target, adj, missin
                     if s + 1 < STEPS:
                         turn_target(s + 1)
                     if s == 1:
-                        turn_adj(1)
+                        for u in range(2):
+                            turn_adj(1, tuple((i, u) for i in range(HOPS)), nc.scalar.copy)
                     if s == 2:
-                        row_sums(1)
+                        row_sums(1, (0, 1, 2))
                     for h, t8, k in todo[:first]:
                         mix_first(late, h, t8, k)
                     add_target(s)
@@ -425,7 +436,7 @@ def tile_graphaggregation_pa_t_kernel(tc, feat_context, feat_target, adj, missin
                     for h, t8, k in todo[first + 0 :]:
                         mix_first(late, h, t8, k)
                     if s == 3:
-                        invert_sums(1)
+                        invert_sums(1, (0, 1, 2))
                     if s + 2 < STEPS:
                         quantise_norm(s + 2)
                     if s < 5 and s % 2 == 0:
@@ -481,4 +492,7 @@ def tile_graphaggregation_pa_t_kernel(tc, feat_context, feat_target, adj, missin
                         nc.vector.tensor_scalar(out=part, in0=part, scalar1=0.0, scalar2=None, op0=ALU.max)
                     else:
                         nc.scalar.activation(out=part, in_=part, func=ACT.Relu)
-                    nc.sync.dma_start(out=out_m[:, 1, ob * P * T + h * size : ob * P * T + (h + 1) * size], in_=part)
+                    if ob in (0, KO - 1):
+                        nc.sync.dma_start(out=out_m[:, 1, ob * P * T + h * size : ob * P * T + (h + 1) * size], in_=part)
+                if 0 < ob < KO - 1:
+                    nc.sync.dma_start(out=out_m[:, 1, ob * P * T : (ob + 1) * P * T], in_=flat)

@@ -23,7 +23,7 @@ KO = CO // P
 SHARE = 5
 LATE = 5
 MIX_FIRST = 2
-MIX_RATE = 15
+MIX_RATE = 14
 
 
 def tile_graphaggregation_pa_t_kernel(tc, feat_context, feat_target, adj, missing_mask_context, W_mlp, b_mlp, out):
@@ -322,25 +322,33 @@ def tile_graphaggregation_pa_t_kernel(tc, feat_context, feat_target, adj, missin
                         in_=wns[b][:].rearrange("p k g o j -> p (k g o j)"),
                     )
 
-                def mix_first(late, h, t8, k):
+                def mix_first(late, h, parts):
                     if h not in ots:
                         ot = late.tile([P, MH, KO, T], F32, name="ot", bufs=2)
                         ots[h] = ot
                     pb = ps_x.tile([P, 2, 256], F32, tag="x")
-                    for b in range(2):
+                    for b, (q, k) in enumerate(parts):
                         for g in range(2):
                             at = (2 * h + g) * 256
                             nc.tensor.matmul_mx(
                                 out=pb[:, b, :],
                                 lhsT=wqk[:, g, k * P : (k + 1) * P].bitcast(FP8X4), lhsT_scale=wsk[:, g, k * P : (k + 1) * P],
-                                rhs=catq[:, 2 * t8 + b, at : at + 256].bitcast(FP8X4), rhs_scale=cats[:, 2 * t8 + b, at : at + 256],
+                                rhs=catq[:, q, at : at + 256].bitcast(FP8X4), rhs_scale=cats[:, q, at : at + 256],
                                 start=(g == 0), stop=(g == 1),
                             )
-                    nc.scalar.activation(
-                        out=ots[h][:, :, k, 8 * t8 : 8 * t8 + 8], in_=pb[:].rearrange("p b (t m) -> p m (b t)", t=4),
-                        func=ACT.Relu, bias=bias_col[:, k : k + 1],
-                    )
-                    if (t8, k) == (1, KO - 1):
+                    (q, k), (q2, k2) = parts
+                    if k == k2:
+                        nc.scalar.activation(
+                            out=ots[h][:, :, k, 4 * q : 4 * q + 8], in_=pb[:].rearrange("p b (t m) -> p m (b t)", t=4),
+                            func=ACT.Relu, bias=bias_col[:, k : k + 1],
+                        )
+                    else:
+                        for b, (q, k) in enumerate(parts):
+                            nc.scalar.activation(
+                                out=ots[h][:, :, k, 4 * q : 4 * q + 4], in_=pb[:, b, :].rearrange("p (t m) -> p m t", t=4),
+                                func=ACT.Relu, bias=bias_col[:, k : k + 1],
+                            )
+                    if parts[-1] == (3, KO - 1):
                         for b in range(2):
                             nc.sync.dma_start(
                                 out=out_o[:, 0, h * MH + 32 * b : h * MH + 32 * b + 32, :],
@@ -392,7 +400,9 @@ def tile_graphaggregation_pa_t_kernel(tc, feat_context, feat_target, adj, missin
                 regroup_context(1, 0, whole, False)
                 neighbour_sums(0)
 
-                mixes = [(h, t8, k) for t8 in range(2) for h in range(2) for k in range(KO)]
+                eights = [[(h, ((0, k), (1, k))) for k in range(KO)] for h in range(2)]
+                fours = [[[(h, ((q, k), (q, k + 1))) for k in range(0, KO, 2)] for q in (2, 3)] for h in range(2)]
+                mixes = eights[0] + fours[0][0] + eights[1][:4] + fours[0][1] + eights[1][4:] + fours[1][0] + fours[1][1]
 
                 def step(s, late):
                     todo = mixes[max(0, s - LATE) * MIX_RATE // 3 : max(0, s + 1 - LATE) * MIX_RATE // 3]
@@ -414,8 +424,8 @@ def tile_graphaggregation_pa_t_kernel(tc, feat_context, feat_target, adj, missin
                             turn_adj(1, tuple((i, u) for i in range(HOPS)), nc.scalar.copy)
                     if s == 2:
                         row_sums(1, (0, 1, 2))
-                    for h, t8, k in todo[:first]:
-                        mix_first(late, h, t8, k)
+                    for h, parts in todo[:first]:
+                        mix_first(late, h, parts)
                     add_target(s)
                     if s + 2 < STEPS:
                         mask_blocks(s + 2, 2)
@@ -430,11 +440,11 @@ def tile_graphaggregation_pa_t_kernel(tc, feat_context, feat_target, adj, missin
                     if s < 4:
                         turn_weights(2 * s)
                         turn_weights(2 * s + 1)
-                    for h, t8, k in todo[first : first + 0]:
-                        mix_first(late, h, t8, k)
+                    for h, parts in todo[first : first + 0]:
+                        mix_first(late, h, parts)
                     interleave_target(s)
-                    for h, t8, k in todo[first + 0 :]:
-                        mix_first(late, h, t8, k)
+                    for h, parts in todo[first + 0 :]:
+                        mix_first(late, h, parts)
                     if s == 3:
                         invert_sums(1, (0, 1, 2))
                     if s + 2 < STEPS:
@@ -492,7 +502,4 @@ def tile_graphaggregation_pa_t_kernel(tc, feat_context, feat_target, adj, missin
                         nc.vector.tensor_scalar(out=part, in0=part, scalar1=0.0, scalar2=None, op0=ALU.max)
                     else:
                         nc.scalar.activation(out=part, in_=part, func=ACT.Relu)
-                    if ob in (0, KO - 1):
-                        nc.sync.dma_start(out=out_m[:, 1, ob * P * T + h * size : ob * P * T + (h + 1) * size], in_=part)
-                if 0 < ob < KO - 1:
-                    nc.sync.dma_start(out=out_m[:, 1, ob * P * T : (ob + 1) * P * T], in_=flat)
+                    nc.sync.dma_start(out=out_m[:, 1, ob * P * T + h * size : ob * P * T + (h + 1) * size], in_=part)

from contextlib import ExitStack

import concourse.mybir as mybir
from concourse.masks import make_identity

BF16 = mybir.dt.bfloat16
F32 = mybir.dt.float32
U32 = mybir.dt.uint32
U8 = mybir.dt.uint8
FP8X4 = mybir.dt.float8_e4m3fn_x4
ALU = mybir.AluOpType
ACT = mybir.ActivationFunctionType

P = 128
T, M, N, D, HOPS, CO = 16, 256, 512, 256, 3, 1024
C = (HOPS + 1) * D
FLOPS = 2 * T * HOPS * M * N * D + 2 * M * T * CO * C

MH = 64
TP = T // 2
STEPS = 2 * TP
KO = CO // P
SHARE = 5
LATE = 5
MIX_FIRST = 2
MIX_RATE = 14


def tile_graphaggregation_pa_t_kernel(tc, feat_context, feat_target, adj, missing_mask_context, W_mlp, b_mlp, out):
    nc = tc.nc
    fc_v = feat_context.rearrange("o (u p e) d t -> p (o u) e (d t)", p=P, e=2)
    ft_v = feat_target.rearrange("o (a m) d t -> m (o a) (d t)", m=P)
    adj_v = adj.rearrange("o i (a m) n -> m a (o i) n", m=P)
    mask_v = missing_mask_context.rearrange("o t n -> (o t) n")
    w_v = W_mlp.rearrange("(p k) c -> p k c", k=KO)
    wn_v = W_mlp.rearrange("(b q) c -> q b c", q=P)
    out_o = out.rearrange("o (a m) (p k) t -> p (o a) m (k t)", m=P, k=KO)
    out_m = out.rearrange("o (a m) c t -> m (o a) (c t)", m=P)

    with ExitStack() as top:
        top.enter_context(tc.manual_schedule())
        const = top.enter_context(tc.tile_pool(name="const", bufs=1))

        adj_r = const.tile([P, 2, HOPS, N], BF16)
        ident = const.tile([P, P], F32)
        ones_l = const.tile([P, P], BF16)
        ones_r = const.tile([P, T], BF16)
        bias_bc = const.tile([P, CO], BF16)
        bias_col = const.tile([P, KO], BF16)
        keep_t = const.tile([P, 4, T], BF16)
        keep_g = const.tile([P, T, 4], BF16)
        rcp = const.tile([P, 2, HOPS, T], F32)
        fcq = const.tile([P, T, D], U32, align_bytes=64)
        fcs = const.tile([P, T, D], U8, align_bytes=64)
        catq = const.tile([P, TP, 1024], U32, align_bytes=64)
        cats = const.tile([P, TP, 1024], U8, align_bytes=64)
        wqk = const.tile([P, 2, CO], U32, tag="wq", align_bytes=64)
        wsk = const.tile([P, 2, CO], U8, tag="ws", align_bytes=64)
        natural = []

        with ExitStack() as ph1:
            loop = ph1.enter_context(tc.tile_pool(name="loop", bufs=2))
            ps_t = ph1.enter_context(tc.psum_pool(name="ps_t", bufs=2))
            ps_s = ph1.enter_context(tc.psum_pool(name="ps_s", bufs=3))
            ps_x = ph1.enter_context(tc.psum_pool(name="ps_x", bufs=3))
            ft_r = loop.tile([P, 2, D * T], BF16, bufs=1)
            with tc.tile_pool(name="big", bufs=1) as big:

                mask_pad = big.tile([P, N], BF16)
                nc.vector.memset(mask_pad[:], 0.0)
                make_identity(nc, ident[:])
                nc.gpsimd.memset(ones_l[:], 1.0 / P)
                nc.gpsimd.memset(ones_r[:], 1.0)
                nc.sync.dma_start(out=adj_r[:, 0, 0], in_=adj_v[:, 0, 0])
                nc.sync.dma_start(out=mask_pad[0:T, :], in_=mask_v)
                nc.sync.dma_start(out=adj_r[:, 0, 1:HOPS], in_=adj_v[:, 0, 1:HOPS])
                fc_raw = big.tile([P, 4, D * T], BF16)
                for h in range(2):
                    for u in range(2):
                        nc.sync.dma_start(
                            out=fc_raw[:, 2 * u : 2 * u + 2, h * 2048 : (h + 1) * 2048], in_=fc_v[:, u, :, h * 2048 : (h + 1) * 2048]
                        )
                nc.sync.dma_start(out=ft_r[:, 0, :], in_=ft_v[:, 0, :])
                nc.sync.dma_start(out=adj_r[:, 1], in_=adj_v[:, 1])
                w_r = big.tile([P, KO, C], BF16, tag="w", align_bytes=64)
                nc.sync.dma_start(out=w_r[:], in_=w_v)
                nc.sync.dma_start(out=ft_r[:, 1, :], in_=ft_v[:, 1, :])
                nc.sync.dma_start(out=bias_col[:], in_=b_mlp.rearrange("(p k) -> p k", k=KO))
                nc.sync.dma_start(out=bias_bc[:], in_=b_mlp.partition_broadcast(P))
                wtg = big.tile([P, 2, CO, 4], BF16, align_bytes=64)

                adj_w = adj_r[:].rearrange("p a i n -> p (a i n)").bitcast(F32).rearrange("p (a i u q) -> p a i u q", a=2, i=HOPS, u=2)
                mask_w = mask_pad[:].bitcast(F32)
                ft_w = ft_r[:].rearrange("p a x -> p (a x)").bitcast(F32).rearrange("p (a d e w) -> p a e w d", a=2, e=2, w=TP)
                w_w = w_r[:].rearrange("p k c -> p (k c)").bitcast(F32).rearrange("p (k h q) -> p k h q", k=KO, q=P)

                def turn_mask():
                    pm = ps_x.tile([P, 512], F32, tag="x")
                    for u in range(2):
                        nc.tensor.transpose(out=pm[:, u * P : (u + 1) * P], in_=mask_w[:, u * P : (u + 1) * P], identity=ident[:])
                    pm_v = pm[:].bitcast(BF16)[:, 0 : 4 * P].rearrange("p (u q e) -> p u e q", u=2, e=2)[:, :, :, 0:T]
                    nc.vector.tensor_scalar(
                        out=keep_t[:].rearrange("p (u e) t -> p u e t", u=2), in0=pm_v, scalar1=-1.0, scalar2=1.0, op0=ALU.mult, op1=ALU.add
                    )
                    nc.vector.tensor_scalar(
                        out=keep_g[:].rearrange("p t (u e) -> p u e t", u=2), in0=pm_v, scalar1=-1.0, scalar2=1.0, op0=ALU.mult, op1=ALU.add
                    )

                adj_ts, sums = {}, {}

                def turn_adj(a, blocks, engine):
                    if a not in adj_ts:
                        adj_t = big.tile([P, HOPS, 2, P], F32, name="adj_t")
                        adj_ts[a] = adj_t
                    pa = ps_x.tile([P, 4, P], F32, tag="x")
                    for n, (i, u) in enumerate(blocks):
                        nc.tensor.transpose(out=pa[:, n, :], in_=adj_w[:, a, i, u, :], identity=ident[:])
                    i, u, n = blocks[0][0], blocks[0][1], len(blocks)
                    dst = adj_ts[a][:, i] if n == 2 else adj_ts[a][:, :, u, :]
                    engine(out=dst, in_=pa[:, 0:n, :])

                def row_sums(a, hops):
                    adj_b = adj_ts[a][:].rearrange("p i u m -> p (i u m)").bitcast(BF16).rearrange("p (i u m e) -> p i u e m", i=HOPS, u=2, e=2)
                    psum_s = ps_x.tile([P, HOPS, T], F32, tag="x")
                    for n, i in enumerate(hops):
                        nc.tensor.matmul(out=psum_s[:, n, :], lhsT=ones_l[:], rhs=ones_r[:], start=True, stop=False)
                        for j in range(4):
                            nc.tensor.matmul(out=psum_s[:, n, :], lhsT=adj_b[:, i, j // 2, j % 2, :], rhs=keep_t[:, j, :], start=False, stop=(j == 3))
                    sums[a, hops] = psum_s

                def invert_sums(a, hops):
                    nc.vector.reciprocal(out=rcp[:, a, hops[0] : hops[-1] + 1, :], in_=sums[a, hops][:, 0 : len(hops), :])

                fc_view = fc_raw[:].rearrange("p j (d e q t) -> p q e d j t", e=2, q=4, t=4)
                us, pts, ngs, nqs, nss, cgs, fcgs, p0s, p1s, flats, ots, pairs = {}, {}, {}, {}, {}, {}, {}, {}, {}, {}, {}, {}

                def open_scalings(s):
                    u = loop.tile([P, 2, HOPS, N], BF16, bufs=3, name="u")
                    us[s] = u
                    if s > 3:
                        nc.vector.memset(u[:, 0, 0, 0:2], 0.0)

                def scale_block(s, n, share, gp):
                    a, tp = s // TP, s % TP
                    if s not in us:
                        open_scalings(s)
                    tt, i = n % 2, n // 2
                    dst, src, sc = us[s][:, tt, i, :], adj_r[:, a, i, :], rcp[:, a, i, 2 * tp + tt : 2 * tp + tt + 1]
                    if n < share and gp:
                        nc.gpsimd.tensor_scalar(out=dst, in0=src, scalar1=sc, scalar2=0.0, op0=ALU.mult, op1=ALU.add)
                    elif n < share:
                        nc.vector.tensor_scalar(out=dst, in0=src, scalar1=sc, scalar2=None, op0=ALU.mult)
                    else:
                        nc.scalar.activation(out=dst, in_=src, func=ACT.Copy, scale=sc)

                def scale_blocks(s, share, gp=False):
                    for n in range(2 * HOPS):
                        scale_block(s, n, share, gp)

                PAIRS = (((0, 0), (1, 0)), ((0, 1), (0, 2)), ((1, 1), (1, 2)))

                def turn_blocks(s, b):
                    u_w = us[s][:].rearrange("p t i n -> p (t i n)").bitcast(F32).rearrange("p (t i u q) -> p t i u q", t=2, i=HOPS, u=2)
                    pt = ps_t.tile([P, 2, 2, P], F32, tag="t")
                    for u in range(2):
                        for n, (tt, i) in enumerate(PAIRS[b]):
                            nc.tensor.transpose(out=pt[:, u, n, :], in_=u_w[:, tt, i, u, :], identity=ident[:])
                    pts[s, b] = pt

                def mask_blocks(s, b):
                    tp = s % TP
                    if b == 0:
                        ng = loop.tile([P, 2 * HOPS * P, 4], BF16, align_bytes=64, name="ng")
                        ngs[s] = ng
                    at, lo, hi = ((4, 0, 2), (0, 0, 1), (2, 1, 2))[b]
                    w = 2 * P // (hi - lo)
                    keep = keep_g[:, 2 * tp + lo : 2 * tp + hi].rearrange("p t (u e) -> p t u e", u=2)
                    nc.vector.tensor_tensor(
                        out=ngs[s][:, at * P : (at + 2) * P, :].rearrange("p (t m) (u e) -> p t m u e", m=w, u=2),
                        in0=pts[s, b][:].rearrange("p u n m -> p (u n m)").bitcast(BF16).rearrange("p (u t m e) -> p t m u e", u=2, m=w, e=2),
                        in1=keep.unsqueeze(2).to_broadcast([P, hi - lo, w, 2, 2]), op=ALU.mult,
                    )

                def quantise_norm(s):
                    nq = loop.tile([P, 2 * HOPS * P], U32, align_bytes=64, name="nq")
                    ns = loop.tile([P, 2 * HOPS * P], U8, align_bytes=64, name="ns")
                    for lo, hi in ((4 * P, 6 * P), (0, 4 * P)):
                        nc.vector.quantize_mx(
                            out=nq[:, lo:hi].bitcast(FP8X4), scales=ns[:, lo:hi], in_=ngs[s][:, lo:hi, :].rearrange("p c j -> p (c j)")
                        )
                    nqs[s] = nq
                    nss[s] = ns

                def regroup_context(q, e, h, vec):
                    if q not in fcgs:
                        fcg = big.tile([P, 4, 2, P, 4], BF16, align_bytes=64, name="fcg")
                        fcgs[q] = fcg
                    lo, hi = h
                    dst = fcgs[q][:, :, e, lo:hi, :].rearrange("p t d j -> p d j t")
                    if vec:
                        nc.vector.tensor_copy(out=dst, in_=fc_view[:, q, e, lo:hi])
                    else:
                        nc.scalar.copy(out=dst, in_=fc_view[:, q, e, lo:hi])

                def quantise_context(q):
                    nc.vector.quantize_mx(
                        out=fcq[:, 4 * q : 4 * q + 4, :].rearrange("p t d -> p (t d)").bitcast(FP8X4),
                        scales=fcs[:, 4 * q : 4 * q + 4, :].rearrange("p t d -> p (t d)"),
                        in_=fcgs[q][:].rearrange("p t e d j -> p (t e d j)"),
                    )

                def turn_target(s):
                    a, tp = s // TP, s % TP
                    pf = ps_x.tile([P, 512], F32, tag="x")
                    for e in range(2):
                        nc.tensor.transpose(out=pf[:, e * P : (e + 1) * P], in_=ft_w[:, a, e, tp, :], identity=ident[:])
                    pair = loop.tile([P, 2, 2, P, 2], BF16, name="pair", bufs=3)
                    nc.scalar.copy(out=pair[:, 0], in_=pf[:].bitcast(BF16)[:, 0 : 4 * P].rearrange("p (e m t) -> p t m e", e=2, t=2))
                    pairs[s] = pair
                    if s % 2 == 0:
                        cg = loop.tile([P, 4096], BF16, align_bytes=64, name="cg")
                        flats[s // 2] = cg
                    w = P if a else MH
                    if a:
                        cg_v = flats[s // 2][:].rearrange("p (b h g t m j) -> p b h g t m j", b=2, g=2, t=2, m=w, j=4)[:, s % 2]
                    else:
                        cg_v = flats[s // 2][:].rearrange("p (h g b t m j) -> p b h g t m j", b=2, g=2, t=2, m=w, j=4)[:, s % 2]
                    cgs[s] = cg_v

                def interleave_target(s):
                    w = P if s >= TP else MH
                    words = pairs[s][:].rearrange("p x t m e -> p (x t m e)").bitcast(F32).rearrange("p (x t h m) -> p h t m x", x=2, t=2, m=w)
                    flat_w = flats[s // 2][:].bitcast(F32)
                    if s >= TP:
                        dst = flat_w.rearrange("p (b h g t m x) -> p b h g t m x", b=2, g=2, t=2, m=w, x=2)[:, s % 2]
                    else:
                        dst = flat_w.rearrange("p (h g b t m x) -> p b h g t m x", b=2, g=2, t=2, m=w, x=2)[:, s % 2]
                    for h in range(P // w):
                        nc.scalar.copy(out=dst[:, h, 0], in_=words[:, h])

                def hop_pass(dst, s, t, e, lo, hi):
                    nc.tensor.matmul_mx(
                        out=dst,
                        lhsT=fcq[:, t, e * P : (e + 1) * P].bitcast(FP8X4), lhsT_scale=fcs[:, t, e * P : (e + 1) * P],
                        rhs=nqs[s][:, lo:hi].bitcast(FP8X4), rhs_scale=nss[s][:, lo:hi],
                        start=True, stop=True,
                    )

                def neighbour_sums(s):
                    tp = s % TP
                    p0 = ps_s.tile([P, 2, 2, P], F32, tag="s")
                    for tt in range(2):
                        for e in range(2):
                            hop_pass(p0[:, tt, e, :], s, 2 * tp + tt, e, (4 + tt) * P, (5 + tt) * P)
                    p0s[s] = p0
                    p1s[s] = []
                    for tt in range(2):
                        pp = ps_s.tile([P, 2, 2, P], F32, tag="s")
                        for e in range(2):
                            hop_pass(pp[:, e].rearrange("p h m -> p (h m)"), s, 2 * tp + tt, e, 2 * tt * P, 2 * (tt + 1) * P)
                        p1s[s].append(pp)

                def add_target(s):
                    w = P if s >= TP else MH
                    ft = pairs[s][:, 0]
                    nc.vector.tensor_tensor(out=pairs[s][:, 1], in0=p0s[s][:].rearrange("p t e m -> p t m e"), in1=ft, op=ALU.add)
                    for tt in range(2):
                        nc.vector.tensor_tensor(
                            out=cgs[s][:, :, 1, tt].rearrange("p h m (i e) -> p h m i e", i=2),
                            in0=p1s[s][tt][:].rearrange("p e i (h m) -> p h m i e", m=w),
                            in1=ft[:, tt].rearrange("p (h m) e -> p h m e", m=w).unsqueeze(3).to_broadcast([P, P // w, w, 2, 2]), op=ALU.add,
                        )

                def quantise_cat(s):
                    if s < TP and s % 2 == 0:
                        return
                    lo, hi = (0, 2) if s < TP else (s % 2, s % 2 + 1)
                    nc.vector.quantize_mx(
                        out=catq[:, s // 2, 512 * lo : 512 * hi].bitcast(FP8X4), scales=cats[:, s // 2, 512 * lo : 512 * hi],
                        in_=flats[s // 2][:, 2048 * lo : 2048 * hi],
                    )

                def turn_weights(k):
                    pw = ps_x.tile([P, 512], F32, tag="x")
                    for h in range(4):
                        nc.tensor.transpose(out=pw[:, h * P : (h + 1) * P], in_=w_w[:, k, h, :], identity=ident[:])
                    wtg_w = wtg[:].rearrange("p g o j -> p (g o j)").bitcast(F32).rearrange("p (g o h) -> p g o h", g=2, h=2)
                    nc.scalar.copy(out=wtg_w[:, :, k * P : (k + 1) * P, :], in_=pw[:].rearrange("p (g h o) -> p g o h", g=2, h=2))

                def quantise_weights(g):
                    nc.vector.quantize_mx(
                        out=wqk[:, g, :].bitcast(FP8X4), scales=wsk[:, g, :], in_=wtg[:, g].rearrange("p o j -> p (o j)")
                    )

                wns = {}

                wns_w = []

                def load_natural(dst, b):
                    nc.sync.dma_start(out=dst, in_=wn_v[:, 4 * b : 4 * b + 4, :])
                    wns_w.append(dst.rearrange("p k c -> p (k c)").bitcast(F32).rearrange("p (k h q) -> p k h q", k=4, q=P))

                def turn_natural(late, b):
                    wt2 = late.tile([P, 2, 2, P, 4], BF16, align_bytes=64, name="wt2")
                    wt2_w = wt2[:].rearrange("p k g o j -> p (k g o j)").bitcast(F32).rearrange("p (k g o h) -> p k g o h", k=2, g=2, h=2)
                    for k in range(2):
                        pw = ps_x.tile([P, 512], F32, tag="x")
                        for h in range(4):
                            nc.tensor.transpose(out=pw[:, h * P : (h + 1) * P], in_=wns_w[b // 2][:, 2 * (b % 2) + k, h, :], identity=ident[:])
                        nc.scalar.copy(out=wt2_w[:, k], in_=pw[:].rearrange("p (g h o) -> p g o h", g=2, h=2))
                    wns[b] = wt2

                def quantise_natural(b):
                    if b == 0:
                        wqn = const.tile([P, KO, 2, P], U32, tag="wq", align_bytes=64)
                        wsn = const.tile([P, KO, 2, P], U8, tag="ws", align_bytes=64)
                        natural.extend((wqn, wsn))
                    wqn, wsn = natural
                    nc.vector.quantize_mx(
                        out=wqn[:, 2 * b : 2 * b + 2].rearrange("p k g o -> p (k g o)").bitcast(FP8X4),
                        scales=wsn[:, 2 * b : 2 * b + 2].rearrange("p k g o -> p (k g o)"),
                        in_=wns[b][:].rearrange("p k g o j -> p (k g o j)"),
                    )

                def mix_first(late, h, parts):
                    if h not in ots:
                        ot = late.tile([P, MH, KO, T], F32, name="ot", bufs=2)
                        ots[h] = ot
                    pb = ps_x.tile([P, 2, 256], F32, tag="x")
                    for b, (q, k) in enumerate(parts):
                        for g in range(2):
                            at = (2 * h + g) * 256
                            nc.tensor.matmul_mx(
                                out=pb[:, b, :],
                                lhsT=wqk[:, g, k * P : (k + 1) * P].bitcast(FP8X4), lhsT_scale=wsk[:, g, k * P : (k + 1) * P],
                                rhs=catq[:, q, at : at + 256].bitcast(FP8X4), rhs_scale=cats[:, q, at : at + 256],
                                start=(g == 0), stop=(g == 1),
                            )
                    (q, k), (q2, k2) = parts
                    if k == k2:
                        nc.scalar.activation(
                            out=ots[h][:, :, k, 4 * q : 4 * q + 8], in_=pb[:].rearrange("p b (t m) -> p m (b t)", t=4),
                            func=ACT.Relu, bias=bias_col[:, k : k + 1],
                        )
                    else:
                        for b, (q, k) in enumerate(parts):
                            nc.scalar.activation(
                                out=ots[h][:, :, k, 4 * q : 4 * q + 4], in_=pb[:, b, :].rearrange("p (t m) -> p m t", t=4),
                                func=ACT.Relu, bias=bias_col[:, k : k + 1],
                            )
                    if parts[-1] == (3, KO - 1):
                        for b in range(2):
                            nc.sync.dma_start(
                                out=out_o[:, 0, h * MH + 32 * b : h * MH + 32 * b + 32, :],
                                in_=ots[h][:, 32 * b : 32 * b + 32].rearrange("p m k t -> p m (k t)"),
                            )

                whole, low, high = (0, P), (0, P // 2), (P // 2, P)
                turn_adj(0, ((0, 0), (0, 1)), nc.vector.tensor_copy)
                turn_mask()
                row_sums(0, (0,))
                turn_adj(0, ((1, 0), (1, 1)), nc.scalar.copy)
                turn_adj(0, ((2, 0), (2, 1)), nc.scalar.copy)
                invert_sums(0, (0,))
                scale_block(0, 0, 4, False)
                scale_block(0, 1, 4, False)
                row_sums(0, (1,))
                row_sums(0, (2,))
                turn_blocks(0, 0)
                invert_sums(0, (1,))
                scale_block(0, 2, 4, False)
                scale_block(0, 3, 4, False)
                invert_sums(0, (2,))
                scale_block(0, 4, 4, False)
                scale_block(0, 5, 4, False)
                turn_blocks(0, 1)
                scale_blocks(1, 2)
                mask_blocks(0, 0)
                mask_blocks(0, 1)
                turn_blocks(0, 2)
                turn_blocks(1, 0)
                scale_blocks(2, 4, True)
                mask_blocks(0, 2)
                mask_blocks(1, 0)
                turn_blocks(1, 1)
                turn_blocks(1, 2)
                quantise_norm(0)
                mask_blocks(1, 1)
                mask_blocks(1, 2)
                turn_blocks(2, 0)
                turn_blocks(2, 1)
                quantise_norm(1)
                regroup_context(0, 0, low, False)
                regroup_context(0, 1, low, False)
                regroup_context(0, 0, high, False)
                regroup_context(0, 1, high, True)
                scale_blocks(3, 4, True)
                turn_target(0)
                quantise_context(0)
                regroup_context(1, 0, whole, False)
                neighbour_sums(0)

                eights = [[(h, ((0, k), (1, k))) for k in range(KO)] for h in range(2)]
                fours = [[[(h, ((q, k), (q, k + 1))) for k in range(0, KO, 2)] for q in (2, 3)] for h in range(2)]
                mixes = eights[0] + fours[0][0] + eights[1][:4] + fours[0][1] + eights[1][4:] + fours[1][0] + fours[1][1]

                def step(s, late):
                    todo = mixes[max(0, s - LATE) * MIX_RATE // 3 : max(0, s + 1 - LATE) * MIX_RATE // 3]
                    first = min(MIX_FIRST, len(todo) if s > TP else max(0, 16 - max(0, s - LATE) * MIX_RATE // 3))
                    if s < 5:
                        regroup_context((s + 3) // 2, (s + 1) % 2, whole, False)
                    if s + 4 < STEPS:
                        open_scalings(s + 4)
                    if s + 2 < STEPS:
                        mask_blocks(s + 2, 0)
                        turn_blocks(s + 2, 2)
                        mask_blocks(s + 2, 1)
                    if s + 3 < STEPS:
                        turn_blocks(s + 3, 0)
                    if s + 1 < STEPS:
                        turn_target(s + 1)
                    if s == 1:
                        for u in range(2):
                            turn_adj(1, tuple((i, u) for i in range(HOPS)), nc.scalar.copy)
                    if s == 2:
                        row_sums(1, (0, 1, 2))
                    for h, parts in todo[:first]:
                        mix_first(late, h, parts)
                    add_target(s)
                    if s + 2 < STEPS:
                        mask_blocks(s + 2, 2)
                    if s > 0:
                        quantise_cat(s - 1)
                    if s + 4 < STEPS:
                        scale_blocks(s + 4, SHARE, True)
                    if s + 1 < STEPS:
                        neighbour_sums(s + 1)
                    if s + 3 < STEPS:
                        turn_blocks(s + 3, 1)
                    if s < 4:
                        turn_weights(2 * s)
                        turn_weights(2 * s + 1)
                    for h, parts in todo[first : first + 0]:
                        mix_first(late, h, parts)
                    interleave_target(s)
                    for h, parts in todo[first + 0 :]:
                        mix_first(late, h, parts)
                    if s == 3:
                        invert_sums(1, (0, 1, 2))
                    if s + 2 < STEPS:
                        quantise_norm(s + 2)
                    if s < 5 and s % 2 == 0:
                        quantise_context(s // 2 + 1)
                    if s >= TP + 4 and s < TP + 8:
                        quantise_natural(s - TP - 4)
                    if s >= TP + 3 and s < TP + 7:
                        turn_natural(late, s - TP - 3)
                    if s == 4:
                        quantise_weights(0)
                        quantise_weights(1)

                for s in range(LATE):
                    step(s, None)
            with tc.tile_pool(name="late", bufs=1) as late:
                wr2 = late.tile([P, 4, C], BF16, align_bytes=64)
                load_natural(wr2[:], 0)
                for s in range(LATE, STEPS):
                    if s == TP:
                        load_natural(ft_r[:, 0, :].rearrange("p (k c) -> p k c", k=4), 1)
                    step(s, late)
                quantise_cat(STEPS - 1)

        with ExitStack() as ph2:
            opool = ph2.enter_context(tc.tile_pool(name="opool", bufs=8, reuse_waits="tile"))
            ps_o = ph2.enter_context(tc.psum_pool(name="ps_o", bufs=8, reuse_waits="tile"))
            wqn, wsn = natural
            for ob in range(8):
                ot = opool.tile([P, P, T], F32)
                for tq in range(4):
                    pb = ps_o.tile([P, 4, P], F32)
                    for tt in range(4):
                        q, at = TP // 2 + tq, (tt // 2) * 512 + (tt % 2) * P
                        for g in range(2):
                            nc.tensor.matmul_mx(
                                out=pb[:, tt, :],
                                lhsT=catq[:, q, g * 256 + at : g * 256 + at + P].bitcast(FP8X4),
                                lhsT_scale=cats[:, q, g * 256 + at : g * 256 + at + P],
                                rhs=wqn[:, ob, g, :].bitcast(FP8X4),
                                rhs_scale=wsn[:, ob, g, :],
                                start=(g == 0), stop=(g == 1),
                            )
                    nc.vector.tensor_tensor(
                        out=ot[:, :, 4 * tq : 4 * tq + 4], in0=pb[:].rearrange("p t o -> p o t"),
                        in1=bias_bc[:, ob * P : (ob + 1) * P].unsqueeze(2).to_broadcast([P, P, 4]), op=ALU.add,
                    )
                flat = ot[:].rearrange("p o t -> p (o t)")
                pieces = 4 if ob == KO - 1 else 2
                size = P * T // pieces
                for h in range(pieces):
                    part = flat[:, h * size : (h + 1) * size]
                    if ob == KO - 1 and h % 2 == 1:
                        nc.vector.tensor_scalar(out=part, in0=part, scalar1=0.0, scalar2=None, op0=ALU.max)
                    else:
                        nc.scalar.activation(out=part, in_=part, func=ACT.Relu)
                    nc.sync.dma_start(out=out_m[:, 1, ob * P * T + h * size : ob * P * T + (h + 1) * size], in_=part)
